import numpy as np
import ml_dtypes


def mxq(x, axis, fmt="e4m3"):
    dtype, down = {"e4m3": (ml_dtypes.float8_e4m3fn, 7), "e5m2": (ml_dtypes.float8_e5m2, 14)}[fmt]
    v = np.moveaxis(np.asarray(x, np.float32).astype(ml_dtypes.bfloat16).astype(np.float64), axis, -1)
    blocks = v.reshape(v.shape[:-1] + (-1, 32))
    amax = np.abs(blocks).max(-1, keepdims=True)
    byte = np.maximum(np.where(amax > 0, np.frexp(amax)[1] - 1 + 127, 0) - down, 1)
    scale = np.exp2(byte - 127.0)
    codes = (blocks / scale).astype(np.float32).astype(dtype).astype(np.float64)
    return np.moveaxis((codes * scale).reshape(v.shape), -1, axis)


WIDE = False


def mx_kscale(k):
    if not WIDE:
        return np.ones(k)
    levels = np.array([10, -10, 5, -5, 0])
    if k % 512:
        return np.exp2(np.random.permutation(np.resize(levels, k // 32))).repeat(32)
    a = np.empty((k // 512, 16))
    for p in range(k // 512):
        a[p, :8] = np.random.permutation(np.resize(levels, 8))
        for g in range(8):
            far = levels[np.abs(levels - a[p, g]) >= 10]
            a[p, g + 8] = far[np.random.randint(len(far))]
    return np.exp2(a.ravel()).repeat(32)


BF16 = ml_dtypes.bfloat16


def bf(x):
    return np.asarray(x, np.float32).astype(BF16)


def f64(x):
    return np.asarray(x).astype(np.float64)


B, T, H, P, M = 16, 1024, 1024, 256, 64


def make_mapping():
    m = np.zeros((M, P))
    cols = np.arange(P)
    m[np.random.permutation(cols % M), cols] = 0.5 + np.random.random(P)
    m[np.random.randint(0, M, size=P), cols] = 0.5 + np.random.random(P)
    m[0, 0] = 1.0
    return m


def masked_max(phone, mapping):
    out = np.empty(phone.shape[:2] + (mapping.shape[0],))
    for b in range(phone.shape[0]):
        allo = phone[b][:, None, :] * mapping
        allo = np.where(mapping > 0, allo, -np.inf)
        out[b] = allo.max(-1)
    return out


def log_softmax(v, axis):
    shifted = v - v.max(axis, keepdims=True)
    return shifted - np.log(np.exp(shifted).sum(axis, keepdims=True))


def setup_inputs():
    s = mx_kscale(H)
    return {"enc_output": bf(np.random.standard_normal((B, T, H)) * s),
            "feature2phone": bf(np.random.standard_normal((H, P)) / s[:, None]),
            "mapping": bf(make_mapping())}


def reference(enc_output, feature2phone, mapping):
    mapping = f64(mapping)
    phone = (mxq(f64(enc_output), 2, "e4m3") @ mxq(f64(feature2phone), 0, "e4m3")) / np.sqrt(H)
    phoneme = masked_max(phone, mapping)
    return log_softmax(phoneme, 2)

@@ -1,0 +1,464 @@
+from contextlib import ExitStack
+
+import concourse.mybir as mybir
+from concourse.masks import make_identity
+
+F32 = mybir.dt.float32
+BF16 = mybir.dt.bfloat16
+I32 = mybir.dt.int32
+U32 = mybir.dt.uint32
+U8 = mybir.dt.uint8
+FP8X4 = mybir.dt.float8_e4m3fn_x4
+ALU = mybir.AluOpType
+ACT = mybir.ActivationFunctionType
+AX = mybir.AxisListType
+
+TOKENS = 16 * 1024
+H = 1024
+PHONES = 256
+PHONEMES = 64
+FLOPS = 2 * TOKENS * H * PHONES
+
+P = 128
+BLOCK = 512
+NBLK = TOKENS // BLOCK
+NPAIR = NBLK // 2
+DEPTH = 6
+NV = 2
+SLOTS = DEPTH * P
+AHEAD = 3
+GROUPS = ((0, 12), (12, 20), (20, 26), (26, 32))
+NEG_BIG = -3.0e38
+W_ENG = ("sv", "sv", "sv", "sv", "sv", "sv")
+EARLY_N = (2, 2, 3, 3, 3, 3)
+EARLY_ENG = ("s", "s", "s", "s", "s", "s")
+PHASES = 4
+V_PHASE = 1
+E_PHASE = 3
+SEED_POS = 4
+
+
+def tile_compositionalphoneticsmodel_t_kernel(tc, enc_output, feature2phone, mapping, out):
+    nc = tc.nc
+    enc_v = enc_output.rearrange("b t k -> (b t) k").rearrange("(n p s) k -> n p (s k)", p=P, s=4)
+    out_v = out.rearrange("b t m -> (b t) m").rearrange("(n p s) m -> p n (s m)", p=P, s=4)
+    w_v = feature2phone.rearrange("(g q t) p -> q g (t p)", g=2, q=P, t=4)
+
+    with ExitStack() as ctx:
+        const = ctx.enter_context(tc.tile_pool(name="const", bufs=1))
+        xpool = ctx.enter_context(tc.tile_pool(name="xpool", bufs=4))
+        gpool = ctx.enter_context(tc.tile_pool(name="gpool", bufs=4))
+        cpool = ctx.enter_context(tc.tile_pool(name="cpool", bufs=8))
+        apool = ctx.enter_context(tc.tile_pool(name="apool", bufs=6))
+        spool = ctx.enter_context(tc.tile_pool(name="spool", bufs=2))
+        ps_t = ctx.enter_context(tc.psum_pool(name="ps_t", bufs=3))
+        ps_m = ctx.enter_context(tc.psum_pool(name="ps_m", bufs=3))
+        ps_f = ctx.enter_context(tc.psum_pool(name="ps_f", bufs=1))
+        ctx.enter_context(tc.manual_schedule())
+
+        xs = {}
+        grs = {}
+        cds = {}
+        accs = {}
+        pfs = {}
+        c0s = {}
+        tps = {}
+        t3s = {}
+
+        map2 = const.tile([P, PHONES], BF16)
+        nc.sync.dma_start(out=map2[0:64, :], in_=mapping)
+        nc.sync.dma_start(out=map2[64:128, :], in_=mapping)
+        wl = const.tile([P, 4, 2, PHONES], BF16)
+        nc.sync.dma_start(out=wl[:].rearrange("q (g u) e p -> q g (u e p)", g=2), in_=w_v)
+
+        def load(b):
+            x = xpool.tile([P, 4 * H], BF16)
+            nc.sync.dma_start(out=x[:], in_=enc_v[b])
+            xs[b] = x
+
+        for b in range(4):
+            load(b)
+
+        part_i = const.tile([P, 1], I32)
+        nc.gpsimd.iota(part_i[:], pattern=[[0, 1]], base=0, channel_multiplier=1)
+        slot_i = const.tile([P, NV * DEPTH], I32)
+        nc.gpsimd.iota(slot_i[:], pattern=[[2 * DEPTH, NV], [1, DEPTH]], base=0, channel_multiplier=0)
+        iota_i = const.tile([P, P], I32)
+        nc.gpsimd.iota(iota_i[:], pattern=[[1, P]], base=0, channel_multiplier=0)
+        ident_b = const.tile([P, P], BF16)
+        make_identity(nc, ident_b[:])
+        ident_f = const.tile([P, P], F32)
+        make_identity(nc, ident_f[:])
+
+        part_f = const.tile([P, 1], F32)
+        nc.vector.tensor_copy(out=part_f[:], in_=part_i[:])
+        slot_f = const.tile([P, NV * DEPTH], F32)
+        nc.vector.tensor_copy(out=slot_f[:], in_=slot_i[:])
+        half_d = const.tile([P, 1], F32)
+        nc.vector.tensor_scalar(out=half_d[:], in0=part_f[:], scalar1=64.0, scalar2=float(DEPTH), op0=ALU.is_ge, op1=ALU.mult)
+        want0 = const.tile([P, NV * DEPTH], F32)
+        nc.vector.tensor_scalar(out=want0[:], in0=slot_f[:], scalar1=half_d[:, 0:1], scalar2=None, op0=ALU.add)
+        iota_f = const.tile([P, P], F32)
+        nc.vector.tensor_copy(out=iota_f[:], in_=iota_i[:])
+        tri = const.tile([P, P], BF16)
+        nc.vector.tensor_scalar(out=tri[:], in0=iota_f[:], scalar1=part_f[:, 0:1], scalar2=None, op0=ALU.is_gt)
+        ones = const.tile([P, P], BF16)
+        nc.vector.memset(ones[:], 1.0)
+        gain_b = const.tile([P, NV, 32], BF16)
+        nc.vector.memset(gain_b[:], 0.0)
+
+        mask = const.tile([P, PHONES], F32)
+        nc.vector.tensor_single_scalar(out=mask[:], in_=map2[:], scalar=0.0, op=ALU.is_gt)
+        incl = const.tile([P, PHONES], F32)
+        nc.vector.tensor_tensor_scan(out=incl[:], data0=mask[:], data1=mask[:], initial=0.0, op0=ALU.add, op1=ALU.max)
+        rank1 = const.tile([P, PHONES], F32)
+        nc.vector.tensor_tensor(out=rank1[:], in0=incl[:], in1=mask[:], op=ALU.mult)
+        count = incl[:, PHONES - 1 : PHONES]
+        valid = const.tile([P, NV * DEPTH], F32)
+        nc.vector.tensor_scalar(out=valid[:], in0=want0[:], scalar1=count, scalar2=None, op0=ALU.is_lt)
+        valid_v = valid[:].rearrange("v (h d) -> v h d", d=DEPTH)
+        active = valid_v[:, :, 0]
+        act_b = const.tile([P, NV, 32], BF16)
+        nc.vector.tensor_copy(out=act_b[:], in_=valid_v[:, :, 0:1].to_broadcast([P, NV, 32]))
+        want_t = const.tile([P, NV * DEPTH], F32)
+        nc.vector.tensor_tensor(out=want_t[:], in0=want0[:], in1=valid[:], op=ALU.mult)
+        want1 = const.tile([P, NV * DEPTH], F32)
+        nc.vector.tensor_single_scalar(out=want1[:], in_=want_t[:], scalar=1.0, op=ALU.add)
+
+        lid_p = ps_m.tile([P, NV, 32], F32, tag="pm")
+        nc.tensor.matmul(out=lid_p[:, 0, :], lhsT=tri[:], rhs=act_b[:, 0, :], start=True, stop=True)
+        nc.tensor.matmul(out=lid_p[:, 1, :], lhsT=ones[:], rhs=act_b[:, 0, :], start=True, stop=False)
+        nc.tensor.matmul(out=lid_p[:, 1, :], lhsT=tri[:], rhs=act_b[:, 1, :], start=False, stop=True)
+
+        sgw = const.tile([P, NV * DEPTH, PHONES], BF16)
+        gain_v = const.tile([P, NV * DEPTH], F32)
+
+        def sgw_make(d):
+            for h in range(NV):
+                j = h * DEPTH + d
+                nc.vector.scalar_tensor_tensor(
+                    out=sgw[:, j, :], in0=rank1[:], scalar=want1[:, j : j + 1], in1=map2[:],
+                    op0=ALU.is_equal, op1=ALU.mult, accum_out=gain_v[:, j : j + 1],
+                )
+
+        sgw_make(0)
+
+        lid_t = const.tile([P, NV], F32)
+        nc.vector.scalar_tensor_tensor(out=lid_t[:], in0=lid_p[:, :, 0], scalar=1.0, in1=active, op0=ALU.add, op1=ALU.mult)
+        lane_id = const.tile([P, NV], F32)
+        nc.vector.tensor_single_scalar(out=lane_id[:], in_=lid_t[:], scalar=-1.0, op=ALU.add)
+        compact = const.tile([P, NV, P], BF16)
+        for h in range(NV):
+            nc.vector.tensor_scalar(out=compact[:, h, :], in0=iota_f[:], scalar1=lane_id[:, h : h + 1], scalar2=None, op0=ALU.is_equal)
+        tg1 = const.tile([P, 1], F32)
+        nc.vector.scalar_tensor_tensor(out=tg1[:], in0=lid_p[:, 1, 0:1], scalar=lane_id[:, 0:1], in1=valid_v[:, 1, 0:1], op0=ALU.subtract, op1=ALU.mult)
+        tgt_b = const.tile([P, NV], BF16)
+        nc.vector.tensor_copy(out=tgt_b[:, 0:1], in_=lane_id[:, 0:1])
+        nc.vector.tensor_scalar(out=tgt_b[:, 1:2], in0=tg1[:], scalar1=lane_id[:, 0:1], scalar2=None, op0=ALU.add)
+
+        wt = []
+
+        def wt_make(c):
+            wt_p = ps_t.tile([P, 8 * P], BF16, tag="pt")
+            for a in range(4):
+                for e in range(2):
+                    nc.tensor.transpose(wt_p[:, (a * 2 + e) * P : (a * 2 + e + 1) * P], wl[:, a, e, c * P : (c + 1) * P], ident_b[:])
+            wt_c = const.tile([P, 8 * P], BF16, name="wt%d" % c)
+            nc.scalar.copy(out=wt_c[:], in_=wt_p[:])
+            wt.append(wt_c)
+
+        sel = const.tile([P, DEPTH, 2, P], BF16)
+
+        def sel_make(d):
+            sel_p = ps_f.tile([P, 2, P], F32, tag="pf%d" % (d % 2), name="sel_p")
+            for c in range(2):
+                for h in range(NV):
+                    nc.tensor.matmul(
+                        out=sel_p[:, c, :],
+                        lhsT=sgw[:, h * DEPTH + d, c * P : (c + 1) * P],
+                        rhs=compact[:, h, :],
+                        start=(h == 0),
+                        stop=(h == NV - 1),
+                    )
+            nc.scalar.activation(out=sel[:, d, :, :], in_=sel_p[:], func=ACT.Sign)
+
+        wg = const.tile([P, 2, DEPTH, P * 4], BF16, align_bytes=64)
+        w_codes = const.tile([P, 2, DEPTH, P], U32, align_bytes=64)
+        w_scales = const.tile([P, 2, DEPTH, P], U8, align_bytes=64)
+
+        def wslot_make(d, engines):
+            for g in range(2):
+                wp = ps_m.tile([P, 4 * P], F32, tag="pm")
+                for ue in range(4):
+                    for c in range(2):
+                        nc.tensor.matmul(
+                            out=wp[:, ue * P : (ue + 1) * P],
+                            lhsT=wt[c][:, (g * 4 + ue) * P : (g * 4 + ue + 1) * P],
+                            rhs=sel[:, d, c, :],
+                            start=(c == 0),
+                            stop=(c == 1),
+                        )
+                dst = wg[:, g, d, :].rearrange("q (l t) -> q l t", t=4)
+                src = wp[:].rearrange("q (t l) -> q l t", t=4)
+                if engines[g] == "v":
+                    nc.vector.tensor_copy(out=dst, in_=src)
+                else:
+                    nc.scalar.copy(out=dst, in_=src)
+
+        def wslot_quant(d):
+            for g in range(2):
+                nc.vector.quantize_mx(out=w_codes[:, g, d, :].bitcast(FP8X4), scales=w_scales[:, g, d, :], in_=wg[:, g, d, :])
+
+        gain = const.tile([P, DEPTH], F32)
+        perm2 = const.tile([P, NV * P], F32)
+        bias = const.tile([P, PHONEMES], F32)
+
+        def gain_make():
+            nc.vector.tensor_copy(out=gain_b[:, :, 0:DEPTH], in_=gain_v[:].rearrange("v (h d) -> v h d", d=DEPTH))
+            gain_p = ps_f.tile([P, 32], F32, tag="pf0")
+            for h in range(NV):
+                nc.tensor.matmul(out=gain_p[:], lhsT=compact[:, h, :], rhs=gain_b[:, h, :], start=(h == 0), stop=(h == NV - 1))
+            nc.vector.tensor_single_scalar(out=gain[:], in_=gain_p[:, 0:DEPTH], scalar=1.0 / 32.0, op=ALU.mult)
+
+        def perm_make():
+            row_p = ps_f.tile([P, NV * P], F32, tag="pf1")
+            for h in range(NV):
+                nc.tensor.matmul(out=row_p[:, h * P : (h + 1) * P], lhsT=tgt_b[:, h : h + 1].to_broadcast([P, P]), rhs=ident_b[:], start=True, stop=True)
+            nc.vector.tensor_scalar(out=perm2[:], in0=row_p[:], scalar1=part_f[:, 0:1], scalar2=None, op0=ALU.is_equal)
+            nc.vector.tensor_scalar(out=bias[:], in0=row_p[:, 64:128], scalar1=0.0, scalar2=NEG_BIG, op0=ALU.is_lt, op1=ALU.mult)
+
+        v_all = const.tile([P, NBLK * 256], F32)
+        neg_max = const.tile([P, NBLK * 4], F32)
+        sums = const.tile([P, NBLK * 4], F32)
+        logs = const.tile([P, NBLK * 4], F32)
+        neg_l = const.tile([P, NBLK * 4], F32)
+
+        def a_bank(b, k, engine="s"):
+            if k == 0:
+                gr = gpool.tile([P, 2 * BLOCK * 4], BF16, align_bytes=64)
+                grs[b] = gr
+            g = k // 2
+            sp = k % 2
+            xw = xs[b][:].bitcast(F32)
+            grw = grs[b][:].bitcast(F32)
+            pt = ps_t.tile([P, 4 * P], F32, tag="pt")
+            for u in range(2):
+                for s2 in range(2):
+                    col = (2 * sp + s2) * 512 + 256 * g
+                    nc.tensor.transpose(pt[:, (u * 2 + s2) * P : (u * 2 + s2 + 1) * P], xw[:, col + u : col + 256 : 2], ident_f[:])
+            lo = g * 1024 + sp * 512
+            dst = grw[:, lo : lo + 512].rearrange("q (t u) -> q t u", u=2)
+            src = pt[:].rearrange("q (u t) -> q t u", u=2)
+            if engine == "v":
+                nc.vector.tensor_copy(out=dst, in_=src)
+            else:
+                nc.scalar.copy(out=dst, in_=src)
+
+        def quant(b, g):
+            if g == 0:
+                codes = cpool.tile([P, 2 * BLOCK], U32, align_bytes=64)
+                scales = cpool.tile([P, 2 * BLOCK], U8, align_bytes=64)
+                cds[b] = (codes, scales)
+            codes, scales = cds[b]
+            nc.vector.quantize_mx(
+                out=codes[:, g * BLOCK : (g + 1) * BLOCK].bitcast(FP8X4),
+                scales=scales[:, g * BLOCK : (g + 1) * BLOCK],
+                in_=grs[b][:, g * BLOCK * 4 : (g + 1) * BLOCK * 4],
+            )
+
+        def mx(b, d):
+            if d == 0:
+                acc = apool.tile([P, BLOCK], F32)
+                accs[b] = acc
+            codes, scales = cds[b]
+            pm = ps_m.tile([P, BLOCK], F32, tag="pm")
+            for g in range(2):
+                nc.tensor.matmul_mx(
+                    out=pm[:],
+                    lhsT=w_codes[:, g, d, :].bitcast(FP8X4),
+                    lhsT_scale=w_scales[:, g, d, :],
+                    rhs=codes[:, g * BLOCK : (g + 1) * BLOCK].bitcast(FP8X4),
+                    rhs_scale=scales[:, g * BLOCK : (g + 1) * BLOCK],
+                    start=(g == 0),
+                    stop=(g == 1),
+                )
+            if d == 0:
+                nc.scalar.activation(out=accs[b][:], in_=pm[:], func=ACT.Copy, scale=gain[:, 0:1])
+            else:
+                nc.vector.scalar_tensor_tensor(out=accs[b][:], in0=pm[:], scalar=gain[:, d : d + 1], in1=accs[b][:], op0=ALU.mult, op1=ALU.max)
+
+        def f_bank(b, h):
+            pf = ps_f.tile([P, 4 * P], F32, tag="pf%d" % h, name="pf%d" % h)
+            for s in range(4):
+                nc.tensor.transpose(pf[:, s * P : (s + 1) * P], accs[b][:, s * P : (s + 1) * P], perm2[:, h * P : (h + 1) * P])
+            pfs[(b, h)] = pf
+            if h == 0:
+                c0 = spool.tile([P, 4 * P], F32)
+                nc.scalar.copy(out=c0[:], in_=pf[:])
+                c0s[b] = c0
+
+        def t_max(b):
+            if b % 2 == 0:
+                tp = spool.tile([P, 2, 4, P], F32)
+                tps[b // 2] = tp
+            nc.vector.tensor_tensor(out=tps[b // 2][:, b % 2, :, :].rearrange("p s c -> p (s c)"), in0=pfs[(b, 1)][:], in1=c0s[b][:], op=ALU.max)
+
+        def bias_add(j, eng, lo=0, hi=8):
+            if lo == 0:
+                t3 = spool.tile([P, 8, PHONEMES], F32)
+                t3s[j] = t3
+            eng.tensor_tensor(
+                out=t3s[j][:, lo:hi, :],
+                in0=tps[j][:].rearrange("p b s c -> p (b s) c")[:, lo:hi, 64:128],
+                in1=bias[:].unsqueeze(1).to_broadcast([P, hi - lo, PHONEMES]),
+                op=ALU.add,
+            )
+
+        def v_max(j, lo=0, hi=8):
+            vv = v_all[:, j * 512 + lo * 64 : j * 512 + hi * 64].rearrange("p (s m) -> p s m", m=PHONEMES)
+            nc.vector.tensor_tensor(out=vv, in0=tps[j][:].rearrange("p b s c -> p (b s) c")[:, lo:hi, 0:64], in1=t3s[j][:, lo:hi, :], op=ALU.max)
+            nc.vector.tensor_reduce(out=neg_max[:, j * 8 + lo : j * 8 + hi], in_=vv, axis=AX.X, op=ALU.max, negate=True)
+
+        def exps(j, lo=0, hi=8):
+            for i in range(j * 8 + lo, j * 8 + hi):
+                ex = spool.tile([P, PHONEMES], F32)
+                nc.scalar.activation(
+                    out=ex[:], in_=v_all[:, i * 64 : (i + 1) * 64], func=ACT.Exp,
+                    bias=neg_max[:, i : i + 1], scale=1.0, accum_out=sums[:, i : i + 1],
+                )
+
+        def group_ln(gi, eng):
+            g0, g1 = GROUPS[gi]
+            cols = slice(g0 * 4, g1 * 4)
+            nc.scalar.activation(out=logs[:, cols], in_=sums[:, cols], func=ACT.Ln)
+            eng.tensor_tensor(out=neg_l[:, cols], in0=neg_max[:, cols], in1=logs[:, cols], op=ALU.subtract)
+
+        def finish(b0, b1, eng, queue):
+            n = (b1 - b0) * 4
+            vg = v_all[:, b0 * 256 : b1 * 256]
+            vg3 = vg.rearrange("p (i m) -> p i m", m=PHONEMES)
+            eng.tensor_tensor(out=vg3, in0=vg3, in1=neg_l[:, b0 * 4 : b1 * 4].unsqueeze(2).to_broadcast([P, n, PHONEMES]), op=ALU.add)
+            queue.dma_start(out=out_v[:, b0:b1, :], in_=vg.rearrange("p (n f) -> p n f", f=256))
+
+        def finish_scalar(b0, b1, queue):
+            for i in range(b0 * 4, b1 * 4):
+                nc.scalar.activation(out=v_all[:, i * 64 : (i + 1) * 64], in_=v_all[:, i * 64 : (i + 1) * 64], func=ACT.Identity, bias=neg_l[:, i : i + 1], scale=1.0)
+            queue.dma_start(out=out_v[:, b0:b1, :], in_=v_all[:, b0 * 256 : b1 * 256].rearrange("p (n f) -> p n f", f=256))
+
+        def a_block(b, ks, engine="s"):
+            for k in ks:
+                a_bank(b, k, engine)
+                if k == 3 and b + 4 < NBLK:
+                    load(b + 4)
+
+        wt_make(0)
+        wt_make(1)
+        sel_make(0)
+        sgw_make(1)
+        sel_make(1)
+        sgw_make(2)
+        early = [(b, k) for b in range(4) for k in range(4)]
+        for d in range(DEPTH):
+            wslot_make(d, W_ENG[d])
+            if d + 2 < DEPTH:
+                sel_make(d + 2)
+            if d + 3 < DEPTH:
+                sgw_make(d + 3)
+            for b, k in early[sum(EARLY_N[:d]) : sum(EARLY_N[: d + 1])]:
+                a_block(b, [k], EARLY_ENG[d])
+            wslot_quant(d)
+            if d == 3:
+                quant(0, 0)
+                quant(0, 1)
+            if d == 4:
+                gain_make()
+                perm_make()
+        for b, k in early[sum(EARLY_N) :]:
+            a_block(b, [k])
+        quant(1, 0)
+        quant(1, 1)
+        mx(0, 0)
+        mx(1, 0)
+        quant(2, 0)
+        quant(2, 1)
+        quant(3, 0)
+        quant(3, 1)
+
+        pending = []
+        finished = 0
+        for j in range(NPAIR):
+            p0, p1 = 2 * j, 2 * j + 1
+            n0, n1 = p0 + 2, p1 + 2
+            if j == 0:
+                a_list = [4, 5, 6, 7]
+                q_list = []
+            else:
+                a_list = [b for b in (p0 + 2 * AHEAD, p1 + 2 * AHEAD) if b < NBLK]
+                q_list = [b for b in (p0 + 2 * AHEAD - 2, p1 + 2 * AHEAD - 2) if b < NBLK]
+            f_list = [p0 - 2, p1 - 2] if 1 <= j <= NPAIR else []
+            m_banks = []
+            if j < NPAIR:
+                m_banks += [(b, d) for d in range(1, DEPTH) for b in (p0, p1)]
+            if n0 < NBLK:
+                m_banks = m_banks[:SEED_POS] + [(n0, 0), (n1, 0)] + m_banks[SEED_POS:]
+            a_banks = [("a", b, k) for b in a_list for k in range(4)]
+            na = len(a_banks) // 2
+            t_banks = []
+            if f_list:
+                t_banks += [("f", f_list[0], 0), ("f", f_list[0], 1)]
+            t_banks += a_banks[:na]
+            if f_list:
+                t_banks += [("f", f_list[1], 0), ("f", f_list[1], 1)]
+            t_banks += a_banks[na:]
+            quants = [(b, g) for b in q_list for g in range(2)]
+            for ph in range(PHASES):
+                for b, d in m_banks[len(m_banks) * ph // PHASES : len(m_banks) * (ph + 1) // PHASES]:
+                    mx(b, d)
+                if ph == V_PHASE and j >= 2:
+                    v_max(j - 2)
+                if ph == E_PHASE and j >= 2:
+                    exps(j - 2)
+                    for gi in range(len(GROUPS)):
+                        if GROUPS[gi][1] == 2 * (j - 1):
+                            group_ln(gi, nc.gpsimd)
+                            pending.extend(range(GROUPS[gi][0], GROUPS[gi][1], 2))
+                tp_n = 2 if j == NPAIR - 1 else PHASES
+                for kind, b, k in t_banks[len(t_banks) * min(ph, tp_n) // tp_n : len(t_banks) * min(ph + 1, tp_n) // tp_n]:
+                    if kind == "a":
+                        a_block(b, [k])
+                    else:
+                        f_bank(b, k)
+                        if k == 1:
+                            t_max(b)
+                            if b % 2 == 1:
+                                bias_add(b // 2, nc.gpsimd)
+                for b, g in quants[len(quants) * ph // PHASES : len(quants) * (ph + 1) // PHASES]:
+                    quant(b, g)
+                if ph % 2 == 1 and finished < len(pending):
+                    finish(pending[finished], pending[finished] + 2, nc.gpsimd, nc.gpsimd)
+                    finished += 1
+            if j == 0:
+                for b in (4, 5):
+                    quant(b, 0)
+                    quant(b, 1)
+
+        assert finished == len(pending)
+        z = NPAIR - 1
+        v_max(z - 1)
+        f_bank(2 * z, 0)
+        f_bank(2 * z, 1)
+        f_bank(2 * z + 1, 0)
+        exps(z - 1)
+        for b in (2 * z, 2 * z + 1):
+            lo = 4 * (b % 2)
+            t_max(b)
+            if b == 2 * z:
+                f_bank(b + 1, 1)
+            bias_add(z, nc.vector, lo, lo + 4)
+            v_max(z, lo, lo + 4)
+            exps(z, lo, lo + 4)
+        g0 = GROUPS[-1][0]
+        group_ln(len(GROUPS) - 1, nc.vector)
+        finish(g0, g0 + 2, nc.vector, nc.sync)
+        finish_scalar(g0 + 2, g0 + 4, nc.scalar)
+        finish(g0 + 4, NBLK, nc.vector, nc.sync)

@@ -22,20 +22,15 @@ FLOPS = 2 * TOKENS * H * PHONES
 P = 128
 BLOCK = 512
 NBLK = TOKENS // BLOCK
-NPAIR = NBLK // 2
 DEPTH = 6
 NV = 2
 SLOTS = DEPTH * P
-AHEAD = 3
+STRIDED = 4
 GROUPS = ((0, 12), (12, 20), (20, 26), (26, 32))
+XBUFS = 6
 NEG_BIG = -3.0e38
 W_ENG = ("sv", "sv", "sv", "sv", "sv", "sv")
 EARLY_N = (2, 2, 3, 3, 3, 3)
-EARLY_ENG = ("s", "s", "s", "s", "s", "s")
-PHASES = 4
-V_PHASE = 1
-E_PHASE = 3
-SEED_POS = 4
 
 
 def tile_compositionalphoneticsmodel_t_kernel(tc, enc_output, feature2phone, mapping, out):
@@ -46,23 +41,23 @@ def tile_compositionalphoneticsmodel_t_kernel(tc, enc_output, feature2phone, map
 
     with ExitStack() as ctx:
         const = ctx.enter_context(tc.tile_pool(name="const", bufs=1))
-        xpool = ctx.enter_context(tc.tile_pool(name="xpool", bufs=4))
-        gpool = ctx.enter_context(tc.tile_pool(name="gpool", bufs=4))
-        cpool = ctx.enter_context(tc.tile_pool(name="cpool", bufs=8))
+        xpool = ctx.enter_context(tc.tile_pool(name="xpool", bufs=XBUFS))
+        rpool = ctx.enter_context(tc.tile_pool(name="rpool", bufs=2))
+        gpool = ctx.enter_context(tc.tile_pool(name="gpool", bufs=3))
+        cpool = ctx.enter_context(tc.tile_pool(name="cpool", bufs=6))
         apool = ctx.enter_context(tc.tile_pool(name="apool", bufs=6))
-        spool = ctx.enter_context(tc.tile_pool(name="spool", bufs=2))
+        spool = ctx.enter_context(tc.tile_pool(name="spool", bufs=4))
         ps_t = ctx.enter_context(tc.psum_pool(name="ps_t", bufs=3))
         ps_m = ctx.enter_context(tc.psum_pool(name="ps_m", bufs=3))
         ps_f = ctx.enter_context(tc.psum_pool(name="ps_f", bufs=1))
         ctx.enter_context(tc.manual_schedule())
 
         xs = {}
+        xrs = {}
         grs = {}
         cds = {}
         accs = {}
         pfs = {}
-        c0s = {}
-        tps = {}
         t3s = {}
 
         map2 = const.tile([P, PHONES], BF16)
@@ -76,7 +71,7 @@ def tile_compositionalphoneticsmodel_t_kernel(tc, enc_output, feature2phone, map
             nc.sync.dma_start(out=x[:], in_=enc_v[b])
             xs[b] = x
 
-        for b in range(4):
+        for b in range(XBUFS):
             load(b)
 
         part_i = const.tile([P, 1], I32)
@@ -233,26 +228,35 @@ def tile_compositionalphoneticsmodel_t_kernel(tc, enc_output, feature2phone, map
         logs = const.tile([P, NBLK * 4], F32)
         neg_l = const.tile([P, NBLK * 4], F32)
 
-        def a_bank(b, k, engine="s"):
+        def reorder(b):
+            xr = rpool.tile([P, 4 * H // 2], F32)
+            for h in range(2):
+                nc.scalar.copy(
+                    out=xr[:, h * 1024 : (h + 1) * 1024].rearrange("p (c u w) -> p c u w", u=2, w=P),
+                    in_=xs[b][:].bitcast(F32)[:, h * 1024 : (h + 1) * 1024].rearrange("p (c w u) -> p c u w", u=2, w=P),
+                )
+            xrs[b] = xr
+            if b + XBUFS - 1 < NBLK:
+                load(b + XBUFS - 1)
+
+        def a_bank(b, k):
             if k == 0:
                 gr = gpool.tile([P, 2 * BLOCK * 4], BF16, align_bytes=64)
                 grs[b] = gr
             g = k // 2
             sp = k % 2
-            xw = xs[b][:].bitcast(F32)
             grw = grs[b][:].bitcast(F32)
             pt = ps_t.tile([P, 4 * P], F32, tag="pt")
             for u in range(2):
                 for s2 in range(2):
                     col = (2 * sp + s2) * 512 + 256 * g
-                    nc.tensor.transpose(pt[:, (u * 2 + s2) * P : (u * 2 + s2 + 1) * P], xw[:, col + u : col + 256 : 2], ident_f[:])
+                    if b < STRIDED:
+                        words = xs[b][:].bitcast(F32)[:, col + u : col + 256 : 2]
+                    else:
+                        words = xrs[b][:, col + u * P : col + (u + 1) * P]
+                    nc.tensor.transpose(pt[:, (u * 2 + s2) * P : (u * 2 + s2 + 1) * P], words, ident_f[:])
             lo = g * 1024 + sp * 512
-            dst = grw[:, lo : lo + 512].rearrange("q (t u) -> q t u", u=2)
-            src = pt[:].rearrange("q (u t) -> q t u", u=2)
-            if engine == "v":
-                nc.vector.tensor_copy(out=dst, in_=src)
-            else:
-                nc.scalar.copy(out=dst, in_=src)
+            nc.scalar.copy(out=grw[:, lo : lo + 512].rearrange("q (t u) -> q t u", u=2), in_=pt[:].rearrange("q (u t) -> q t u", u=2))
 
         def quant(b, g):
             if g == 0:
@@ -287,40 +291,34 @@ def tile_compositionalphoneticsmodel_t_kernel(tc, enc_output, feature2phone, map
             else:
                 nc.vector.scalar_tensor_tensor(out=accs[b][:], in0=pm[:], scalar=gain[:, d : d + 1], in1=accs[b][:], op0=ALU.mult, op1=ALU.max)
 
-        def f_bank(b, h):
-            pf = ps_f.tile([P, 4 * P], F32, tag="pf%d" % h, name="pf%d" % h)
-            for s in range(4):
-                nc.tensor.transpose(pf[:, s * P : (s + 1) * P], accs[b][:, s * P : (s + 1) * P], perm2[:, h * P : (h + 1) * P])
-            pfs[(b, h)] = pf
-            if h == 0:
-                c0 = spool.tile([P, 4 * P], F32)
-                nc.scalar.copy(out=c0[:], in_=pf[:])
-                c0s[b] = c0
+        def f_bank(b, fb):
+            pf = ps_f.tile([P, 2, 2, P], F32, tag="pf%d" % fb, name="pf%d" % fb)
+            for s2 in range(2):
+                s = 2 * fb + s2
+                for h in range(2):
+                    nc.tensor.transpose(pf[:, s2, h, :], accs[b][:, s * P : (s + 1) * P], perm2[:, h * P : (h + 1) * P])
+            pfs[(b, fb)] = pf
 
-        def t_max(b):
-            if b % 2 == 0:
-                tp = spool.tile([P, 2, 4, P], F32)
-                tps[b // 2] = tp
-            nc.vector.tensor_tensor(out=tps[b // 2][:, b % 2, :, :].rearrange("p s c -> p (s c)"), in0=pfs[(b, 1)][:], in1=c0s[b][:], op=ALU.max)
+        def join(b, step):
+            for fb in range(2):
+                pf = pfs[(b, fb)]
+                if step == 0:
+                    t3 = spool.tile([P, 2, PHONEMES], F32)
+                    t3s[(b, fb)] = t3
+                    nc.vector.tensor_tensor(out=t3[:], in0=pf[:, :, 0, 64:128], in1=bias[:].unsqueeze(1).to_broadcast([P, 2, PHONEMES]), op=ALU.add)
+                elif step == 1:
+                    t3 = t3s[(b, fb)]
+                    nc.vector.tensor_tensor(out=t3[:], in0=pf[:, :, 1, 0:64], in1=t3[:], op=ALU.max)
+                else:
+                    vv = v_all[:, b * 256 + fb * 128 : b * 256 + (fb + 1) * 128].rearrange("p (s m) -> p s m", m=PHONEMES)
+                    nc.vector.tensor_tensor(out=vv, in0=pf[:, :, 0, 0:64], in1=t3s[(b, fb)][:], op=ALU.max)
 
-        def bias_add(j, eng, lo=0, hi=8):
-            if lo == 0:
-                t3 = spool.tile([P, 8, PHONEMES], F32)
-                t3s[j] = t3
-            eng.tensor_tensor(
-                out=t3s[j][:, lo:hi, :],
-                in0=tps[j][:].rearrange("p b s c -> p (b s) c")[:, lo:hi, 64:128],
-                in1=bias[:].unsqueeze(1).to_broadcast([P, hi - lo, PHONEMES]),
-                op=ALU.add,
-            )
+        def row_max(b):
+            vv = v_all[:, b * 256 : (b + 1) * 256].rearrange("p (s m) -> p s m", m=PHONEMES)
+            nc.vector.tensor_reduce(out=neg_max[:, b * 4 : (b + 1) * 4], in_=vv, axis=AX.X, op=ALU.max, negate=True)
 
-        def v_max(j, lo=0, hi=8):
-            vv = v_all[:, j * 512 + lo * 64 : j * 512 + hi * 64].rearrange("p (s m) -> p s m", m=PHONEMES)
-            nc.vector.tensor_tensor(out=vv, in0=tps[j][:].rearrange("p b s c -> p (b s) c")[:, lo:hi, 0:64], in1=t3s[j][:, lo:hi, :], op=ALU.max)
-            nc.vector.tensor_reduce(out=neg_max[:, j * 8 + lo : j * 8 + hi], in_=vv, axis=AX.X, op=ALU.max, negate=True)
-
-        def exps(j, lo=0, hi=8):
-            for i in range(j * 8 + lo, j * 8 + hi):
+        def exps(b):
+            for i in range(b * 4, b * 4 + 4):
                 ex = spool.tile([P, PHONEMES], F32)
                 nc.scalar.activation(
                     out=ex[:], in_=v_all[:, i * 64 : (i + 1) * 64], func=ACT.Exp,
@@ -333,23 +331,17 @@ def tile_compositionalphoneticsmodel_t_kernel(tc, enc_output, feature2phone, map
             nc.scalar.activation(out=logs[:, cols], in_=sums[:, cols], func=ACT.Ln)
             eng.tensor_tensor(out=neg_l[:, cols], in0=neg_max[:, cols], in1=logs[:, cols], op=ALU.subtract)
 
-        def finish(b0, b1, eng, queue):
+        def finish(b0, b1, eng):
             n = (b1 - b0) * 4
-            vg = v_all[:, b0 * 256 : b1 * 256]
-            vg3 = vg.rearrange("p (i m) -> p i m", m=PHONEMES)
+            vg3 = v_all[:, b0 * 256 : b1 * 256].rearrange("p (i m) -> p i m", m=PHONEMES)
             eng.tensor_tensor(out=vg3, in0=vg3, in1=neg_l[:, b0 * 4 : b1 * 4].unsqueeze(2).to_broadcast([P, n, PHONEMES]), op=ALU.add)
-            queue.dma_start(out=out_v[:, b0:b1, :], in_=vg.rearrange("p (n f) -> p n f", f=256))
 
-        def finish_scalar(b0, b1, queue):
+        def finish_scalar(b0, b1):
             for i in range(b0 * 4, b1 * 4):
                 nc.scalar.activation(out=v_all[:, i * 64 : (i + 1) * 64], in_=v_all[:, i * 64 : (i + 1) * 64], func=ACT.Identity, bias=neg_l[:, i : i + 1], scale=1.0)
-            queue.dma_start(out=out_v[:, b0:b1, :], in_=v_all[:, b0 * 256 : b1 * 256].rearrange("p (n f) -> p n f", f=256))
 
-        def a_block(b, ks, engine="s"):
-            for k in ks:
-                a_bank(b, k, engine)
-                if k == 3 and b + 4 < NBLK:
-                    load(b + 4)
+        def store(b0, b1, queue):
+            queue.dma_start(out=out_v[:, b0:b1, :], in_=v_all[:, b0 * 256 : b1 * 256].rearrange("p (n f) -> p n f", f=256))
 
         wt_make(0)
         wt_make(1)
@@ -357,7 +349,7 @@ def tile_compositionalphoneticsmodel_t_kernel(tc, enc_output, feature2phone, map
         sgw_make(1)
         sel_make(1)
         sgw_make(2)
-        early = [(b, k) for b in range(4) for k in range(4)]
+        early = [(b, k) for b in range(STRIDED) for k in range(4)]
         for d in range(DEPTH):
             wslot_make(d, W_ENG[d])
             if d + 2 < DEPTH:
@@ -365,7 +357,7 @@ def tile_compositionalphoneticsmodel_t_kernel(tc, enc_output, feature2phone, map
             if d + 3 < DEPTH:
                 sgw_make(d + 3)
             for b, k in early[sum(EARLY_N[:d]) : sum(EARLY_N[: d + 1])]:
-                a_block(b, [k], EARLY_ENG[d])
+                a_bank(b, k)
             wslot_quant(d)
             if d == 3:
                 quant(0, 0)
@@ -373,92 +365,90 @@ def tile_compositionalphoneticsmodel_t_kernel(tc, enc_output, feature2phone, map
             if d == 4:
                 gain_make()
                 perm_make()
-        for b, k in early[sum(EARLY_N) :]:
-            a_block(b, [k])
+        for b in range(XBUFS, XBUFS + STRIDED - 1):
+            load(b)
         quant(1, 0)
         quant(1, 1)
         mx(0, 0)
         mx(1, 0)
+        reorder(4)
         quant(2, 0)
         quant(2, 1)
-        quant(3, 0)
-        quant(3, 1)
 
         pending = []
-        finished = 0
-        for j in range(NPAIR):
-            p0, p1 = 2 * j, 2 * j + 1
-            n0, n1 = p0 + 2, p1 + 2
-            if j == 0:
-                a_list = [4, 5, 6, 7]
-                q_list = []
+        stores = []
+        for h in range(NBLK):
+            p0 = h - h % 2
+            if h % 2 == 0:
+                m_run = [(b, d) for d in (1, 2, 3) for b in (p0, p0 + 1)]
             else:
-                a_list = [b for b in (p0 + 2 * AHEAD, p1 + 2 * AHEAD) if b < NBLK]
-                q_list = [b for b in (p0 + 2 * AHEAD - 2, p1 + 2 * AHEAD - 2) if b < NBLK]
-            f_list = [p0 - 2, p1 - 2] if 1 <= j <= NPAIR else []
-            m_banks = []
-            if j < NPAIR:
-                m_banks += [(b, d) for d in range(1, DEPTH) for b in (p0, p1)]
-            if n0 < NBLK:
-                m_banks = m_banks[:SEED_POS] + [(n0, 0), (n1, 0)] + m_banks[SEED_POS:]
-            a_banks = [("a", b, k) for b in a_list for k in range(4)]
-            na = len(a_banks) // 2
-            t_banks = []
-            if f_list:
-                t_banks += [("f", f_list[0], 0), ("f", f_list[0], 1)]
-            t_banks += a_banks[:na]
-            if f_list:
-                t_banks += [("f", f_list[1], 0), ("f", f_list[1], 1)]
-            t_banks += a_banks[na:]
-            quants = [(b, g) for b in q_list for g in range(2)]
-            for ph in range(PHASES):
-                for b, d in m_banks[len(m_banks) * ph // PHASES : len(m_banks) * (ph + 1) // PHASES]:
-                    mx(b, d)
-                if ph == V_PHASE and j >= 2:
-                    v_max(j - 2)
-                if ph == E_PHASE and j >= 2:
-                    exps(j - 2)
-                    for gi in range(len(GROUPS)):
-                        if GROUPS[gi][1] == 2 * (j - 1):
-                            group_ln(gi, nc.gpsimd)
-                            pending.extend(range(GROUPS[gi][0], GROUPS[gi][1], 2))
-                tp_n = 2 if j == NPAIR - 1 else PHASES
-                for kind, b, k in t_banks[len(t_banks) * min(ph, tp_n) // tp_n : len(t_banks) * min(ph + 1, tp_n) // tp_n]:
-                    if kind == "a":
-                        a_block(b, [k])
-                    else:
-                        f_bank(b, k)
-                        if k == 1:
-                            t_max(b)
-                            if b % 2 == 1:
-                                bias_add(b // 2, nc.gpsimd)
-                for b, g in quants[len(quants) * ph // PHASES : len(quants) * (ph + 1) // PHASES]:
-                    quant(b, g)
-                if ph % 2 == 1 and finished < len(pending):
-                    finish(pending[finished], pending[finished] + 2, nc.gpsimd, nc.gpsimd)
-                    finished += 1
-            if j == 0:
-                for b in (4, 5):
-                    quant(b, 0)
-                    quant(b, 1)
+                m_run = [(b, d) for d in (4, 5) for b in (p0, p0 + 1)]
+                if p0 + 2 < NBLK:
+                    m_run += [(p0 + 2, 0), (p0 + 3, 0)]
+            for b, d in m_run:
+                mx(b, d)
+            a = h + 4
+            q = h + 3
+            f = h - 2
+            for k in range(4):
+                if a < NBLK:
+                    a_bank(a, k)
+                if k < 2 and f >= 0:
+                    f_bank(f, k)
+            if f >= 1:
+                row_max(f - 1)
+            if f >= 0:
+                join(f, 0)
+            if q < NBLK:
+                quant(q, 0)
+            if f >= 0:
+                join(f, 1)
+            if q < NBLK:
+                quant(q, 1)
+            if f >= 0:
+                join(f, 2)
+            if a + 1 < NBLK:
+                reorder(a + 1)
+            if f >= 2:
+                exps(f - 2)
+                for gi in range(len(GROUPS)):
+                    if GROUPS[gi][1] == f - 1:
+                        group_ln(gi, nc.gpsimd)
+                        pending.extend(range(GROUPS[gi][0], GROUPS[gi][1], 2))
+            if stores:
+                s0 = stores.pop(0)
+                store(s0, s0 + 2, nc.sync)
+            if pending:
+                s0 = pending.pop(0)
+                finish(s0, s0 + 2, nc.gpsimd)
+                stores.append(s0)
 
-        assert finished == len(pending)
-        z = NPAIR - 1
-        v_max(z - 1)
-        f_bank(2 * z, 0)
-        f_bank(2 * z, 1)
-        f_bank(2 * z + 1, 0)
+        assert not pending
+        for s0 in stores:
+            store(s0, s0 + 2, nc.sync)
+        z = NBLK - 1
+        f_bank(z - 1, 0)
+        f_bank(z - 1, 1)
+        row_max(z - 2)
+        exps(z - 3)
+        join(z - 1, 0)
+        join(z - 1, 1)
+        join(z - 1, 2)
+        f_bank(z, 0)
+        f_bank(z, 1)
+        exps(z - 2)
+        row_max(z - 1)
+        join(z, 0)
+        join(z, 1)
+        join(z, 2)
         exps(z - 1)
-        for b in (2 * z, 2 * z + 1):
-            lo = 4 * (b % 2)
-            t_max(b)
-            if b == 2 * z:
-                f_bank(b + 1, 1)
-            bias_add(z, nc.vector, lo, lo + 4)
-            v_max(z, lo, lo + 4)
-            exps(z, lo, lo + 4)
+        row_max(z)
+        exps(z)
         g0 = GROUPS[-1][0]
         group_ln(len(GROUPS) - 1, nc.vector)
-        finish(g0, g0 + 2, nc.vector, nc.sync)
-        finish_scalar(g0 + 2, g0 + 4, nc.scalar)
-        finish(g0 + 4, NBLK, nc.vector, nc.sync)
+        finish(g0, g0 + 2, nc.vector)
+        store(g0, g0 + 2, nc.sync)
+        finish_scalar(g0 + 2, g0 + 4)
+        store(g0 + 2, g0 + 4, nc.scalar)
+        finish(g0 + 4, NBLK, nc.vector)
+        store(g0 + 4, NBLK, nc.sync)

@@ -25,12 +25,12 @@ NBLK = TOKENS // BLOCK
 DEPTH = 6
 NV = 2
 SLOTS = DEPTH * P
-STRIDED = 4
+STRIDED = 3
 GROUPS = ((0, 12), (12, 20), (20, 26), (26, 32))
 XBUFS = 6
 NEG_BIG = -3.0e38
 W_ENG = ("sv", "sv", "sv", "sv", "sv", "sv")
-EARLY_N = (2, 2, 3, 3, 3, 3)
+EARLY_N = (2, 2, 2, 2, 2, 2)
 
 
 def tile_compositionalphoneticsmodel_t_kernel(tc, enc_output, feature2phone, mapping, out):
@@ -228,16 +228,17 @@ def tile_compositionalphoneticsmodel_t_kernel(tc, enc_output, feature2phone, map
         logs = const.tile([P, NBLK * 4], F32)
         neg_l = const.tile([P, NBLK * 4], F32)
 
-        def reorder(b):
-            xr = rpool.tile([P, 4 * H // 2], F32)
-            for h in range(2):
-                nc.scalar.copy(
-                    out=xr[:, h * 1024 : (h + 1) * 1024].rearrange("p (c u w) -> p c u w", u=2, w=P),
-                    in_=xs[b][:].bitcast(F32)[:, h * 1024 : (h + 1) * 1024].rearrange("p (c w u) -> p c u w", u=2, w=P),
-                )
-            xrs[b] = xr
-            if b + XBUFS - 1 < NBLK:
-                load(b + XBUFS - 1)
+        def reorder(b, g):
+            if g == 0:
+                xr = rpool.tile([P, 2, 4, 2, P], F32)
+                xrs[b] = xr
+            src = xs[b][:].bitcast(F32)
+            nc.scalar.copy(
+                out=xrs[b][:, g, :, :, :],
+                in_=src.rearrange("p (s c) -> p s c", s=4)[:, :, g * 256 : (g + 1) * 256].rearrange("p s (w u) -> p s u w", u=2),
+            )
+            if g == 1 and b + XBUFS < NBLK:
+                load(b + XBUFS)
 
         def a_bank(b, k):
             if k == 0:
@@ -249,14 +250,16 @@ def tile_compositionalphoneticsmodel_t_kernel(tc, enc_output, feature2phone, map
             pt = ps_t.tile([P, 4 * P], F32, tag="pt")
             for u in range(2):
                 for s2 in range(2):
-                    col = (2 * sp + s2) * 512 + 256 * g
+                    s = 2 * sp + s2
                     if b < STRIDED:
-                        words = xs[b][:].bitcast(F32)[:, col + u : col + 256 : 2]
+                        words = xs[b][:].bitcast(F32)[:, s * 512 + 256 * g + u : s * 512 + 256 * g + 256 : 2]
                     else:
-                        words = xrs[b][:, col + u * P : col + (u + 1) * P]
+                        words = xrs[b][:, g, s, u, :]
                     nc.tensor.transpose(pt[:, (u * 2 + s2) * P : (u * 2 + s2 + 1) * P], words, ident_f[:])
             lo = g * 1024 + sp * 512
             nc.scalar.copy(out=grw[:, lo : lo + 512].rearrange("q (t u) -> q t u", u=2), in_=pt[:].rearrange("q (u t) -> q t u", u=2))
+            if b < STRIDED and k == 3 and b + XBUFS < NBLK:
+                load(b + XBUFS)
 
         def quant(b, g):
             if g == 0:
@@ -299,26 +302,25 @@ def tile_compositionalphoneticsmodel_t_kernel(tc, enc_output, feature2phone, map
                     nc.tensor.transpose(pf[:, s2, h, :], accs[b][:, s * P : (s + 1) * P], perm2[:, h * P : (h + 1) * P])
             pfs[(b, fb)] = pf
 
-        def join(b, step):
-            for fb in range(2):
-                pf = pfs[(b, fb)]
-                if step == 0:
-                    t3 = spool.tile([P, 2, PHONEMES], F32)
-                    t3s[(b, fb)] = t3
-                    nc.vector.tensor_tensor(out=t3[:], in0=pf[:, :, 0, 64:128], in1=bias[:].unsqueeze(1).to_broadcast([P, 2, PHONEMES]), op=ALU.add)
-                elif step == 1:
-                    t3 = t3s[(b, fb)]
-                    nc.vector.tensor_tensor(out=t3[:], in0=pf[:, :, 1, 0:64], in1=t3[:], op=ALU.max)
-                else:
-                    vv = v_all[:, b * 256 + fb * 128 : b * 256 + (fb + 1) * 128].rearrange("p (s m) -> p s m", m=PHONEMES)
-                    nc.vector.tensor_tensor(out=vv, in0=pf[:, :, 0, 0:64], in1=t3s[(b, fb)][:], op=ALU.max)
+        def join(b, fb, step):
+            pf = pfs[(b, fb)]
+            if step == 0:
+                t3 = spool.tile([P, 2, PHONEMES], F32)
+                t3s[(b, fb)] = t3
+                nc.vector.tensor_tensor(out=t3[:], in0=pf[:, :, 0, 64:128], in1=bias[:].unsqueeze(1).to_broadcast([P, 2, PHONEMES]), op=ALU.add)
+            elif step == 1:
+                t3 = t3s[(b, fb)]
+                nc.vector.tensor_tensor(out=t3[:], in0=pf[:, :, 1, 0:64], in1=t3[:], op=ALU.max)
+            else:
+                vv = v_all[:, b * 256 + fb * 128 : b * 256 + (fb + 1) * 128].rearrange("p (s m) -> p s m", m=PHONEMES)
+                nc.vector.tensor_tensor(out=vv, in0=pf[:, :, 0, 0:64], in1=t3s[(b, fb)][:], op=ALU.max)
 
-        def row_max(b):
-            vv = v_all[:, b * 256 : (b + 1) * 256].rearrange("p (s m) -> p s m", m=PHONEMES)
-            nc.vector.tensor_reduce(out=neg_max[:, b * 4 : (b + 1) * 4], in_=vv, axis=AX.X, op=ALU.max, negate=True)
+        def row_max(b, fb):
+            vv = v_all[:, b * 256 + fb * 128 : b * 256 + (fb + 1) * 128].rearrange("p (s m) -> p s m", m=PHONEMES)
+            nc.vector.tensor_reduce(out=neg_max[:, b * 4 + fb * 2 : b * 4 + fb * 2 + 2], in_=vv, axis=AX.X, op=ALU.max, negate=True)
 
-        def exps(b):
-            for i in range(b * 4, b * 4 + 4):
+        def exps(b, fb):
+            for i in range(b * 4 + fb * 2, b * 4 + fb * 2 + 2):
                 ex = spool.tile([P, PHONEMES], F32)
                 nc.scalar.activation(
                     out=ex[:], in_=v_all[:, i * 64 : (i + 1) * 64], func=ACT.Exp,
@@ -365,60 +367,58 @@ def tile_compositionalphoneticsmodel_t_kernel(tc, enc_output, feature2phone, map
             if d == 4:
                 gain_make()
                 perm_make()
-        for b in range(XBUFS, XBUFS + STRIDED - 1):
-            load(b)
         quant(1, 0)
         quant(1, 1)
         mx(0, 0)
         mx(1, 0)
-        reorder(4)
+        reorder(3, 0)
+        reorder(3, 1)
         quant(2, 0)
-        quant(2, 1)
 
         pending = []
         stores = []
-        for h in range(NBLK):
-            p0 = h - h % 2
-            if h % 2 == 0:
-                m_run = [(b, d) for d in (1, 2, 3) for b in (p0, p0 + 1)]
-            else:
-                m_run = [(b, d) for d in (4, 5) for b in (p0, p0 + 1)]
+        NPH = 2 * NBLK
+        for i in range(NPH + 5):
+            p0 = i // 4 * 2
+            m_run = []
+            if i < NPH:
+                m_all = [(b, d) for d in range(1, DEPTH) for b in (p0, p0 + 1)]
                 if p0 + 2 < NBLK:
-                    m_run += [(p0 + 2, 0), (p0 + 3, 0)]
-            for b, d in m_run:
-                mx(b, d)
-            a = h + 4
-            q = h + 3
-            f = h - 2
-            for k in range(4):
-                if a < NBLK:
-                    a_bank(a, k)
-                if k < 2 and f >= 0:
-                    f_bank(f, k)
-            if f >= 1:
-                row_max(f - 1)
-            if f >= 0:
-                join(f, 0)
-            if q < NBLK:
-                quant(q, 0)
-            if f >= 0:
-                join(f, 1)
-            if q < NBLK:
-                quant(q, 1)
-            if f >= 0:
-                join(f, 2)
-            if a + 1 < NBLK:
-                reorder(a + 1)
-            if f >= 2:
-                exps(f - 2)
-                for gi in range(len(GROUPS)):
-                    if GROUPS[gi][1] == f - 1:
+                    m_all += [(p0 + 2, 0), (p0 + 3, 0)]
+                m_run = m_all[i % 4 * 3 : i % 4 * 3 + 3]
+            a = i + 6
+            q = i + 5
+            r = i + 8
+            f = i - 3
+            for n in range(3):
+                if n < len(m_run):
+                    mx(*m_run[n])
+                if n < 2 and 0 <= f - 1 < NPH:
+                    join((f - 1) // 2, (f - 1) % 2, n + 1)
+            if a < NPH:
+                a_bank(a // 2, a % 2 * 2)
+            if 0 <= f < NPH:
+                f_bank(f // 2, f % 2)
+            if a < NPH:
+                a_bank(a // 2, a % 2 * 2 + 1)
+            if 0 <= f - 1 < NPH:
+                row_max((f - 1) // 2, (f - 1) % 2)
+            if q < NPH:
+                quant(q // 2, q % 2)
+            if 0 <= f < NPH:
+                join(f // 2, f % 2, 0)
+            if r < NPH:
+                reorder(r // 2, r % 2)
+            if 0 <= f - 2 < NPH:
+                exps((f - 2) // 2, (f - 2) % 2)
+                for gi in range(len(GROUPS) - 1):
+                    if 2 * GROUPS[gi][1] == f - 1:
                         group_ln(gi, nc.gpsimd)
                         pending.extend(range(GROUPS[gi][0], GROUPS[gi][1], 2))
-            if stores:
+            if i % 2 == 1 and stores:
                 s0 = stores.pop(0)
                 store(s0, s0 + 2, nc.sync)
-            if pending:
+            if i % 2 == 1 and pending:
                 s0 = pending.pop(0)
                 finish(s0, s0 + 2, nc.gpsimd)
                 stores.append(s0)
@@ -426,24 +426,6 @@ def tile_compositionalphoneticsmodel_t_kernel(tc, enc_output, feature2phone, map
         assert not pending
         for s0 in stores:
             store(s0, s0 + 2, nc.sync)
-        z = NBLK - 1
-        f_bank(z - 1, 0)
-        f_bank(z - 1, 1)
-        row_max(z - 2)
-        exps(z - 3)
-        join(z - 1, 0)
-        join(z - 1, 1)
-        join(z - 1, 2)
-        f_bank(z, 0)
-        f_bank(z, 1)
-        exps(z - 2)
-        row_max(z - 1)
-        join(z, 0)
-        join(z, 1)
-        join(z, 2)
-        exps(z - 1)
-        row_max(z)
-        exps(z)
         g0 = GROUPS[-1][0]
         group_ln(len(GROUPS) - 1, nc.vector)
         finish(g0, g0 + 2, nc.vector)

@@ -25,12 +25,19 @@ NBLK = TOKENS // BLOCK
 DEPTH = 6
 NV = 2
 SLOTS = DEPTH * P
-STRIDED = 3
-GROUPS = ((0, 12), (12, 20), (20, 26), (26, 32))
+STRIDED = 1
+GROUPS = ((0, 14), (14, 22), (22, 28), (28, 32))
 XBUFS = 6
+HEAD_X = (2, 2, 2, 2, 1, 1)
+HEAD_R = (2, 2, 2, 2, 1, 0)
+HEAD_Q = (0, 1, 1, 1, 1, 1)
+R_LEAD = 4
+X_RUN = (3, 3, 2)
+F_RUN = (1, 1, 2)
+Q_RUN = (1, 2, 1)
+WARM = 4
 NEG_BIG = -3.0e38
 W_ENG = ("sv", "sv", "sv", "sv", "sv", "sv")
-EARLY_N = (2, 2, 2, 2, 2, 2)
 
 
 def tile_compositionalphoneticsmodel_t_kernel(tc, enc_output, feature2phone, mapping, out):
@@ -42,7 +49,7 @@ def tile_compositionalphoneticsmodel_t_kernel(tc, enc_output, feature2phone, map
     with ExitStack() as ctx:
         const = ctx.enter_context(tc.tile_pool(name="const", bufs=1))
         xpool = ctx.enter_context(tc.tile_pool(name="xpool", bufs=XBUFS))
-        rpool = ctx.enter_context(tc.tile_pool(name="rpool", bufs=2))
+        rpool = ctx.enter_context(tc.tile_pool(name="rpool", bufs=3))
         gpool = ctx.enter_context(tc.tile_pool(name="gpool", bufs=3))
         cpool = ctx.enter_context(tc.tile_pool(name="cpool", bufs=6))
         apool = ctx.enter_context(tc.tile_pool(name="apool", bufs=6))
@@ -64,20 +71,21 @@ def tile_compositionalphoneticsmodel_t_kernel(tc, enc_output, feature2phone, map
         nc.sync.dma_start(out=map2[0:64, :], in_=mapping)
         nc.sync.dma_start(out=map2[64:128, :], in_=mapping)
         wl = const.tile([P, 4, 2, PHONES], BF16)
-        nc.sync.dma_start(out=wl[:].rearrange("q (g u) e p -> q g (u e p)", g=2), in_=w_v)
 
-        def load(b):
+        def load(b, parts=1):
             x = xpool.tile([P, 4 * H], BF16)
-            nc.sync.dma_start(out=x[:], in_=enc_v[b])
+            n = 4 * H // parts
+            for i in range(parts):
+                nc.sync.dma_start(out=x[:, i * n : (i + 1) * n], in_=enc_v[b][:, i * n : (i + 1) * n])
             xs[b] = x
 
-        for b in range(XBUFS):
+        nc.sync.dma_start(out=wl[:].rearrange("q (g u) e p -> q g (u e p)", g=2), in_=w_v)
+        load(0, 2)
+        for b in range(1, XBUFS):
             load(b)
 
         part_i = const.tile([P, 1], I32)
         nc.gpsimd.iota(part_i[:], pattern=[[0, 1]], base=0, channel_multiplier=1)
-        slot_i = const.tile([P, NV * DEPTH], I32)
-        nc.gpsimd.iota(slot_i[:], pattern=[[2 * DEPTH, NV], [1, DEPTH]], base=0, channel_multiplier=0)
         iota_i = const.tile([P, P], I32)
         nc.gpsimd.iota(iota_i[:], pattern=[[1, P]], base=0, channel_multiplier=0)
         ident_b = const.tile([P, P], BF16)
@@ -87,69 +95,43 @@ def tile_compositionalphoneticsmodel_t_kernel(tc, enc_output, feature2phone, map
 
         part_f = const.tile([P, 1], F32)
         nc.vector.tensor_copy(out=part_f[:], in_=part_i[:])
-        slot_f = const.tile([P, NV * DEPTH], F32)
-        nc.vector.tensor_copy(out=slot_f[:], in_=slot_i[:])
-        half_d = const.tile([P, 1], F32)
-        nc.vector.tensor_scalar(out=half_d[:], in0=part_f[:], scalar1=64.0, scalar2=float(DEPTH), op0=ALU.is_ge, op1=ALU.mult)
-        want0 = const.tile([P, NV * DEPTH], F32)
-        nc.vector.tensor_scalar(out=want0[:], in0=slot_f[:], scalar1=half_d[:, 0:1], scalar2=None, op0=ALU.add)
+        base = const.tile([P, 1], F32)
+        nc.vector.tensor_scalar(out=base[:], in0=part_f[:], scalar1=64.0, scalar2=float(DEPTH), op0=ALU.is_ge, op1=ALU.mult)
         iota_f = const.tile([P, P], F32)
         nc.vector.tensor_copy(out=iota_f[:], in_=iota_i[:])
         tri = const.tile([P, P], BF16)
         nc.vector.tensor_scalar(out=tri[:], in0=iota_f[:], scalar1=part_f[:, 0:1], scalar2=None, op0=ALU.is_gt)
-        ones = const.tile([P, P], BF16)
+        ones = const.tile([P, BLOCK], BF16)
         nc.vector.memset(ones[:], 1.0)
-        gain_b = const.tile([P, NV, 32], BF16)
-        nc.vector.memset(gain_b[:], 0.0)
+        warm_p = ps_m.tile([P, BLOCK], F32, tag="pm")
+        for i in range(WARM):
+            nc.tensor.matmul(out=warm_p[:], lhsT=ones[:, 0:P], rhs=ones[:], start=True, stop=True)
 
         mask = const.tile([P, PHONES], F32)
         nc.vector.tensor_single_scalar(out=mask[:], in_=map2[:], scalar=0.0, op=ALU.is_gt)
         incl = const.tile([P, PHONES], F32)
         nc.vector.tensor_tensor_scan(out=incl[:], data0=mask[:], data1=mask[:], initial=0.0, op0=ALU.add, op1=ALU.max)
+        count = incl[:, PHONES - 1 : PHONES]
+        act_b = const.tile([P, NV, 32], BF16)
+        for h in range(NV):
+            nc.vector.tensor_scalar(
+                out=act_b[:, h, :], in0=count.to_broadcast([P, 32]), scalar1=base[:, 0:1], scalar2=float(2 * DEPTH * h),
+                op0=ALU.subtract, op1=ALU.is_gt,
+            )
+        active = const.tile([P, NV], F32)
+        nc.vector.tensor_copy(out=active[:], in_=act_b[:, :, 0])
         rank1 = const.tile([P, PHONES], F32)
         nc.vector.tensor_tensor(out=rank1[:], in0=incl[:], in1=mask[:], op=ALU.mult)
-        count = incl[:, PHONES - 1 : PHONES]
-        valid = const.tile([P, NV * DEPTH], F32)
-        nc.vector.tensor_scalar(out=valid[:], in0=want0[:], scalar1=count, scalar2=None, op0=ALU.is_lt)
-        valid_v = valid[:].rearrange("v (h d) -> v h d", d=DEPTH)
-        active = valid_v[:, :, 0]
-        act_b = const.tile([P, NV, 32], BF16)
-        nc.vector.tensor_copy(out=act_b[:], in_=valid_v[:, :, 0:1].to_broadcast([P, NV, 32]))
-        want_t = const.tile([P, NV * DEPTH], F32)
-        nc.vector.tensor_tensor(out=want_t[:], in0=want0[:], in1=valid[:], op=ALU.mult)
-        want1 = const.tile([P, NV * DEPTH], F32)
-        nc.vector.tensor_single_scalar(out=want1[:], in_=want_t[:], scalar=1.0, op=ALU.add)
-
-        lid_p = ps_m.tile([P, NV, 32], F32, tag="pm")
-        nc.tensor.matmul(out=lid_p[:, 0, :], lhsT=tri[:], rhs=act_b[:, 0, :], start=True, stop=True)
-        nc.tensor.matmul(out=lid_p[:, 1, :], lhsT=ones[:], rhs=act_b[:, 0, :], start=True, stop=False)
-        nc.tensor.matmul(out=lid_p[:, 1, :], lhsT=tri[:], rhs=act_b[:, 1, :], start=False, stop=True)
-
-        sgw = const.tile([P, NV * DEPTH, PHONES], BF16)
-        gain_v = const.tile([P, NV * DEPTH], F32)
-
-        def sgw_make(d):
-            for h in range(NV):
-                j = h * DEPTH + d
-                nc.vector.scalar_tensor_tensor(
-                    out=sgw[:, j, :], in0=rank1[:], scalar=want1[:, j : j + 1], in1=map2[:],
-                    op0=ALU.is_equal, op1=ALU.mult, accum_out=gain_v[:, j : j + 1],
-                )
-
-        sgw_make(0)
-
-        lid_t = const.tile([P, NV], F32)
-        nc.vector.scalar_tensor_tensor(out=lid_t[:], in0=lid_p[:, :, 0], scalar=1.0, in1=active, op0=ALU.add, op1=ALU.mult)
-        lane_id = const.tile([P, NV], F32)
-        nc.vector.tensor_single_scalar(out=lane_id[:], in_=lid_t[:], scalar=-1.0, op=ALU.add)
-        compact = const.tile([P, NV, P], BF16)
+        rel = const.tile([P, NV, PHONES], BF16)
+        left_b = const.tile([P, NV, 32], BF16)
         for h in range(NV):
-            nc.vector.tensor_scalar(out=compact[:, h, :], in0=iota_f[:], scalar1=lane_id[:, h : h + 1], scalar2=None, op0=ALU.is_equal)
-        tg1 = const.tile([P, 1], F32)
-        nc.vector.scalar_tensor_tensor(out=tg1[:], in0=lid_p[:, 1, 0:1], scalar=lane_id[:, 0:1], in1=valid_v[:, 1, 0:1], op0=ALU.subtract, op1=ALU.mult)
-        tgt_b = const.tile([P, NV], BF16)
-        nc.vector.tensor_copy(out=tgt_b[:, 0:1], in_=lane_id[:, 0:1])
-        nc.vector.tensor_scalar(out=tgt_b[:, 1:2], in0=tg1[:], scalar1=lane_id[:, 0:1], scalar2=None, op0=ALU.add)
+            nc.vector.tensor_scalar(
+                out=rel[:, h, :], in0=rank1[:], scalar1=base[:, 0:1], scalar2=float(2 * DEPTH * h + 1), op0=ALU.subtract, op1=ALU.subtract
+            )
+            nc.vector.tensor_scalar(
+                out=left_b[:, h, :], in0=count.to_broadcast([P, 32]), scalar1=base[:, 0:1], scalar2=float(2 * DEPTH * h),
+                op0=ALU.subtract, op1=ALU.subtract,
+            )
 
         wt = []
 
@@ -165,16 +147,9 @@ def tile_compositionalphoneticsmodel_t_kernel(tc, enc_output, feature2phone, map
         sel = const.tile([P, DEPTH, 2, P], BF16)
 
         def sel_make(d):
-            sel_p = ps_f.tile([P, 2, P], F32, tag="pf%d" % (d % 2), name="sel_p")
+            sel_p = ps_f.tile([P, 2, P], BF16, tag="pf%d" % (d % 2), name="sel_p")
             for c in range(2):
-                for h in range(NV):
-                    nc.tensor.matmul(
-                        out=sel_p[:, c, :],
-                        lhsT=sgw[:, h * DEPTH + d, c * P : (c + 1) * P],
-                        rhs=compact[:, h, :],
-                        start=(h == 0),
-                        stop=(h == NV - 1),
-                    )
+                nc.tensor.transpose(sel_p[:, c, :], takes[:, d, c * P : (c + 1) * P], ident_b[:])
             nc.scalar.activation(out=sel[:, d, :, :], in_=sel_p[:], func=ACT.Sign)
 
         wg = const.tile([P, 2, DEPTH, P * 4], BF16, align_bytes=64)
@@ -209,11 +184,7 @@ def tile_compositionalphoneticsmodel_t_kernel(tc, enc_output, feature2phone, map
         bias = const.tile([P, PHONEMES], F32)
 
         def gain_make():
-            nc.vector.tensor_copy(out=gain_b[:, :, 0:DEPTH], in_=gain_v[:].rearrange("v (h d) -> v h d", d=DEPTH))
-            gain_p = ps_f.tile([P, 32], F32, tag="pf0")
-            for h in range(NV):
-                nc.tensor.matmul(out=gain_p[:], lhsT=compact[:, h, :], rhs=gain_b[:, h, :], start=(h == 0), stop=(h == NV - 1))
-            nc.vector.tensor_single_scalar(out=gain[:], in_=gain_p[:, 0:DEPTH], scalar=1.0 / 32.0, op=ALU.mult)
+            nc.vector.tensor_single_scalar(out=gain[:], in_=gain_l[:], scalar=1.0 / 32.0, op=ALU.mult)
 
         def perm_make():
             row_p = ps_f.tile([P, NV * P], F32, tag="pf1")
@@ -228,40 +199,42 @@ def tile_compositionalphoneticsmodel_t_kernel(tc, enc_output, feature2phone, map
         logs = const.tile([P, NBLK * 4], F32)
         neg_l = const.tile([P, NBLK * 4], F32)
 
-        def reorder(b, g):
-            if g == 0:
-                xr = rpool.tile([P, 2, 4, 2, P], F32)
+        def reorder(n, eng="s"):
+            b, k = n // 4, n % 4
+            g, sp = k // 2, k % 2
+            if k == 0:
+                xr = rpool.tile([P, 4, 2, 2, P], F32)
                 xrs[b] = xr
-            src = xs[b][:].bitcast(F32)
-            nc.scalar.copy(
-                out=xrs[b][:, g, :, :, :],
-                in_=src.rearrange("p (s c) -> p s c", s=4)[:, :, g * 256 : (g + 1) * 256].rearrange("p s (w u) -> p s u w", u=2),
-            )
-            if g == 1 and b + XBUFS < NBLK:
+            src = xs[b][:].bitcast(F32).rearrange("p (s c) -> p s c", s=4)[:, 2 * sp : 2 * sp + 2, g * 256 : (g + 1) * 256].rearrange("p s (w u) -> p s u w", u=2)
+            if eng == "v":
+                nc.vector.tensor_copy(out=xrs[b][:, k, :, :, :], in_=src)
+            else:
+                nc.scalar.copy(out=xrs[b][:, k, :, :, :], in_=src)
+            if k == 3 and b + XBUFS < NBLK:
                 load(b + XBUFS)
 
-        def a_bank(b, k):
+        def a_bank(n):
+            b, k = n // 4, n % 4
             if k == 0:
                 gr = gpool.tile([P, 2 * BLOCK * 4], BF16, align_bytes=64)
                 grs[b] = gr
-            g = k // 2
-            sp = k % 2
+            g, sp = k // 2, k % 2
             grw = grs[b][:].bitcast(F32)
             pt = ps_t.tile([P, 4 * P], F32, tag="pt")
             for u in range(2):
                 for s2 in range(2):
-                    s = 2 * sp + s2
                     if b < STRIDED:
-                        words = xs[b][:].bitcast(F32)[:, s * 512 + 256 * g + u : s * 512 + 256 * g + 256 : 2]
+                        lo = (2 * sp + s2) * 512 + 256 * g
+                        words = xs[b][:].bitcast(F32)[:, lo + u : lo + 256 : 2]
                     else:
-                        words = xrs[b][:, g, s, u, :]
+                        words = xrs[b][:, k, s2, u, :]
                     nc.tensor.transpose(pt[:, (u * 2 + s2) * P : (u * 2 + s2 + 1) * P], words, ident_f[:])
-            lo = g * 1024 + sp * 512
-            nc.scalar.copy(out=grw[:, lo : lo + 512].rearrange("q (t u) -> q t u", u=2), in_=pt[:].rearrange("q (u t) -> q t u", u=2))
+            nc.scalar.copy(out=grw[:, k * 512 : (k + 1) * 512].rearrange("q (t u) -> q t u", u=2), in_=pt[:].rearrange("q (u t) -> q t u", u=2))
             if b < STRIDED and k == 3 and b + XBUFS < NBLK:
                 load(b + XBUFS)
 
-        def quant(b, g):
+        def quant(n):
+            b, g = n // 2, n % 2
             if g == 0:
                 codes = cpool.tile([P, 2 * BLOCK], U32, align_bytes=64)
                 scales = cpool.tile([P, 2 * BLOCK], U8, align_bytes=64)
@@ -294,7 +267,8 @@ def tile_compositionalphoneticsmodel_t_kernel(tc, enc_output, feature2phone, map
             else:
                 nc.vector.scalar_tensor_tensor(out=accs[b][:], in0=pm[:], scalar=gain[:, d : d + 1], in1=accs[b][:], op0=ALU.mult, op1=ALU.max)
 
-        def f_bank(b, fb):
+        def f_bank(n):
+            b, fb = n // 2, n % 2
             pf = ps_f.tile([P, 2, 2, P], F32, tag="pf%d" % fb, name="pf%d" % fb)
             for s2 in range(2):
                 s = 2 * fb + s2
@@ -302,7 +276,8 @@ def tile_compositionalphoneticsmodel_t_kernel(tc, enc_output, feature2phone, map
                     nc.tensor.transpose(pf[:, s2, h, :], accs[b][:, s * P : (s + 1) * P], perm2[:, h * P : (h + 1) * P])
             pfs[(b, fb)] = pf
 
-        def join(b, fb, step):
+        def join(n, step):
+            b, fb = n // 2, n % 2
             pf = pfs[(b, fb)]
             if step == 0:
                 t3 = spool.tile([P, 2, PHONEMES], F32)
@@ -315,11 +290,13 @@ def tile_compositionalphoneticsmodel_t_kernel(tc, enc_output, feature2phone, map
                 vv = v_all[:, b * 256 + fb * 128 : b * 256 + (fb + 1) * 128].rearrange("p (s m) -> p s m", m=PHONEMES)
                 nc.vector.tensor_tensor(out=vv, in0=pf[:, :, 0, 0:64], in1=t3s[(b, fb)][:], op=ALU.max)
 
-        def row_max(b, fb):
+        def row_max(n):
+            b, fb = n // 2, n % 2
             vv = v_all[:, b * 256 + fb * 128 : b * 256 + (fb + 1) * 128].rearrange("p (s m) -> p s m", m=PHONEMES)
             nc.vector.tensor_reduce(out=neg_max[:, b * 4 + fb * 2 : b * 4 + fb * 2 + 2], in_=vv, axis=AX.X, op=ALU.max, negate=True)
 
-        def exps(b, fb):
+        def exps(n):
+            b, fb = n // 2, n % 2
             for i in range(b * 4 + fb * 2, b * 4 + fb * 2 + 2):
                 ex = spool.tile([P, PHONEMES], F32)
                 nc.scalar.activation(
@@ -346,85 +323,160 @@ def tile_compositionalphoneticsmodel_t_kernel(tc, enc_output, feature2phone, map
             queue.dma_start(out=out_v[:, b0:b1, :], in_=v_all[:, b0 * 256 : b1 * 256].rearrange("p (n f) -> p n f", f=256))
 
         wt_make(0)
+        lid_p = ps_m.tile([P, NV, 32], F32, tag="pm")
+        nc.tensor.matmul(out=lid_p[:, 0, :], lhsT=tri[:], rhs=act_b[:, 0, :], start=True, stop=True)
+        nc.tensor.matmul(out=lid_p[:, 1, :], lhsT=ones[:, 0:P], rhs=act_b[:, 0, :], start=True, stop=False)
+        nc.tensor.matmul(out=lid_p[:, 1, :], lhsT=tri[:], rhs=act_b[:, 1, :], start=False, stop=True)
+
+        compact = const.tile([P, NV, P], BF16)
+        for h in range(NV):
+            nc.vector.tensor_scalar(
+                out=compact[:, h, :], in0=iota_f[:], scalar1=lid_p[:, h, 0:1], scalar2=active[:, h : h + 1], op0=ALU.is_equal, op1=ALU.mult
+            )
+        lid = const.tile([P, NV], F32)
+        nc.vector.tensor_copy(out=lid[:], in_=lid_p[:, :, 0])
+
+        n_p = ps_m.tile([P, 32], F32, tag="pm")
+        rk_p = ps_m.tile([P, 2, PHONES], F32, tag="pm")
+        for h in range(NV):
+            nc.tensor.matmul(out=rk_p[:, 1, :], lhsT=compact[:, h, :], rhs=map2[:], start=(h == 0), stop=(h == NV - 1))
+        for h in range(NV):
+            nc.tensor.matmul(out=n_p[:], lhsT=compact[:, h, :], rhs=left_b[:, h, :], start=(h == 0), stop=(h == NV - 1))
+        for h in range(NV):
+            nc.tensor.matmul(out=rk_p[:, 0, :], lhsT=compact[:, h, :], rhs=rel[:, h, :], start=(h == 0), stop=(h == NV - 1))
+        gains = const.tile([P, PHONES], BF16)
+        nc.scalar.copy(out=gains[:], in_=rk_p[:, 1, :])
+        want = const.tile([P, DEPTH], F32)
+        nc.vector.scalar_tensor_tensor(out=want[:], in0=iota_f[:, 0:DEPTH], scalar=n_p[:, 0:1], in1=iota_f[:, 0:DEPTH], op0=ALU.is_lt, op1=ALU.mult)
+
+        takes = const.tile([P, DEPTH, PHONES], BF16)
+        gain_l = const.tile([P, DEPTH], F32)
+
+        def takes_make(d):
+            nc.vector.scalar_tensor_tensor(
+                out=takes[:, d, :], in0=rk_p[:, 0, :], scalar=want[:, d : d + 1], in1=gains[:], op0=ALU.is_equal, op1=ALU.mult,
+                accum_out=gain_l[:, d : d + 1],
+            )
+
         wt_make(1)
+        for d in range(DEPTH):
+            takes_make(d)
+        lid_t = const.tile([P, NV], F32)
+        nc.vector.scalar_tensor_tensor(out=lid_t[:], in0=lid[:], scalar=1.0, in1=active[:], op0=ALU.add, op1=ALU.mult)
+        lane_id = const.tile([P, NV], F32)
+        nc.vector.tensor_single_scalar(out=lane_id[:], in_=lid_t[:], scalar=-1.0, op=ALU.add)
+        tg1 = const.tile([P, 1], F32)
+        nc.vector.scalar_tensor_tensor(out=tg1[:], in0=lid[:, 1:2], scalar=lane_id[:, 0:1], in1=active[:, 1:2], op0=ALU.subtract, op1=ALU.mult)
+        tgt_b = const.tile([P, NV], BF16)
+        nc.vector.tensor_copy(out=tgt_b[:, 0:1], in_=lane_id[:, 0:1])
+        nc.vector.tensor_scalar(out=tgt_b[:, 1:2], in0=tg1[:], scalar1=lane_id[:, 0:1], scalar2=None, op0=ALU.add)
         sel_make(0)
-        sgw_make(1)
+        a_bank(0)
         sel_make(1)
-        sgw_make(2)
-        early = [(b, k) for b in range(STRIDED) for k in range(4)]
+        a_bank(1)
+        reorder(4, "v")
+        x_n = 2
+        r_n = 5
+        q_n = 0
         for d in range(DEPTH):
             wslot_make(d, W_ENG[d])
             if d + 2 < DEPTH:
                 sel_make(d + 2)
-            if d + 3 < DEPTH:
-                sgw_make(d + 3)
-            for b, k in early[sum(EARLY_N[:d]) : sum(EARLY_N[: d + 1])]:
-                a_bank(b, k)
+            for n in range(x_n, x_n + HEAD_X[d]):
+                a_bank(n)
+            x_n += HEAD_X[d]
+            for n in range(r_n, r_n + HEAD_R[d]):
+                reorder(n, "v")
+            r_n += HEAD_R[d]
             wslot_quant(d)
+            for n in range(q_n, q_n + HEAD_Q[d]):
+                quant(n)
+            q_n += HEAD_Q[d]
             if d == 3:
-                quant(0, 0)
-                quant(0, 1)
-            if d == 4:
-                gain_make()
                 perm_make()
-        quant(1, 0)
-        quant(1, 1)
+                gain_make()
         mx(0, 0)
         mx(1, 0)
-        reorder(3, 0)
-        reorder(3, 1)
-        quant(2, 0)
+        for n in range(r_n, x_n + R_LEAD):
+            reorder(n)
+        r_n = x_n + R_LEAD
 
+        nh = 2 * NBLK
+        f_n = 0
+        joins = []
+        exp_q = []
+        group = 0
         pending = []
         stores = []
-        NPH = 2 * NBLK
-        for i in range(NPH + 5):
-            p0 = i // 4 * 2
-            m_run = []
-            if i < NPH:
-                m_all = [(b, d) for d in range(1, DEPTH) for b in (p0, p0 + 1)]
-                if p0 + 2 < NBLK:
-                    m_all += [(p0 + 2, 0), (p0 + 3, 0)]
-                m_run = m_all[i % 4 * 3 : i % 4 * 3 + 3]
-            a = i + 6
-            q = i + 5
-            r = i + 8
-            f = i - 3
-            for n in range(3):
-                if n < len(m_run):
-                    mx(*m_run[n])
-                if n < 2 and 0 <= f - 1 < NPH:
-                    join((f - 1) // 2, (f - 1) % 2, n + 1)
-            if a < NPH:
-                a_bank(a // 2, a % 2 * 2)
-            if 0 <= f < NPH:
-                f_bank(f // 2, f % 2)
-            if a < NPH:
-                a_bank(a // 2, a % 2 * 2 + 1)
-            if 0 <= f - 1 < NPH:
-                row_max((f - 1) // 2, (f - 1) % 2)
-            if q < NPH:
-                quant(q // 2, q % 2)
-            if 0 <= f < NPH:
-                join(f // 2, f % 2, 0)
-            if r < NPH:
-                reorder(r // 2, r % 2)
-            if 0 <= f - 2 < NPH:
-                exps((f - 2) // 2, (f - 2) % 2)
-                for gi in range(len(GROUPS) - 1):
-                    if 2 * GROUPS[gi][1] == f - 1:
-                        group_ln(gi, nc.gpsimd)
-                        pending.extend(range(GROUPS[gi][0], GROUPS[gi][1], 2))
-            if i % 2 == 1 and stores:
-                s0 = stores.pop(0)
-                store(s0, s0 + 2, nc.sync)
-            if i % 2 == 1 and pending:
-                s0 = pending.pop(0)
-                finish(s0, s0 + 2, nc.gpsimd)
-                stores.append(s0)
+        for j in range(NBLK // 2):
+            m_list = [(b, d) for d in range(1, DEPTH) for b in (2 * j, 2 * j + 1)]
+            if j + 1 < NBLK // 2:
+                m_list += [(2 * j + 2, 0), (2 * j + 3, 0)]
+            for ph in range(3):
+                m_run = m_list[4 * ph : 4 * ph + 4]
+                for n, (b, d) in enumerate(m_run):
+                    mx(b, d)
+                    for i in range(-(-len(joins) // (len(m_run) - n))):
+                        joins.pop(0)()
+                x_run = range(x_n, min(2 * nh, x_n + X_RUN[ph]))
+                f_run = range(f_n, min(4 * j, f_n + (F_RUN[ph] if x_n < 2 * nh else 2)))
+                x_n, f_n = max(x_n, x_run.stop), max(f_n, f_run.stop)
+                t_run = [(a_bank, n) for n in x_run]
+                for i, n in enumerate(f_run):
+                    t_run[1 + 2 * i : 1 + 2 * i] = [(f_bank, n)]
+                for make, n in t_run:
+                    make(n)
+                for n in range(q_n, min(nh, q_n + Q_RUN[ph])):
+                    quant(n)
+                    q_n = n + 1
+                for n in f_run:
+                    join(n, 0)
+                joins += [lambda n=n, s=s: join(n, s) for s in (1, 2) for n in f_run]
+                joins += [lambda n=n: row_max(n) for n in f_run]
+                for n in range(r_n, min(2 * nh, r_n + X_RUN[ph])):
+                    reorder(n)
+                    r_n = n + 1
+                for n in exp_q:
+                    exps(n)
+                    if group < len(GROUPS) - 1 and n == 2 * GROUPS[group][1] - 1:
+                        group_ln(group, nc.gpsimd)
+                        pending.extend(range(GROUPS[group][0], GROUPS[group][1], 2))
+                        group += 1
+                exp_q = list(f_run)
+                if stores:
+                    s0 = stores.pop(0)
+                    store(s0, s0 + 2, nc.sync)
+                if pending:
+                    s0 = pending.pop(0)
+                    finish(s0, s0 + 2, nc.gpsimd)
+                    stores.append(s0)
+        for step in joins:
+            step()
+        for n in exp_q:
+            exps(n)
+        rest = range(f_n, nh)
+        for n in rest:
+            f_bank(n)
+        for n in rest[:2]:
+            join(n, 0)
+        for s in (1, 2):
+            for n in rest[:2]:
+                join(n, s)
+        for n in rest[2:]:
+            join(n, 0)
+        for n in rest[:2]:
+            row_max(n)
+            exps(n)
+        for s in (1, 2):
+            for n in rest[2:]:
+                join(n, s)
+        for n in rest[2:]:
+            row_max(n)
+            exps(n)
 
-        assert not pending
-        for s0 in stores:
+        for s0 in pending:
+            finish(s0, s0 + 2, nc.gpsimd)
+        for s0 in stores + pending:
             store(s0, s0 + 2, nc.sync)
         g0 = GROUPS[-1][0]
         group_ln(len(GROUPS) - 1, nc.vector)
@@ -432,5 +484,3 @@ def tile_compositionalphoneticsmodel_t_kernel(tc, enc_output, feature2phone, map
         store(g0, g0 + 2, nc.sync)
         finish_scalar(g0 + 2, g0 + 4)
         store(g0 + 2, g0 + 4, nc.scalar)
-        finish(g0 + 4, NBLK, nc.vector)
-        store(g0 + 4, NBLK, nc.sync)

@@ -32,9 +32,9 @@ HEAD_X = (2, 2, 2, 2, 1, 1)
 HEAD_R = (2, 2, 2, 2, 1, 0)
 HEAD_Q = (0, 1, 1, 1, 1, 1)
 R_LEAD = 4
-X_RUN = (3, 3, 2)
-F_RUN = (1, 1, 2)
-Q_RUN = (1, 2, 1)
+X_RUN = (2, 2, 2, 2)
+F_RUN = (1, 1, 1, 1)
+Q_RUN = (1, 1, 1, 1)
 WARM = 4
 NEG_BIG = -3.0e38
 W_ENG = ("sv", "sv", "sv", "sv", "sv", "sv")
@@ -208,6 +208,8 @@ def tile_compositionalphoneticsmodel_t_kernel(tc, enc_output, feature2phone, map
             src = xs[b][:].bitcast(F32).rearrange("p (s c) -> p s c", s=4)[:, 2 * sp : 2 * sp + 2, g * 256 : (g + 1) * 256].rearrange("p s (w u) -> p s u w", u=2)
             if eng == "v":
                 nc.vector.tensor_copy(out=xrs[b][:, k, :, :, :], in_=src)
+            elif eng == "p":
+                nc.gpsimd.tensor_copy(out=xrs[b][:, k, :, :, :].bitcast(I32), in_=src.bitcast(I32))
             else:
                 nc.scalar.copy(out=xrs[b][:, k, :, :, :], in_=src)
             if k == 3 and b + XBUFS < NBLK:
@@ -412,14 +414,14 @@ def tile_compositionalphoneticsmodel_t_kernel(tc, enc_output, feature2phone, map
             m_list = [(b, d) for d in range(1, DEPTH) for b in (2 * j, 2 * j + 1)]
             if j + 1 < NBLK // 2:
                 m_list += [(2 * j + 2, 0), (2 * j + 3, 0)]
-            for ph in range(3):
-                m_run = m_list[4 * ph : 4 * ph + 4]
+            for ph in range(4):
+                m_run = m_list[3 * ph : 3 * ph + 3]
                 for n, (b, d) in enumerate(m_run):
                     mx(b, d)
                     for i in range(-(-len(joins) // (len(m_run) - n))):
                         joins.pop(0)()
                 x_run = range(x_n, min(2 * nh, x_n + X_RUN[ph]))
-                f_run = range(f_n, min(4 * j, f_n + (F_RUN[ph] if x_n < 2 * nh else 2)))
+                f_run = range(f_n, min(4 * j + (1 if ph == 3 else 0), f_n + (F_RUN[ph] if x_n < 2 * nh else 2)))
                 x_n, f_n = max(x_n, x_run.stop), max(f_n, f_run.stop)
                 t_run = [(a_bank, n) for n in x_run]
                 for i, n in enumerate(f_run):

@@ -36,6 +36,7 @@ X_RUN = (2, 2, 2, 2)
 F_RUN = (1, 1, 1, 1)
 Q_RUN = (1, 1, 1, 1)
 WARM = 4
+R_ENG = ("s", "s", "s", "p")
 NEG_BIG = -3.0e38
 W_ENG = ("sv", "sv", "sv", "sv", "sv", "sv")
 
@@ -436,7 +437,7 @@ def tile_compositionalphoneticsmodel_t_kernel(tc, enc_output, feature2phone, map
                 joins += [lambda n=n, s=s: join(n, s) for s in (1, 2) for n in f_run]
                 joins += [lambda n=n: row_max(n) for n in f_run]
                 for n in range(r_n, min(2 * nh, r_n + X_RUN[ph])):
-                    reorder(n)
+                    reorder(n, R_ENG[ph])
                     r_n = n + 1
                 for n in exp_q:
                     exps(n)

@@ -24,21 +24,22 @@ BLOCK = 512
 NBLK = TOKENS // BLOCK
 DEPTH = 6
 NV = 2
-SLOTS = DEPTH * P
 STRIDED = 1
-GROUPS = ((0, 14), (14, 22), (22, 28), (28, 32))
-XBUFS = 6
-HEAD_X = (2, 2, 2, 2, 1, 1)
-HEAD_R = (2, 2, 2, 2, 1, 0)
-HEAD_Q = (0, 1, 1, 1, 1, 1)
-R_LEAD = 4
-X_RUN = (2, 2, 2, 2)
-F_RUN = (1, 1, 1, 1)
-Q_RUN = (1, 1, 1, 1)
-WARM = 4
-R_ENG = ("s", "s", "s", "p")
+GROUPS = ((0, 16), (16, 26), (26, 32))
+XBUFS = 5
+EXTRA = 96
+FAR = 1024.0
+WARM = 8
+HEAD_X = (3, 3, 3, 2, 2, 1)
+HEAD_R = (2, 3, 3, 2, 2, 0)
+HEAD_Q = (0, 1, 1, 1, 2, 2)
+R_LEAD = 6
+Q_RUN = (0, 1, 3)
+Q_LEAD = 7
+T_ORDER = "xxx0xx1xxx"
+R_ENG = "ppsppsps"
 NEG_BIG = -3.0e38
-W_ENG = ("sv", "sv", "sv", "sv", "sv", "sv")
+W_ENG = ("sv", "vv", "vv", "sv", "vv", "sv")
 
 
 def tile_compositionalphoneticsmodel_t_kernel(tc, enc_output, feature2phone, mapping, out):
@@ -55,18 +56,23 @@ def tile_compositionalphoneticsmodel_t_kernel(tc, enc_output, feature2phone, map
         cpool = ctx.enter_context(tc.tile_pool(name="cpool", bufs=6))
         apool = ctx.enter_context(tc.tile_pool(name="apool", bufs=6))
         spool = ctx.enter_context(tc.tile_pool(name="spool", bufs=4))
+        vpool = ctx.enter_context(tc.tile_pool(name="vpool", bufs=3))
         ps_t = ctx.enter_context(tc.psum_pool(name="ps_t", bufs=3))
         ps_m = ctx.enter_context(tc.psum_pool(name="ps_m", bufs=3))
-        ps_f = ctx.enter_context(tc.psum_pool(name="ps_f", bufs=1))
+        ps_f = ctx.enter_context(tc.psum_pool(name="ps_f", bufs=2))
         ctx.enter_context(tc.manual_schedule())
 
         xs = {}
         xrs = {}
+        pts = {}
+        pms = {}
+        a1s = {}
+        movs = {}
+        ends = {}
         grs = {}
         cds = {}
         accs = {}
         pfs = {}
-        t3s = {}
 
         map2 = const.tile([P, PHONES], BF16)
         nc.sync.dma_start(out=map2[0:64, :], in_=mapping)
@@ -94,19 +100,30 @@ def tile_compositionalphoneticsmodel_t_kernel(tc, enc_output, feature2phone, map
         ident_f = const.tile([P, P], F32)
         make_identity(nc, ident_f[:])
 
+        ones = const.tile([P, BLOCK], BF16)
+        nc.vector.memset(ones[:], 1.0)
+        warm_p = ps_m.tile([P, BLOCK], F32, tag="pm")
+        for i in range(WARM):
+            nc.tensor.matmul(out=warm_p[:], lhsT=ones[:, 0:P], rhs=ones[:], start=True, stop=True)
         part_f = const.tile([P, 1], F32)
         nc.vector.tensor_copy(out=part_f[:], in_=part_i[:])
         base = const.tile([P, 1], F32)
         nc.vector.tensor_scalar(out=base[:], in0=part_f[:], scalar1=64.0, scalar2=float(DEPTH), op0=ALU.is_ge, op1=ALU.mult)
         iota_f = const.tile([P, P], F32)
         nc.vector.tensor_copy(out=iota_f[:], in_=iota_i[:])
+        iota_n = const.tile([P, P], F32)
+        nc.vector.tensor_single_scalar(out=iota_n[:], in_=iota_f[:], scalar=-FAR, op=ALU.add)
+        iota_x = const.tile([P, P], F32)
+        nc.vector.tensor_single_scalar(out=iota_x[:], in_=iota_f[:], scalar=-float(EXTRA), op=ALU.add)
         tri = const.tile([P, P], BF16)
         nc.vector.tensor_scalar(out=tri[:], in0=iota_f[:], scalar1=part_f[:, 0:1], scalar2=None, op0=ALU.is_gt)
-        ones = const.tile([P, BLOCK], BF16)
-        nc.vector.memset(ones[:], 1.0)
-        warm_p = ps_m.tile([P, BLOCK], F32, tag="pm")
-        for i in range(WARM):
-            nc.tensor.matmul(out=warm_p[:], lhsT=ones[:, 0:P], rhs=ones[:], start=True, stop=True)
+        far = const.tile([P, P], BF16)
+        nc.vector.tensor_scalar(out=far[:], in0=iota_f[:], scalar1=part_f[:, 0:1], scalar2=FAR, op0=ALU.is_equal, op1=ALU.mult)
+        tri_a = const.tile([P, P], BF16)
+        nc.vector.tensor_tensor(out=tri_a[:], in0=tri[:], in1=far[:], op=ALU.subtract)
+        tri_b = const.tile([P, P], BF16)
+        nc.vector.tensor_scalar(out=tri_b[:], in0=iota_f[:], scalar1=part_f[:, 0:1], scalar2=None, op0=ALU.is_lt)
+        nc.vector.tensor_tensor(out=tri_b[:], in0=tri_b[:], in1=far[:], op=ALU.add)
 
         mask = const.tile([P, PHONES], F32)
         nc.vector.tensor_single_scalar(out=mask[:], in_=map2[:], scalar=0.0, op=ALU.is_gt)
@@ -148,7 +165,7 @@ def tile_compositionalphoneticsmodel_t_kernel(tc, enc_output, feature2phone, map
         sel = const.tile([P, DEPTH, 2, P], BF16)
 
         def sel_make(d):
-            sel_p = ps_f.tile([P, 2, P], BF16, tag="pf%d" % (d % 2), name="sel_p")
+            sel_p = ps_f.tile([P, 2, P], BF16, tag="pf")
             for c in range(2):
                 nc.tensor.transpose(sel_p[:, c, :], takes[:, d, c * P : (c + 1) * P], ident_b[:])
             nc.scalar.activation(out=sel[:, d, :, :], in_=sel_p[:], func=ACT.Sign)
@@ -181,24 +198,36 @@ def tile_compositionalphoneticsmodel_t_kernel(tc, enc_output, feature2phone, map
                 nc.vector.quantize_mx(out=w_codes[:, g, d, :].bitcast(FP8X4), scales=w_scales[:, g, d, :], in_=wg[:, g, d, :])
 
         gain = const.tile([P, DEPTH], F32)
-        perm2 = const.tile([P, NV * P], F32)
+        perm = const.tile([P, 2, P], F32)
         bias = const.tile([P, PHONEMES], F32)
+        bias_x = const.tile([P, 1], F32)
 
         def gain_make():
             nc.vector.tensor_single_scalar(out=gain[:], in_=gain_l[:], scalar=1.0 / 32.0, op=ALU.mult)
 
         def perm_make():
-            row_p = ps_f.tile([P, NV * P], F32, tag="pf1")
-            for h in range(NV):
-                nc.tensor.matmul(out=row_p[:, h * P : (h + 1) * P], lhsT=tgt_b[:, h : h + 1].to_broadcast([P, P]), rhs=ident_b[:], start=True, stop=True)
-            nc.vector.tensor_scalar(out=perm2[:], in0=row_p[:], scalar1=part_f[:, 0:1], scalar2=None, op0=ALU.is_equal)
-            nc.vector.tensor_scalar(out=bias[:], in0=row_p[:, 64:128], scalar1=0.0, scalar2=NEG_BIG, op0=ALU.is_lt, op1=ALU.mult)
+            shown = const.tile([P, P], BF16)
+            nc.vector.tensor_tensor(out=shown[:], in0=others[:], in1=place[:, 1, :], op=ALU.add)
+            perm_p = ps_f.tile([P, 2, P], BF16, tag="pf")
+            nc.tensor.transpose(perm_p[:, 0, :], place[:, 0, :], ident_b[:])
+            nc.tensor.transpose(perm_p[:, 1, :], shown[:], ident_b[:])
+            nc.scalar.copy(out=perm[:], in_=perm_p[:])
+            row_p = ps_f.tile([P, P], F32, tag="pf")
+            nc.tensor.matmul(out=row_p[:], lhsT=act_b[:, 0, 0:1].to_broadcast([P, P]), rhs=ident_b[:], start=True, stop=True)
+            nc.vector.tensor_scalar(out=bias[:], in0=row_p[:, 64:128], scalar1=0.5, scalar2=NEG_BIG, op0=ALU.is_lt, op1=ALU.mult)
+            nc.vector.tensor_scalar(out=bias_x[:], in0=part_f[:], scalar1=lid[:, 2:3], scalar2=NEG_BIG, op0=ALU.is_ge, op1=ALU.mult)
 
         v_all = const.tile([P, NBLK * 256], F32)
         neg_max = const.tile([P, NBLK * 4], F32)
         sums = const.tile([P, NBLK * 4], F32)
         logs = const.tile([P, NBLK * 4], F32)
         neg_l = const.tile([P, NBLK * 4], F32)
+
+        loads = []
+
+        def loads_flush(n):
+            for i in range(n):
+                load(loads.pop(0))
 
         def reorder(n, eng="s"):
             b, k = n // 4, n % 4
@@ -214,27 +243,33 @@ def tile_compositionalphoneticsmodel_t_kernel(tc, enc_output, feature2phone, map
             else:
                 nc.scalar.copy(out=xrs[b][:, k, :, :, :], in_=src)
             if k == 3 and b + XBUFS < NBLK:
-                load(b + XBUFS)
+                loads.append(b + XBUFS)
 
-        def a_bank(n):
+        def a_transpose(n, i):
             b, k = n // 4, n % 4
-            if k == 0:
+            g, sp = k // 2, k % 2
+            if k == 0 and i == 0:
                 gr = gpool.tile([P, 2 * BLOCK * 4], BF16, align_bytes=64)
                 grs[b] = gr
-            g, sp = k // 2, k % 2
-            grw = grs[b][:].bitcast(F32)
-            pt = ps_t.tile([P, 4 * P], F32, tag="pt")
-            for u in range(2):
-                for s2 in range(2):
-                    if b < STRIDED:
-                        lo = (2 * sp + s2) * 512 + 256 * g
-                        words = xs[b][:].bitcast(F32)[:, lo + u : lo + 256 : 2]
-                    else:
-                        words = xrs[b][:, k, s2, u, :]
-                    nc.tensor.transpose(pt[:, (u * 2 + s2) * P : (u * 2 + s2 + 1) * P], words, ident_f[:])
-            nc.scalar.copy(out=grw[:, k * 512 : (k + 1) * 512].rearrange("q (t u) -> q t u", u=2), in_=pt[:].rearrange("q (u t) -> q t u", u=2))
-            if b < STRIDED and k == 3 and b + XBUFS < NBLK:
-                load(b + XBUFS)
+            if i == 0:
+                pt = ps_t.tile([P, 4 * P], F32, tag="pt")
+                pts[n] = pt
+            u, s2 = i // 2, i % 2
+            if b < STRIDED:
+                lo = (2 * sp + s2) * 512 + 256 * g
+                words = xs[b][:].bitcast(F32)[:, lo + u : lo + 256 : 2]
+            else:
+                words = xrs[b][:, k, s2, u, :]
+            nc.tensor.transpose(pts[n][:, i * P : (i + 1) * P], words, ident_f[:])
+            if i == 3:
+                grw = grs[b][:].bitcast(F32)
+                nc.scalar.copy(out=grw[:, k * 512 : (k + 1) * 512].rearrange("q (t u) -> q t u", u=2), in_=pts[n][:].rearrange("q (u t) -> q t u", u=2))
+                if b < STRIDED and k == 3 and b + XBUFS < NBLK:
+                    loads.append(b + XBUFS)
+
+        def a_bank(n):
+            for i in range(4):
+                a_transpose(n, i)
 
         def quant(n):
             b, g = n // 2, n % 2
@@ -249,58 +284,88 @@ def tile_compositionalphoneticsmodel_t_kernel(tc, enc_output, feature2phone, map
                 in_=grs[b][:, g * BLOCK * 4 : (g + 1) * BLOCK * 4],
             )
 
-        def mx(b, d):
-            if d == 0:
-                acc = apool.tile([P, BLOCK], F32)
-                accs[b] = acc
+        def mx_pass(b, d, g):
+            if g == 0:
+                if d == 0:
+                    acc = apool.tile([P, BLOCK], F32)
+                    accs[b] = acc
+                pm = ps_m.tile([P, BLOCK], F32, tag="pm")
+                pms[(b, d)] = pm
+            pm = pms[(b, d)]
             codes, scales = cds[b]
-            pm = ps_m.tile([P, BLOCK], F32, tag="pm")
-            for g in range(2):
-                nc.tensor.matmul_mx(
-                    out=pm[:],
-                    lhsT=w_codes[:, g, d, :].bitcast(FP8X4),
-                    lhsT_scale=w_scales[:, g, d, :],
-                    rhs=codes[:, g * BLOCK : (g + 1) * BLOCK].bitcast(FP8X4),
-                    rhs_scale=scales[:, g * BLOCK : (g + 1) * BLOCK],
-                    start=(g == 0),
-                    stop=(g == 1),
-                )
-            if d == 0:
+            nc.tensor.matmul_mx(
+                out=pm[:],
+                lhsT=w_codes[:, g, d, :].bitcast(FP8X4),
+                lhsT_scale=w_scales[:, g, d, :],
+                rhs=codes[:, g * BLOCK : (g + 1) * BLOCK].bitcast(FP8X4),
+                rhs_scale=scales[:, g * BLOCK : (g + 1) * BLOCK],
+                start=(g == 0),
+                stop=(g == 1),
+            )
+            if g == 1 and d == 0:
                 nc.scalar.activation(out=accs[b][:], in_=pm[:], func=ACT.Copy, scale=gain[:, 0:1])
-            else:
+            elif g == 1:
                 nc.vector.scalar_tensor_tensor(out=accs[b][:], in0=pm[:], scalar=gain[:, d : d + 1], in1=accs[b][:], op0=ALU.mult, op1=ALU.max)
 
-        def f_bank(n):
-            b, fb = n // 2, n % 2
-            pf = ps_f.tile([P, 2, 2, P], F32, tag="pf%d" % fb, name="pf%d" % fb)
-            for s2 in range(2):
-                s = 2 * fb + s2
+        def mx(b, d):
+            mx_pass(b, d, 0)
+            mx_pass(b, d, 1)
+
+        def extra_move(b):
+            mov = vpool.tile([P, BLOCK], F32)
+            nc.sync.dma_start(out=mov[0 : P - EXTRA, :], in_=accs[b][EXTRA:P, :])
+            movs[b] = mov
+
+        def extra_join(b):
+            n = P - EXTRA
+            nc.vector.scalar_tensor_tensor(
+                out=accs[b][0:n, :], in0=movs[b][0:n, :], scalar=bias_x[0:n, 0:1], in1=accs[b][0:n, :], op0=ALU.add, op1=ALU.max
+            )
+
+        def f_transpose(b, s):
+            if s == 0:
+                pf = ps_f.tile([P, 4, P], F32, tag="pf")
+                pfs[b] = pf
+            nc.tensor.transpose(pfs[b][:, s, :], accs[b][:, s * P : (s + 1) * P], perm[:, 0, :])
+            if s == 3:
+                a1 = spool.tile([P, 4, PHONEMES], F32)
+                a1s[b] = a1
+                nc.scalar.copy(out=a1[:], in_=pfs[b][:, :, 64:128])
+                nc.gpsimd.tensor_tensor(out=a1[:], in0=a1[:], in1=bias[:].unsqueeze(1).to_broadcast([P, 4, PHONEMES]), op=ALU.add)
+
+        def end_bank(b, fb, pool, tag):
+            pf = pool.tile([P, 2, 2, P], F32, tag=tag)
+            for i in range(2):
                 for h in range(2):
-                    nc.tensor.transpose(pf[:, s2, h, :], accs[b][:, s * P : (s + 1) * P], perm2[:, h * P : (h + 1) * P])
-            pfs[(b, fb)] = pf
+                    s = 2 * fb + i
+                    nc.tensor.transpose(pf[:, h, i, :], accs[b][:, s * P : (s + 1) * P], perm[:, h, :])
+            u = spool.tile([P, 2, P], F32)
+            nc.scalar.copy(out=u[:], in_=pf[:, 1, :, :])
+            ends[(b, fb)] = (pf, u)
 
-        def join(n, step):
-            b, fb = n // 2, n % 2
-            pf = pfs[(b, fb)]
+        def end_join(b, fb, step):
+            pf, u = ends[(b, fb)]
             if step == 0:
-                t3 = spool.tile([P, 2, PHONEMES], F32)
-                t3s[(b, fb)] = t3
-                nc.vector.tensor_tensor(out=t3[:], in0=pf[:, :, 0, 64:128], in1=bias[:].unsqueeze(1).to_broadcast([P, 2, PHONEMES]), op=ALU.add)
+                nc.vector.tensor_tensor(out=u[:], in0=pf[:, 0, :, :], in1=u[:], op=ALU.max)
             elif step == 1:
-                t3 = t3s[(b, fb)]
-                nc.vector.tensor_tensor(out=t3[:], in0=pf[:, :, 1, 0:64], in1=t3[:], op=ALU.max)
+                t = spool.tile([P, 2, PHONEMES], F32)
+                nc.vector.tensor_tensor(out=t[:], in0=u[:, :, 64:128], in1=bias[:].unsqueeze(1).to_broadcast([P, 2, PHONEMES]), op=ALU.add)
+                ends[(b, fb)] = (t, u)
             else:
+                t, u = ends[(b, fb)]
                 vv = v_all[:, b * 256 + fb * 128 : b * 256 + (fb + 1) * 128].rearrange("p (s m) -> p s m", m=PHONEMES)
-                nc.vector.tensor_tensor(out=vv, in0=pf[:, :, 0, 0:64], in1=t3s[(b, fb)][:], op=ALU.max)
+                nc.vector.tensor_tensor(out=vv, in0=u[:, :, 0:64], in1=t[:], op=ALU.max)
 
-        def row_max(n):
-            b, fb = n // 2, n % 2
-            vv = v_all[:, b * 256 + fb * 128 : b * 256 + (fb + 1) * 128].rearrange("p (s m) -> p s m", m=PHONEMES)
-            nc.vector.tensor_reduce(out=neg_max[:, b * 4 + fb * 2 : b * 4 + fb * 2 + 2], in_=vv, axis=AX.X, op=ALU.max, negate=True)
+        def lane_join(b):
+            vv = v_all[:, b * 256 : (b + 1) * 256].rearrange("p (s m) -> p s m", m=PHONEMES)
+            nc.vector.tensor_tensor(out=vv, in0=pfs[b][:, :, 0:64], in1=a1s[b][:], op=ALU.max)
 
-        def exps(n):
-            b, fb = n // 2, n % 2
-            for i in range(b * 4 + fb * 2, b * 4 + fb * 2 + 2):
+        def row_max(b):
+            vv = v_all[:, b * 256 : (b + 1) * 256].rearrange("p (s m) -> p s m", m=PHONEMES)
+            nc.vector.tensor_reduce(out=neg_max[:, b * 4 : (b + 1) * 4], in_=vv, axis=AX.X, op=ALU.max, negate=True)
+
+        def exps(b):
+            for i in range(b * 4, b * 4 + 4):
                 ex = spool.tile([P, PHONEMES], F32)
                 nc.scalar.activation(
                     out=ex[:], in_=v_all[:, i * 64 : (i + 1) * 64], func=ACT.Exp,
@@ -326,27 +391,35 @@ def tile_compositionalphoneticsmodel_t_kernel(tc, enc_output, feature2phone, map
             queue.dma_start(out=out_v[:, b0:b1, :], in_=v_all[:, b0 * 256 : b1 * 256].rearrange("p (n f) -> p n f", f=256))
 
         wt_make(0)
-        lid_p = ps_m.tile([P, NV, 32], F32, tag="pm")
-        nc.tensor.matmul(out=lid_p[:, 0, :], lhsT=tri[:], rhs=act_b[:, 0, :], start=True, stop=True)
-        nc.tensor.matmul(out=lid_p[:, 1, :], lhsT=ones[:, 0:P], rhs=act_b[:, 0, :], start=True, stop=False)
-        nc.tensor.matmul(out=lid_p[:, 1, :], lhsT=tri[:], rhs=act_b[:, 1, :], start=False, stop=True)
-
-        compact = const.tile([P, NV, P], BF16)
-        for h in range(NV):
-            nc.vector.tensor_scalar(
-                out=compact[:, h, :], in0=iota_f[:], scalar1=lid_p[:, h, 0:1], scalar2=active[:, h : h + 1], op0=ALU.is_equal, op1=ALU.mult
-            )
-        lid = const.tile([P, NV], F32)
+        lid_p = ps_m.tile([P, 3, 32], F32, tag="pm")
+        nc.tensor.matmul(out=lid_p[:, 1, :], lhsT=tri[:], rhs=act_b[:, 1, :], start=True, stop=True)
+        nc.tensor.matmul(out=lid_p[:, 2, :], lhsT=ones[:, 0:P], rhs=act_b[:, 1, :], start=True, stop=True)
+        nc.tensor.matmul(out=lid_p[:, 0, :], lhsT=tri_a[:], rhs=act_b[:, 0, :], start=True, stop=False)
+        nc.tensor.matmul(out=lid_p[:, 0, :], lhsT=tri_b[:], rhs=act_b[:, 1, :], start=False, stop=True)
+        lid = const.tile([P, 3], F32)
         nc.vector.tensor_copy(out=lid[:], in_=lid_p[:, :, 0])
+        place = const.tile([P, NV, P], BF16)
+        partner = const.tile([P, P], BF16)
+        nc.vector.tensor_scalar(
+            out=partner[:], in0=iota_f[:], scalar1=lid[:, 1:2], scalar2=active[:, 1:2], op0=ALU.is_equal, op1=ALU.mult
+        )
+        skip = const.tile([P, 1], F32)
+        nc.vector.tensor_scalar(out=skip[:], in0=lid[:, 0:1], scalar1=float(EXTRA) - FAR, scalar2=lid[:, 2:3], op0=ALU.is_ge, op1=ALU.mult)
+        nc.vector.tensor_scalar(
+            out=place[:, 1, :], in0=iota_x[:], scalar1=lid[:, 1:2], scalar2=active[:, 1:2], op0=ALU.is_equal, op1=ALU.mult
+        )
+        others = const.tile([P, P], BF16)
+        nc.vector.tensor_scalar(out=others[:], in0=iota_n[:], scalar1=skip[:, 0:1], scalar2=lid[:, 0:1], op0=ALU.subtract, op1=ALU.is_equal)
+        nc.vector.tensor_tensor(out=place[:, 0, :], in0=others[:], in1=partner[:], op=ALU.add)
 
         n_p = ps_m.tile([P, 32], F32, tag="pm")
         rk_p = ps_m.tile([P, 2, PHONES], F32, tag="pm")
         for h in range(NV):
-            nc.tensor.matmul(out=rk_p[:, 1, :], lhsT=compact[:, h, :], rhs=map2[:], start=(h == 0), stop=(h == NV - 1))
+            nc.tensor.matmul(out=rk_p[:, 1, :], lhsT=place[:, h, :], rhs=map2[:], start=(h == 0), stop=(h == NV - 1))
         for h in range(NV):
-            nc.tensor.matmul(out=n_p[:], lhsT=compact[:, h, :], rhs=left_b[:, h, :], start=(h == 0), stop=(h == NV - 1))
+            nc.tensor.matmul(out=n_p[:], lhsT=place[:, h, :], rhs=left_b[:, h, :], start=(h == 0), stop=(h == NV - 1))
         for h in range(NV):
-            nc.tensor.matmul(out=rk_p[:, 0, :], lhsT=compact[:, h, :], rhs=rel[:, h, :], start=(h == 0), stop=(h == NV - 1))
+            nc.tensor.matmul(out=rk_p[:, 0, :], lhsT=place[:, h, :], rhs=rel[:, h, :], start=(h == 0), stop=(h == NV - 1))
         gains = const.tile([P, PHONES], BF16)
         nc.scalar.copy(out=gains[:], in_=rk_p[:, 1, :])
         want = const.tile([P, DEPTH], F32)
@@ -364,118 +437,132 @@ def tile_compositionalphoneticsmodel_t_kernel(tc, enc_output, feature2phone, map
         wt_make(1)
         for d in range(DEPTH):
             takes_make(d)
-        lid_t = const.tile([P, NV], F32)
-        nc.vector.scalar_tensor_tensor(out=lid_t[:], in0=lid[:], scalar=1.0, in1=active[:], op0=ALU.add, op1=ALU.mult)
-        lane_id = const.tile([P, NV], F32)
-        nc.vector.tensor_single_scalar(out=lane_id[:], in_=lid_t[:], scalar=-1.0, op=ALU.add)
-        tg1 = const.tile([P, 1], F32)
-        nc.vector.scalar_tensor_tensor(out=tg1[:], in0=lid[:, 1:2], scalar=lane_id[:, 0:1], in1=active[:, 1:2], op0=ALU.subtract, op1=ALU.mult)
-        tgt_b = const.tile([P, NV], BF16)
-        nc.vector.tensor_copy(out=tgt_b[:, 0:1], in_=lane_id[:, 0:1])
-        nc.vector.tensor_scalar(out=tgt_b[:, 1:2], in0=tg1[:], scalar1=lane_id[:, 0:1], scalar2=None, op0=ALU.add)
         sel_make(0)
         a_bank(0)
         sel_make(1)
         a_bank(1)
-        reorder(4, "v")
         x_n = 2
-        r_n = 5
+        r_n = 4
         q_n = 0
         for d in range(DEPTH):
             wslot_make(d, W_ENG[d])
             if d + 2 < DEPTH:
                 sel_make(d + 2)
+            for n in range(r_n, r_n + HEAD_R[d]):
+                reorder(n, "p")
+            r_n += HEAD_R[d]
             for n in range(x_n, x_n + HEAD_X[d]):
                 a_bank(n)
             x_n += HEAD_X[d]
-            for n in range(r_n, r_n + HEAD_R[d]):
-                reorder(n, "v")
-            r_n += HEAD_R[d]
             wslot_quant(d)
+            loads_flush(len(loads))
             for n in range(q_n, q_n + HEAD_Q[d]):
                 quant(n)
             q_n += HEAD_Q[d]
             if d == 3:
-                perm_make()
                 gain_make()
         mx(0, 0)
         mx(1, 0)
+        perm_make()
         for n in range(r_n, x_n + R_LEAD):
-            reorder(n)
+            reorder(n, R_ENG[n % 8])
         r_n = x_n + R_LEAD
 
         nh = 2 * NBLK
-        f_n = 0
-        joins = []
-        exp_q = []
+        npair = NBLK // 2
+        x_done = x_n
+        q_n = Q_LEAD
         group = 0
         pending = []
         stores = []
-        for j in range(NBLK // 2):
-            m_list = [(b, d) for d in range(1, DEPTH) for b in (2 * j, 2 * j + 1)]
-            if j + 1 < NBLK // 2:
-                m_list += [(2 * j + 2, 0), (2 * j + 3, 0)]
-            for ph in range(4):
-                m_run = m_list[3 * ph : 3 * ph + 3]
+        tasks = []
+
+        def finish_some():
+            if stores:
+                s0 = stores.pop(0)
+                store(s0, s0 + 2, nc.sync)
+            if pending:
+                s0 = pending.pop(0)
+                finish(s0, s0 + 2, nc.gpsimd)
+                stores.append(s0)
+
+        for j in range(npair):
+            banks = [(b, d) for d in range(1, DEPTH) for b in (2 * j, 2 * j + 1)]
+            if j + 1 < npair:
+                banks += [(2 * j + 2, 0), (2 * j + 3, 0)]
+            t_list = []
+            for c in T_ORDER:
+                if c == "x":
+                    t_list += [("x", x_n, s) if x_n < 2 * nh else None for s in range(4)]
+                    x_n += 1
+                elif j >= 1:
+                    t_list += [("f", 2 * j - 2 + int(c), s) for s in range(4)]
+                else:
+                    t_list += [None] * 4
+            for ph in range(3):
+                due = len(loads)
+                m_run = banks[4 * ph : 4 * ph + 4]
+                if j >= 1:
+                    if ph < 2:
+                        tasks.append((extra_join, 2 * j - 2 + ph))
+                    if ph == 0 and j >= 2:
+                        tasks += [(lane_join, 2 * j - 3), (row_max, 2 * j - 3)]
                 for n, (b, d) in enumerate(m_run):
                     mx(b, d)
-                    for i in range(-(-len(joins) // (len(m_run) - n))):
-                        joins.pop(0)()
-                x_run = range(x_n, min(2 * nh, x_n + X_RUN[ph]))
-                f_run = range(f_n, min(4 * j + (1 if ph == 3 else 0), f_n + (F_RUN[ph] if x_n < 2 * nh else 2)))
-                x_n, f_n = max(x_n, x_run.stop), max(f_n, f_run.stop)
-                t_run = [(a_bank, n) for n in x_run]
-                for i, n in enumerate(f_run):
-                    t_run[1 + 2 * i : 1 + 2 * i] = [(f_bank, n)]
-                for make, n in t_run:
-                    make(n)
-                for n in range(q_n, min(nh, q_n + Q_RUN[ph])):
-                    quant(n)
-                    q_n = n + 1
-                for n in f_run:
-                    join(n, 0)
-                joins += [lambda n=n, s=s: join(n, s) for s in (1, 2) for n in f_run]
-                joins += [lambda n=n: row_max(n) for n in f_run]
-                for n in range(r_n, min(2 * nh, r_n + X_RUN[ph])):
-                    reorder(n, R_ENG[ph])
-                    r_n = n + 1
-                for n in exp_q:
-                    exps(n)
-                    if group < len(GROUPS) - 1 and n == 2 * GROUPS[group][1] - 1:
+                    if d == DEPTH - 1 and j + 1 < npair:
+                        extra_move(b)
+                    if tasks:
+                        fn, arg = tasks.pop(0)
+                        fn(arg)
+                for fn, arg in tasks:
+                    fn(arg)
+                tasks = []
+                x_ready = x_done
+                for item in t_list[len(t_list) * ph // 3 : len(t_list) * (ph + 1) // 3]:
+                    if item:
+                        kind, n, s = item
+                        if kind == "x":
+                            a_transpose(n, s)
+                            if s == 3:
+                                x_done = n + 1
+                        else:
+                            f_transpose(n, s)
+                for i in range(Q_RUN[ph]):
+                    if q_n < nh:
+                        quant(q_n)
+                        q_n += 1
+                    if ph == 2 and i == 1 and j >= 1:
+                        lane_join(2 * j - 2)
+                        row_max(2 * j - 2)
+                while r_n < min(2 * nh, x_n + R_LEAD - 10 + (10 * (ph + 1)) // 3):
+                    reorder(r_n, R_ENG[r_n % 8])
+                    r_n += 1
+                e = 2 * j - 2 if ph == 2 and j >= 1 else 2 * j - 3 if ph == 0 and j >= 2 else -1
+                if e >= 0:
+                    exps(e)
+                    if group < len(GROUPS) - 1 and e == GROUPS[group][1] - 1:
                         group_ln(group, nc.gpsimd)
                         pending.extend(range(GROUPS[group][0], GROUPS[group][1], 2))
                         group += 1
-                exp_q = list(f_run)
-                if stores:
-                    s0 = stores.pop(0)
-                    store(s0, s0 + 2, nc.sync)
-                if pending:
-                    s0 = pending.pop(0)
-                    finish(s0, s0 + 2, nc.gpsimd)
-                    stores.append(s0)
-        for step in joins:
-            step()
-        for n in exp_q:
-            exps(n)
-        rest = range(f_n, nh)
-        for n in rest:
-            f_bank(n)
-        for n in rest[:2]:
-            join(n, 0)
-        for s in (1, 2):
-            for n in rest[:2]:
-                join(n, s)
-        for n in rest[2:]:
-            join(n, 0)
-        for n in rest[:2]:
-            row_max(n)
-            exps(n)
-        for s in (1, 2):
-            for n in rest[2:]:
-                join(n, s)
-        for n in rest[2:]:
-            row_max(n)
-            exps(n)
+                if j + 1 < npair:
+                    finish_some()
+                loads_flush(due)
+        z = NBLK - 1
+        last = [(b, fb) for b in (z - 1, z) for fb in range(2)]
+        end_bank(z - 1, 0, ps_m, "pm")
+        end_bank(z - 1, 1, ps_m, "pm")
+        end_bank(z, 0, ps_m, "pm")
+        lane_join(z - 2)
+        row_max(z - 2)
+        end_bank(z, 1, ps_f, "pf")
+        exps(z - 2)
+        for half in (last[:2], last[2:]):
+            for step in range(3):
+                for b, fb in half:
+                    end_join(b, fb, step)
+        for b in (z - 1, z):
+            row_max(b)
+            exps(b)
 
         for s0 in pending:
             finish(s0, s0 + 2, nc.gpsimd)
@@ -483,7 +570,7 @@ def tile_compositionalphoneticsmodel_t_kernel(tc, enc_output, feature2phone, map
             store(s0, s0 + 2, nc.sync)
         g0 = GROUPS[-1][0]
         group_ln(len(GROUPS) - 1, nc.vector)
-        finish(g0, g0 + 2, nc.vector)
-        store(g0, g0 + 2, nc.sync)
-        finish_scalar(g0 + 2, g0 + 4)
-        store(g0 + 2, g0 + 4, nc.scalar)
+        finish(g0, g0 + 3, nc.vector)
+        store(g0, g0 + 3, nc.sync)
+        finish_scalar(g0 + 3, g0 + 6)
+        store(g0 + 3, g0 + 6, nc.scalar)

@@ -22,25 +22,30 @@ FLOPS = 2 * TOKENS * H * PHONES
 P = 128
 BLOCK = 512
 NBLK = TOKENS // BLOCK
-DEPTH = 6
-NV = 2
+DEPTH = 5
+FIRST = 3
+PARTNERS = 16
+SECOND = 3
+HELP = 96
+HELPERS = SECOND + PARTNERS
 STRIDED = 1
-GROUPS = ((0, 16), (16, 26), (26, 32))
+GROUPS = ((0, 22), (22, 32))
 XBUFS = 5
-EXTRA = 96
 FAR = 1024.0
-WARM = 8
-HEAD_X = (3, 3, 3, 2, 2, 1)
-HEAD_R = (2, 3, 3, 2, 2, 0)
-HEAD_Q = (0, 1, 1, 1, 2, 2)
+WARM = (7, 2, 2, 3)
+HEAD_ORDER = (0, 2, 1, 3)
+HEAD_X = (2, 3, 3, 2, 2)
+HEAD_ENG = "pp"
+HEAD_R = (2, 3, 3, 2, 2)
+HEAD_Q = (0, 1, 1, 2, 2)
 R_LEAD = 6
-Q_RUN = (0, 1, 3)
-Q_LEAD = 7
-T_ORDER = "xxx0xx1xxx"
-R_ENG = "ppsppsps"
+Q_RUN = (1, 1, 2)
+Q_LEAD = 6
+X_CUTS = (0, 10, 20, 32)
+F_AT = 8
+R_ENG = "vsvvsvsv"
 NEG_BIG = -3.0e38
-W_ENG = ("sv", "vv", "vv", "sv", "vv", "sv")
-
+W_ENG = ("sv", "vv", "sv", "vv", "sv")
 
 def tile_compositionalphoneticsmodel_t_kernel(tc, enc_output, feature2phone, mapping, out):
     nc = tc.nc
@@ -51,15 +56,16 @@ def tile_compositionalphoneticsmodel_t_kernel(tc, enc_output, feature2phone, map
     with ExitStack() as ctx:
         const = ctx.enter_context(tc.tile_pool(name="const", bufs=1))
         xpool = ctx.enter_context(tc.tile_pool(name="xpool", bufs=XBUFS))
-        rpool = ctx.enter_context(tc.tile_pool(name="rpool", bufs=3))
-        gpool = ctx.enter_context(tc.tile_pool(name="gpool", bufs=3))
-        cpool = ctx.enter_context(tc.tile_pool(name="cpool", bufs=6))
-        apool = ctx.enter_context(tc.tile_pool(name="apool", bufs=6))
+        rpool = ctx.enter_context(tc.tile_pool(name="rpool", bufs=10))
+        gpool = ctx.enter_context(tc.tile_pool(name="gpool", bufs=5))
+        cpool = ctx.enter_context(tc.tile_pool(name="cpool", bufs=8))
+        apool = ctx.enter_context(tc.tile_pool(name="apool", bufs=10))
+        bpool = ctx.enter_context(tc.tile_pool(name="bpool", bufs=8))
         spool = ctx.enter_context(tc.tile_pool(name="spool", bufs=4))
-        vpool = ctx.enter_context(tc.tile_pool(name="vpool", bufs=3))
-        ps_t = ctx.enter_context(tc.psum_pool(name="ps_t", bufs=3))
+        qpool = ctx.enter_context(tc.tile_pool(name="qpool", bufs=2))
+        ps_t = ctx.enter_context(tc.psum_pool(name="ps_t", bufs=4))
         ps_m = ctx.enter_context(tc.psum_pool(name="ps_m", bufs=3))
-        ps_f = ctx.enter_context(tc.psum_pool(name="ps_f", bufs=2))
+        ps_f = ctx.enter_context(tc.psum_pool(name="ps_f", bufs=1))
         ctx.enter_context(tc.manual_schedule())
 
         xs = {}
@@ -67,16 +73,16 @@ def tile_compositionalphoneticsmodel_t_kernel(tc, enc_output, feature2phone, map
         pts = {}
         pms = {}
         a1s = {}
-        movs = {}
-        ends = {}
         grs = {}
         cds = {}
         accs = {}
+        tops = {}
+        quads = {}
         pfs = {}
 
-        map2 = const.tile([P, PHONES], BF16)
-        nc.sync.dma_start(out=map2[0:64, :], in_=mapping)
-        nc.sync.dma_start(out=map2[64:128, :], in_=mapping)
+        map2 = const.tile([P, 2, PHONES], BF16)
+        nc.sync.dma_start(out=map2[0:64, 1, :], in_=mapping)
+        nc.sync.dma_start(out=map2[64:128, 1, :], in_=mapping)
         wl = const.tile([P, 4, 2, PHONES], BF16)
 
         def load(b, parts=1):
@@ -99,57 +105,62 @@ def tile_compositionalphoneticsmodel_t_kernel(tc, enc_output, feature2phone, map
         make_identity(nc, ident_b[:])
         ident_f = const.tile([P, P], F32)
         make_identity(nc, ident_f[:])
-
         ones = const.tile([P, BLOCK], BF16)
         nc.vector.memset(ones[:], 1.0)
-        warm_p = ps_m.tile([P, BLOCK], F32, tag="pm")
-        for i in range(WARM):
-            nc.tensor.matmul(out=warm_p[:], lhsT=ones[:, 0:P], rhs=ones[:], start=True, stop=True)
+
+        def warm(n):
+            warm_p = ps_f.tile([P, BLOCK], F32, tag="pf")
+            for i in range(n):
+                nc.tensor.matmul(out=warm_p[:], lhsT=ones[:, 0:P], rhs=ones[:], start=True, stop=True)
+
+        warm(WARM[0])
         part_f = const.tile([P, 1], F32)
         nc.vector.tensor_copy(out=part_f[:], in_=part_i[:])
-        base = const.tile([P, 1], F32)
-        nc.vector.tensor_scalar(out=base[:], in0=part_f[:], scalar1=64.0, scalar2=float(DEPTH), op0=ALU.is_ge, op1=ALU.mult)
         iota_f = const.tile([P, P], F32)
         nc.vector.tensor_copy(out=iota_f[:], in_=iota_i[:])
-        iota_n = const.tile([P, P], F32)
-        nc.vector.tensor_single_scalar(out=iota_n[:], in_=iota_f[:], scalar=-FAR, op=ALU.add)
-        iota_x = const.tile([P, P], F32)
-        nc.vector.tensor_single_scalar(out=iota_x[:], in_=iota_f[:], scalar=-float(EXTRA), op=ALU.add)
+        upper = const.tile([P, 1], F32)
+        nc.vector.tensor_single_scalar(out=upper[:], in_=part_f[:], scalar=64.0, op=ALU.is_ge)
+        lims = const.tile([P, 6], F32)
+        for i, (lo, hi) in enumerate(((10, 12), (17, 14), (-1, 7), (FAR, 5), (FAR, 10), (FAR, 17))):
+            nc.vector.tensor_scalar(out=lims[:, i : i + 1], in0=upper[:], scalar1=float(hi - lo), scalar2=float(lo), op0=ALU.mult, op1=ALU.add)
         tri = const.tile([P, P], BF16)
         nc.vector.tensor_scalar(out=tri[:], in0=iota_f[:], scalar1=part_f[:, 0:1], scalar2=None, op0=ALU.is_gt)
-        far = const.tile([P, P], BF16)
-        nc.vector.tensor_scalar(out=far[:], in0=iota_f[:], scalar1=part_f[:, 0:1], scalar2=FAR, op0=ALU.is_equal, op1=ALU.mult)
-        tri_a = const.tile([P, P], BF16)
-        nc.vector.tensor_tensor(out=tri_a[:], in0=tri[:], in1=far[:], op=ALU.subtract)
-        tri_b = const.tile([P, P], BF16)
-        nc.vector.tensor_scalar(out=tri_b[:], in0=iota_f[:], scalar1=part_f[:, 0:1], scalar2=None, op0=ALU.is_lt)
-        nc.vector.tensor_tensor(out=tri_b[:], in0=tri_b[:], in1=far[:], op=ALU.add)
+        rank_n = const.tile([P, P], F32)
+        nc.vector.tensor_single_scalar(out=rank_n[:, 0:HELP], in_=iota_f[:, 0:HELP], scalar=-1.0, op=ALU.mult)
+        nc.vector.tensor_scalar(
+            out=rank_n[:, HELP + HELPERS : P], in0=iota_f[:, HELP + HELPERS : P], scalar1=-1.0, scalar2=float(HELPERS), op0=ALU.mult, op1=ALU.add
+        )
+
+        strides = const.tile([P, 3], F32)
+        for i, w in enumerate((5.0, 2.0, 3.0)):
+            nc.vector.memset(strides[:, i : i + 1], w)
+        own = const.tile([P, 1], F32)
+        nc.vector.tensor_scalar(out=own[:], in0=part_f[:], scalar1=float(PARTNERS), scalar2=-1.0, op0=ALU.is_lt, op1=ALU.mult)
+        ge_h = const.tile([P, 1], F32)
+        nc.vector.tensor_scalar(out=ge_h[:], in0=part_f[:], scalar1=float(HELP), scalar2=None, op0=ALU.is_ge)
+        ge_e = const.tile([P, 1], F32)
+        nc.vector.tensor_scalar(out=ge_e[:], in0=part_f[:], scalar1=float(HELP + HELPERS), scalar2=None, op0=ALU.is_ge)
+        ge_f = const.tile([P, 1], F32)
+        nc.vector.tensor_scalar(out=ge_f[:], in0=part_f[:], scalar1=float(HELP + SECOND), scalar2=-3.0, op0=ALU.is_ge, op1=ALU.mult)
+        helper = const.tile([P, 1], F32)
+        nc.vector.tensor_tensor(out=helper[:], in0=ge_h[:], in1=ge_e[:], op=ALU.subtract)
+        aid = const.tile([P, 1], F32)
+        nc.vector.scalar_tensor_tensor(out=aid[:], in0=ge_e[:], scalar=-4.0, in1=ge_f[:], op0=ALU.mult, op1=ALU.add)
+        less = const.tile([P, 1], F32)
+        nc.vector.scalar_tensor_tensor(out=less[:], in0=helper[:], scalar=-3.0, in1=own[:], op0=ALU.mult, op1=ALU.add)
+        nc.vector.scalar_tensor_tensor(out=aid[:], in0=ge_h[:], scalar=7.0, in1=aid[:], op0=ALU.mult, op1=ALU.add)
+        step = const.tile([P, DEPTH], F32)
+        nc.vector.tensor_scalar(out=step[:, FIRST:DEPTH], in0=iota_f[:, FIRST:DEPTH], scalar1=less[:, 0:1], scalar2=1.0, op0=ALU.add, op1=ALU.add)
+        nc.vector.tensor_scalar(out=step[:, 0:FIRST], in0=iota_f[:, 0:FIRST], scalar1=aid[:, 0:1], scalar2=1.0, op0=ALU.add, op1=ALU.add)
 
         mask = const.tile([P, PHONES], F32)
-        nc.vector.tensor_single_scalar(out=mask[:], in_=map2[:], scalar=0.0, op=ALU.is_gt)
+        nc.vector.tensor_single_scalar(out=mask[:], in_=map2[:, 1, :], scalar=0.0, op=ALU.is_gt)
         incl = const.tile([P, PHONES], F32)
         nc.vector.tensor_tensor_scan(out=incl[:], data0=mask[:], data1=mask[:], initial=0.0, op0=ALU.add, op1=ALU.max)
         count = incl[:, PHONES - 1 : PHONES]
-        act_b = const.tile([P, NV, 32], BF16)
-        for h in range(NV):
-            nc.vector.tensor_scalar(
-                out=act_b[:, h, :], in0=count.to_broadcast([P, 32]), scalar1=base[:, 0:1], scalar2=float(2 * DEPTH * h),
-                op0=ALU.subtract, op1=ALU.is_gt,
-            )
-        active = const.tile([P, NV], F32)
-        nc.vector.tensor_copy(out=active[:], in_=act_b[:, :, 0])
-        rank1 = const.tile([P, PHONES], F32)
-        nc.vector.tensor_tensor(out=rank1[:], in0=incl[:], in1=mask[:], op=ALU.mult)
-        rel = const.tile([P, NV, PHONES], BF16)
-        left_b = const.tile([P, NV, 32], BF16)
-        for h in range(NV):
-            nc.vector.tensor_scalar(
-                out=rel[:, h, :], in0=rank1[:], scalar1=base[:, 0:1], scalar2=float(2 * DEPTH * h + 1), op0=ALU.subtract, op1=ALU.subtract
-            )
-            nc.vector.tensor_scalar(
-                out=left_b[:, h, :], in0=count.to_broadcast([P, 32]), scalar1=base[:, 0:1], scalar2=float(2 * DEPTH * h),
-                op0=ALU.subtract, op1=ALU.subtract,
-            )
+        over = const.tile([P, 6], BF16)
+        nc.vector.tensor_tensor(out=over[:], in0=count.to_broadcast([P, 6]), in1=lims[:], op=ALU.is_gt)
+        nc.vector.tensor_tensor(out=map2[:, 0, :], in0=incl[:], in1=mask[:], op=ALU.mult)
 
         wt = []
 
@@ -170,11 +181,13 @@ def tile_compositionalphoneticsmodel_t_kernel(tc, enc_output, feature2phone, map
                 nc.tensor.transpose(sel_p[:, c, :], takes[:, d, c * P : (c + 1) * P], ident_b[:])
             nc.scalar.activation(out=sel[:, d, :, :], in_=sel_p[:], func=ACT.Sign)
 
-        wg = const.tile([P, 2, DEPTH, P * 4], BF16, align_bytes=64)
+        wgs = {}
         w_codes = const.tile([P, 2, DEPTH, P], U32, align_bytes=64)
         w_scales = const.tile([P, 2, DEPTH, P], U8, align_bytes=64)
 
         def wslot_make(d, engines):
+            wg = apool.tile([P, 2, P * 4], BF16, tag="acc", align_bytes=64)
+            wgs[d] = wg
             for g in range(2):
                 wp = ps_m.tile([P, 4 * P], F32, tag="pm")
                 for ue in range(4):
@@ -186,7 +199,7 @@ def tile_compositionalphoneticsmodel_t_kernel(tc, enc_output, feature2phone, map
                             start=(c == 0),
                             stop=(c == 1),
                         )
-                dst = wg[:, g, d, :].rearrange("q (l t) -> q l t", t=4)
+                dst = wg[:, g, :].rearrange("q (l t) -> q l t", t=4)
                 src = wp[:].rearrange("q (t l) -> q l t", t=4)
                 if engines[g] == "v":
                     nc.vector.tensor_copy(out=dst, in_=src)
@@ -195,27 +208,20 @@ def tile_compositionalphoneticsmodel_t_kernel(tc, enc_output, feature2phone, map
 
         def wslot_quant(d):
             for g in range(2):
-                nc.vector.quantize_mx(out=w_codes[:, g, d, :].bitcast(FP8X4), scales=w_scales[:, g, d, :], in_=wg[:, g, d, :])
+                nc.vector.quantize_mx(out=w_codes[:, g, d, :].bitcast(FP8X4), scales=w_scales[:, g, d, :], in_=wgs[d][:, g, :])
 
         gain = const.tile([P, DEPTH], F32)
-        perm = const.tile([P, 2, P], F32)
-        bias = const.tile([P, PHONEMES], F32)
-        bias_x = const.tile([P, 1], F32)
+        perm = const.tile([P, P], F32)
+        bias_h = const.tile([P, 1], F32)
 
         def gain_make():
             nc.vector.tensor_single_scalar(out=gain[:], in_=gain_l[:], scalar=1.0 / 32.0, op=ALU.mult)
 
         def perm_make():
-            shown = const.tile([P, P], BF16)
-            nc.vector.tensor_tensor(out=shown[:], in0=others[:], in1=place[:, 1, :], op=ALU.add)
-            perm_p = ps_f.tile([P, 2, P], BF16, tag="pf")
-            nc.tensor.transpose(perm_p[:, 0, :], place[:, 0, :], ident_b[:])
-            nc.tensor.transpose(perm_p[:, 1, :], shown[:], ident_b[:])
+            perm_p = ps_f.tile([P, P], BF16, tag="pf")
+            nc.tensor.transpose(perm_p[:], place[:, 1, :], ident_b[:])
             nc.scalar.copy(out=perm[:], in_=perm_p[:])
-            row_p = ps_f.tile([P, P], F32, tag="pf")
-            nc.tensor.matmul(out=row_p[:], lhsT=act_b[:, 0, 0:1].to_broadcast([P, P]), rhs=ident_b[:], start=True, stop=True)
-            nc.vector.tensor_scalar(out=bias[:], in0=row_p[:, 64:128], scalar1=0.5, scalar2=NEG_BIG, op0=ALU.is_lt, op1=ALU.mult)
-            nc.vector.tensor_scalar(out=bias_x[:], in0=part_f[:], scalar1=lid[:, 2:3], scalar2=NEG_BIG, op0=ALU.is_ge, op1=ALU.mult)
+            nc.vector.tensor_single_scalar(out=bias_h[:], in_=helper[:], scalar=NEG_BIG, op=ALU.mult)
 
         v_all = const.tile([P, NBLK * 256], F32)
         neg_max = const.tile([P, NBLK * 4], F32)
@@ -232,25 +238,24 @@ def tile_compositionalphoneticsmodel_t_kernel(tc, enc_output, feature2phone, map
         def reorder(n, eng="s"):
             b, k = n // 4, n % 4
             g, sp = k // 2, k % 2
-            if k == 0:
-                xr = rpool.tile([P, 4, 2, 2, P], F32)
-                xrs[b] = xr
+            xr = rpool.tile([P, 2, 2, P], F32)
+            xrs[n] = xr
             src = xs[b][:].bitcast(F32).rearrange("p (s c) -> p s c", s=4)[:, 2 * sp : 2 * sp + 2, g * 256 : (g + 1) * 256].rearrange("p s (w u) -> p s u w", u=2)
             if eng == "v":
-                nc.vector.tensor_copy(out=xrs[b][:, k, :, :, :], in_=src)
+                nc.vector.tensor_copy(out=xrs[n][:], in_=src)
             elif eng == "p":
-                nc.gpsimd.tensor_copy(out=xrs[b][:, k, :, :, :].bitcast(I32), in_=src.bitcast(I32))
+                nc.gpsimd.tensor_copy(out=xrs[n][:].bitcast(I32), in_=src.bitcast(I32))
             else:
-                nc.scalar.copy(out=xrs[b][:, k, :, :, :], in_=src)
+                nc.scalar.copy(out=xrs[n][:], in_=src)
             if k == 3 and b + XBUFS < NBLK:
                 loads.append(b + XBUFS)
 
         def a_transpose(n, i):
             b, k = n // 4, n % 4
             g, sp = k // 2, k % 2
-            if k == 0 and i == 0:
-                gr = gpool.tile([P, 2 * BLOCK * 4], BF16, align_bytes=64)
-                grs[b] = gr
+            if (b, g) not in grs:
+                gr = gpool.tile([P, BLOCK * 4], BF16, align_bytes=64)
+                grs[(b, g)] = gr
             if i == 0:
                 pt = ps_t.tile([P, 4 * P], F32, tag="pt")
                 pts[n] = pt
@@ -259,11 +264,11 @@ def tile_compositionalphoneticsmodel_t_kernel(tc, enc_output, feature2phone, map
                 lo = (2 * sp + s2) * 512 + 256 * g
                 words = xs[b][:].bitcast(F32)[:, lo + u : lo + 256 : 2]
             else:
-                words = xrs[b][:, k, s2, u, :]
+                words = xrs[n][:, s2, u, :]
             nc.tensor.transpose(pts[n][:, i * P : (i + 1) * P], words, ident_f[:])
             if i == 3:
-                grw = grs[b][:].bitcast(F32)
-                nc.scalar.copy(out=grw[:, k * 512 : (k + 1) * 512].rearrange("q (t u) -> q t u", u=2), in_=pts[n][:].rearrange("q (u t) -> q t u", u=2))
+                grw = grs[(b, g)][:].bitcast(F32)
+                nc.scalar.copy(out=grw[:, sp * 512 : (sp + 1) * 512].rearrange("q (t u) -> q t u", u=2), in_=pts[n][:].rearrange("q (u t) -> q t u", u=2))
                 if b < STRIDED and k == 3 and b + XBUFS < NBLK:
                     loads.append(b + XBUFS)
 
@@ -281,14 +286,17 @@ def tile_compositionalphoneticsmodel_t_kernel(tc, enc_output, feature2phone, map
             nc.vector.quantize_mx(
                 out=codes[:, g * BLOCK : (g + 1) * BLOCK].bitcast(FP8X4),
                 scales=scales[:, g * BLOCK : (g + 1) * BLOCK],
-                in_=grs[b][:, g * BLOCK * 4 : (g + 1) * BLOCK * 4],
+                in_=grs[(b, g)][:],
             )
 
         def mx_pass(b, d, g):
             if g == 0:
                 if d == 0:
-                    acc = apool.tile([P, BLOCK], F32)
+                    acc = apool.tile([P, BLOCK], F32, tag="acc", align_bytes=64)
                     accs[b] = acc
+                if d == FIRST:
+                    top = bpool.tile([P, BLOCK], F32)
+                    tops[b] = top
                 pm = ps_m.tile([P, BLOCK], F32, tag="pm")
                 pms[(b, d)] = pm
             pm = pms[(b, d)]
@@ -302,59 +310,42 @@ def tile_compositionalphoneticsmodel_t_kernel(tc, enc_output, feature2phone, map
                 start=(g == 0),
                 stop=(g == 1),
             )
-            if g == 1 and d == 0:
-                nc.scalar.activation(out=accs[b][:], in_=pm[:], func=ACT.Copy, scale=gain[:, 0:1])
-            elif g == 1:
-                nc.vector.scalar_tensor_tensor(out=accs[b][:], in0=pm[:], scalar=gain[:, d : d + 1], in1=accs[b][:], op0=ALU.mult, op1=ALU.max)
+            if g == 1:
+                dst = accs[b] if d < FIRST else tops[b]
+                if d in (0, FIRST):
+                    nc.scalar.activation(out=dst[:], in_=pm[:], func=ACT.Copy, scale=gain[:, d : d + 1])
+                else:
+                    nc.vector.scalar_tensor_tensor(out=dst[:], in0=pm[:], scalar=gain[:, d : d + 1], in1=dst[:], op0=ALU.mult, op1=ALU.max)
 
         def mx(b, d):
             mx_pass(b, d, 0)
             mx_pass(b, d, 1)
 
-        def extra_move(b):
-            mov = vpool.tile([P, BLOCK], F32)
-            nc.sync.dma_start(out=mov[0 : P - EXTRA, :], in_=accs[b][EXTRA:P, :])
-            movs[b] = mov
+        def move_second(b):
+            q, r = b // 4, 32 * (b % 4)
+            nc.sync.dma_start(out=e2s[q % 2][r : r + SECOND, :], in_=accs[b][HELP : HELP + SECOND, :])
+            nc.sync.dma_start(out=p2s[q % 2][r : r + SECOND, :], in_=accs[b][0:SECOND, :])
 
-        def extra_join(b):
-            n = P - EXTRA
-            nc.vector.scalar_tensor_tensor(
-                out=accs[b][0:n, :], in0=movs[b][0:n, :], scalar=bias_x[0:n, 0:1], in1=accs[b][0:n, :], op0=ALU.add, op1=ALU.max
-            )
+        def move_first(b):
+            nc.sync.dma_start(out=tops[b][0:PARTNERS, :], in_=accs[b][HELP + SECOND : HELP + HELPERS, :])
 
-        def f_transpose(b, s):
+        def quad_join(q):
+            nc.vector.tensor_tensor(out=p2s[q % 2][:], in0=e2s[q % 2][:], in1=p2s[q % 2][:], op=ALU.max)
+            for i in range(4):
+                nc.sync.dma_start(out=accs[4 * q + i][0:SECOND, :], in_=p2s[q % 2][32 * i : 32 * i + SECOND, :])
+
+        def combine(b):
+            nc.vector.scalar_tensor_tensor(out=tops[b][:], in0=accs[b][:], scalar=bias_h[:, 0:1], in1=tops[b][:], op0=ALU.add, op1=ALU.max)
+
+        def f_transpose(b, s, pool=ps_f, tag="pf"):
             if s == 0:
-                pf = ps_f.tile([P, 4, P], F32, tag="pf")
+                pf = pool.tile([P, 4, P], F32, tag=tag)
                 pfs[b] = pf
-            nc.tensor.transpose(pfs[b][:, s, :], accs[b][:, s * P : (s + 1) * P], perm[:, 0, :])
+            nc.tensor.transpose(pfs[b][:, s, :], tops[b][:, s * P : (s + 1) * P], perm[:])
             if s == 3:
                 a1 = spool.tile([P, 4, PHONEMES], F32)
                 a1s[b] = a1
                 nc.scalar.copy(out=a1[:], in_=pfs[b][:, :, 64:128])
-                nc.gpsimd.tensor_tensor(out=a1[:], in0=a1[:], in1=bias[:].unsqueeze(1).to_broadcast([P, 4, PHONEMES]), op=ALU.add)
-
-        def end_bank(b, fb, pool, tag):
-            pf = pool.tile([P, 2, 2, P], F32, tag=tag)
-            for i in range(2):
-                for h in range(2):
-                    s = 2 * fb + i
-                    nc.tensor.transpose(pf[:, h, i, :], accs[b][:, s * P : (s + 1) * P], perm[:, h, :])
-            u = spool.tile([P, 2, P], F32)
-            nc.scalar.copy(out=u[:], in_=pf[:, 1, :, :])
-            ends[(b, fb)] = (pf, u)
-
-        def end_join(b, fb, step):
-            pf, u = ends[(b, fb)]
-            if step == 0:
-                nc.vector.tensor_tensor(out=u[:], in0=pf[:, 0, :, :], in1=u[:], op=ALU.max)
-            elif step == 1:
-                t = spool.tile([P, 2, PHONEMES], F32)
-                nc.vector.tensor_tensor(out=t[:], in0=u[:, :, 64:128], in1=bias[:].unsqueeze(1).to_broadcast([P, 2, PHONEMES]), op=ALU.add)
-                ends[(b, fb)] = (t, u)
-            else:
-                t, u = ends[(b, fb)]
-                vv = v_all[:, b * 256 + fb * 128 : b * 256 + (fb + 1) * 128].rearrange("p (s m) -> p s m", m=PHONEMES)
-                nc.vector.tensor_tensor(out=vv, in0=u[:, :, 0:64], in1=t[:], op=ALU.max)
 
         def lane_join(b):
             vv = v_all[:, b * 256 : (b + 1) * 256].rearrange("p (s m) -> p s m", m=PHONEMES)
@@ -391,65 +382,108 @@ def tile_compositionalphoneticsmodel_t_kernel(tc, enc_output, feature2phone, map
             queue.dma_start(out=out_v[:, b0:b1, :], in_=v_all[:, b0 * 256 : b1 * 256].rearrange("p (n f) -> p n f", f=256))
 
         wt_make(0)
-        lid_p = ps_m.tile([P, 3, 32], F32, tag="pm")
-        nc.tensor.matmul(out=lid_p[:, 1, :], lhsT=tri[:], rhs=act_b[:, 1, :], start=True, stop=True)
-        nc.tensor.matmul(out=lid_p[:, 2, :], lhsT=ones[:, 0:P], rhs=act_b[:, 1, :], start=True, stop=True)
-        nc.tensor.matmul(out=lid_p[:, 0, :], lhsT=tri_a[:], rhs=act_b[:, 0, :], start=True, stop=False)
-        nc.tensor.matmul(out=lid_p[:, 0, :], lhsT=tri_b[:], rhs=act_b[:, 1, :], start=False, stop=True)
-        lid = const.tile([P, 3], F32)
-        nc.vector.tensor_copy(out=lid[:], in_=lid_p[:, :, 0])
-        place = const.tile([P, NV, P], BF16)
-        partner = const.tile([P, P], BF16)
-        nc.vector.tensor_scalar(
-            out=partner[:], in0=iota_f[:], scalar1=lid[:, 1:2], scalar2=active[:, 1:2], op0=ALU.is_equal, op1=ALU.mult
+        warm(WARM[1])
+        lid_p = ps_m.tile([P, 2, 6], F32, tag="pm")
+        nc.tensor.matmul(out=lid_p[:, 0, :], lhsT=tri[:], rhs=over[:], start=True, stop=True)
+        nc.tensor.matmul(out=lid_p[:, 1, :], lhsT=ones[:, 0:P], rhs=over[:], start=True, stop=True)
+        light = const.tile([P, 1], F32)
+        nc.vector.tensor_scalar(out=light[:], in0=over[:, 2:3], scalar1=-1.0, scalar2=1.0, op0=ALU.mult, op1=ALU.add)
+        aided = const.tile([P, 1], F32)
+        nc.vector.tensor_copy(out=aided[:], in_=over[:, 0:1])
+        only = const.tile([P, 1], F32)
+        nc.vector.tensor_tensor(out=only[:], in0=over[:, 0:1], in1=over[:, 1:2], op=ALU.subtract)
+        part_x = const.tile([P, 1], F32)
+        nc.vector.scalar_tensor_tensor(out=part_x[:], in0=over[:, 0:1], scalar=-FAR, in1=part_f[:], op0=ALU.mult, op1=ALU.add)
+        lid = const.tile([P, 2, 6], F32)
+        nc.vector.tensor_copy(out=lid[:], in_=lid_p[:])
+        steps = const.tile([P, 3], F32)
+        nc.vector.tensor_tensor(out=steps[:], in0=over[:, 3:6], in1=strides[:], op=ALU.mult)
+        lane_c = const.tile([P, 2], BF16)
+        nc.vector.tensor_copy(out=lane_c[:, 1:2], in_=count)
+        rank_l = const.tile([P, 1], F32)
+        nc.vector.tensor_scalar(out=rank_l[:], in0=lid[:, 0, 2:3], scalar1=-1.0, scalar2=part_f[:, 0:1], op0=ALU.mult, op1=ALU.add)
+        two = const.tile([P, 1], F32)
+        nc.vector.scalar_tensor_tensor(out=two[:], in0=lid[:, 0, 1:2], scalar=-2.0, in1=lid[:, 0, 0:1], op0=ALU.mult, op1=ALU.add)
+        rest = const.tile([P, 1], F32)
+        nc.vector.scalar_tensor_tensor(
+            out=rest[:], in0=lid[:, 0, 0:1], scalar=lid[:, 1, 0:1], in1=part_x[:], op0=ALU.subtract, op1=ALU.subtract
         )
-        skip = const.tile([P, 1], F32)
-        nc.vector.tensor_scalar(out=skip[:], in0=lid[:, 0:1], scalar1=float(EXTRA) - FAR, scalar2=lid[:, 2:3], op0=ALU.is_ge, op1=ALU.mult)
+        nc.vector.scalar_tensor_tensor(out=lane_c[:, 0:1], in0=steps[:, 0:1], scalar=steps[:, 1:2], in1=steps[:, 2:3], op0=ALU.add, op1=ALU.add)
+        helps = const.tile([P, 1], F32)
+        nc.vector.tensor_scalar(out=helps[:], in0=rank_l[:], scalar1=float(HELPERS), scalar2=light[:, 0:1], op0=ALU.is_lt, op1=ALU.mult)
+        shift = const.tile([P, 1], F32)
+        nc.vector.tensor_scalar(out=shift[:], in0=two[:], scalar1=lid[:, 1, 1:2], scalar2=only[:, 0:1], op0=ALU.add, op1=ALU.mult)
+        rank_o = const.tile([P, 1], F32)
+        nc.vector.tensor_scalar(out=rank_o[:], in0=rank_l[:], scalar1=float(HELPERS), scalar2=rest[:, 0:1], op0=ALU.min, op1=ALU.add)
+        place = const.tile([P, 2, P], BF16)
         nc.vector.tensor_scalar(
-            out=place[:, 1, :], in0=iota_x[:], scalar1=lid[:, 1:2], scalar2=active[:, 1:2], op0=ALU.is_equal, op1=ALU.mult
+            out=place[:, 1, HELP : HELP + HELPERS], in0=iota_f[:, 0:HELPERS], scalar1=rank_l[:, 0:1], scalar2=light[:, 0:1], op0=ALU.is_equal, op1=ALU.mult
         )
-        others = const.tile([P, P], BF16)
-        nc.vector.tensor_scalar(out=others[:], in0=iota_n[:], scalar1=skip[:, 0:1], scalar2=lid[:, 0:1], op0=ALU.subtract, op1=ALU.is_equal)
-        nc.vector.tensor_tensor(out=place[:, 0, :], in0=others[:], in1=partner[:], op=ALU.add)
+        rank_p = const.tile([P, 1], F32)
+        nc.vector.tensor_tensor(out=rank_p[:], in0=shift[:], in1=lid[:, 0, 1:2], op=ALU.add)
+        rank_r = const.tile([P, 1], F32)
+        nc.vector.scalar_tensor_tensor(out=rank_r[:], in0=helps[:], scalar=FAR, in1=rank_o[:], op0=ALU.mult, op1=ALU.add)
+        front = const.tile([P, HELP], BF16)
+        nc.vector.tensor_scalar(out=front[:], in0=iota_f[:, 0:HELP], scalar1=rank_p[:, 0:1], scalar2=aided[:, 0:1], op0=ALU.is_equal, op1=ALU.mult)
+        nc.vector.tensor_scalar(
+            out=place[:, 0, HELP + HELPERS : P], in0=rank_n[:, HELP + HELPERS : P], scalar1=rank_r[:, 0:1], scalar2=None, op0=ALU.is_equal
+        )
+        nc.vector.scalar_tensor_tensor(
+            out=place[:, 0, 0:HELP], in0=rank_n[:, 0:HELP], scalar=rank_r[:, 0:1], in1=front[:], op0=ALU.is_equal, op1=ALU.add
+        )
+        nc.vector.tensor_copy(out=place[:, 1, HELP + HELPERS : P], in_=place[:, 0, HELP + HELPERS : P])
+        nc.vector.tensor_copy(out=place[:, 0, HELP : HELP + SECOND], in_=place[:, 0, 0:SECOND])
+        nc.vector.tensor_copy(out=place[:, 0, HELP + SECOND : HELP + HELPERS], in_=place[:, 0, 0:PARTNERS])
+        nc.vector.tensor_copy(out=place[:, 1, 0:HELP], in_=place[:, 0, 0:HELP])
 
-        n_p = ps_m.tile([P, 32], F32, tag="pm")
-        rk_p = ps_m.tile([P, 2, PHONES], F32, tag="pm")
-        for h in range(NV):
-            nc.tensor.matmul(out=rk_p[:, 1, :], lhsT=place[:, h, :], rhs=map2[:], start=(h == 0), stop=(h == NV - 1))
-        for h in range(NV):
-            nc.tensor.matmul(out=n_p[:], lhsT=place[:, h, :], rhs=left_b[:, h, :], start=(h == 0), stop=(h == NV - 1))
-        for h in range(NV):
-            nc.tensor.matmul(out=rk_p[:, 0, :], lhsT=place[:, h, :], rhs=rel[:, h, :], start=(h == 0), stop=(h == NV - 1))
-        gains = const.tile([P, PHONES], BF16)
-        nc.scalar.copy(out=gains[:], in_=rk_p[:, 1, :])
+        wt_make(1)
+        warm(WARM[2])
+        for n in HEAD_ORDER[:3]:
+            a_bank(n)
+        warm(WARM[3])
+
+        lane_p = []
+        rk_p = []
+        for h in range(2):
+            lane = ps_t.tile([P, 2], F32, tag="pt", name="lane%d" % h)
+            nc.tensor.matmul(out=lane[:], lhsT=place[:, h, :], rhs=lane_c[:], start=True, stop=True)
+            lane_p.append(lane)
+            rk = ps_m.tile([P, 2, PHONES], F32, tag="pm", name="rk%d" % h)
+            nc.tensor.matmul(out=rk[:].rearrange("p a b -> p (a b)"), lhsT=place[:, h, :], rhs=map2[:].rearrange("p a b -> p (a b)"), start=True, stop=True)
+            rk_p.append(rk)
+        gains = const.tile([P, 2, PHONES], BF16)
+        for h in range(2):
+            nc.scalar.copy(out=gains[:, h, :], in_=rk_p[h][:, 1, :])
         want = const.tile([P, DEPTH], F32)
-        nc.vector.scalar_tensor_tensor(out=want[:], in0=iota_f[:, 0:DEPTH], scalar=n_p[:, 0:1], in1=iota_f[:, 0:DEPTH], op0=ALU.is_lt, op1=ALU.mult)
+        for h, cols in ((0, slice(0, FIRST)), (1, slice(FIRST, DEPTH))):
+            nc.vector.tensor_scalar(
+                out=want[:, cols], in0=step[:, cols], scalar1=lane_p[h][:, 0:1], scalar2=lane_p[h][:, 1:2], op0=ALU.add, op1=ALU.min
+            )
 
         takes = const.tile([P, DEPTH, PHONES], BF16)
         gain_l = const.tile([P, DEPTH], F32)
 
         def takes_make(d):
+            h = 0 if d < FIRST else 1
             nc.vector.scalar_tensor_tensor(
-                out=takes[:, d, :], in0=rk_p[:, 0, :], scalar=want[:, d : d + 1], in1=gains[:], op0=ALU.is_equal, op1=ALU.mult,
+                out=takes[:, d, :], in0=rk_p[h][:, 0, :], scalar=want[:, d : d + 1], in1=gains[:, h, :], op0=ALU.is_equal, op1=ALU.mult,
                 accum_out=gain_l[:, d : d + 1],
             )
 
-        wt_make(1)
         for d in range(DEPTH):
             takes_make(d)
         sel_make(0)
-        a_bank(0)
+        a_bank(HEAD_ORDER[3])
         sel_make(1)
-        a_bank(1)
-        x_n = 2
-        r_n = 4
+        x_n = 4
+        r_n = 4 * STRIDED
         q_n = 0
         for d in range(DEPTH):
             wslot_make(d, W_ENG[d])
             if d + 2 < DEPTH:
                 sel_make(d + 2)
             for n in range(r_n, r_n + HEAD_R[d]):
-                reorder(n, "p")
+                reorder(n, HEAD_ENG[n % 2])
             r_n += HEAD_R[d]
             for n in range(x_n, x_n + HEAD_X[d]):
                 a_bank(n)
@@ -464,113 +498,121 @@ def tile_compositionalphoneticsmodel_t_kernel(tc, enc_output, feature2phone, map
         mx(0, 0)
         mx(1, 0)
         perm_make()
+        e2s = []
+        p2s = []
+        for i in range(2):
+            e2 = const.tile([P, BLOCK], F32, name="e2%d" % i)
+            nc.gpsimd.memset(e2[:], 0.0)
+            e2s.append(e2)
+            p2 = const.tile([P, BLOCK], F32, name="p2%d" % i)
+            nc.gpsimd.memset(p2[:], 0.0)
+            p2s.append(p2)
+
         for n in range(r_n, x_n + R_LEAD):
             reorder(n, R_ENG[n % 8])
         r_n = x_n + R_LEAD
 
         nh = 2 * NBLK
         npair = NBLK // 2
-        x_done = x_n
-        q_n = Q_LEAD
         group = 0
-        pending = []
         stores = []
-        tasks = []
+        pending = []
 
-        def finish_some():
-            if stores:
-                s0 = stores.pop(0)
-                store(s0, s0 + 2, nc.sync)
-            if pending:
-                s0 = pending.pop(0)
-                finish(s0, s0 + 2, nc.gpsimd)
-                stores.append(s0)
-
-        for j in range(npair):
-            banks = [(b, d) for d in range(1, DEPTH) for b in (2 * j, 2 * j + 1)]
-            if j + 1 < npair:
-                banks += [(2 * j + 2, 0), (2 * j + 3, 0)]
-            t_list = []
-            for c in T_ORDER:
-                if c == "x":
-                    t_list += [("x", x_n, s) if x_n < 2 * nh else None for s in range(4)]
-                    x_n += 1
-                elif j >= 1:
-                    t_list += [("f", 2 * j - 2 + int(c), s) for s in range(4)]
-                else:
-                    t_list += [None] * 4
+        for j in range(npair - 2):
+            b0 = 2 * j
             for ph in range(3):
                 due = len(loads)
-                m_run = banks[4 * ph : 4 * ph + 4]
-                if j >= 1:
-                    if ph < 2:
-                        tasks.append((extra_join, 2 * j - 2 + ph))
-                    if ph == 0 and j >= 2:
-                        tasks += [(lane_join, 2 * j - 3), (row_max, 2 * j - 3)]
-                for n, (b, d) in enumerate(m_run):
+                m_run = (
+                    [(b0, 1), (b0 + 1, 1), (b0, 3)],
+                    [(b0, 2), (b0 + 1, 2), (b0 + 1, 3)],
+                    ([(b0 - 2, 4), (b0 - 1, 4)] if j >= 1 else []) + [(b0 + 2, 0), (b0 + 3, 0)],
+                )[ph]
+                tasks = []
+                if ph == 0 and j >= 3:
+                    tasks.append((combine, b0 - 5))
+                if ph == 2 and j >= 2:
+                    tasks.append((combine, b0 - 4))
+                if ph >= 1 and j >= 3:
+                    tasks += [(lane_join, b0 - 7 + ph), (row_max, b0 - 7 + ph)]
+                if ph == 0 and j >= 2 and j % 2 == 0:
+                    tasks.append((quad_join, j // 2 - 1))
+                for b, d in m_run:
                     mx(b, d)
-                    if d == DEPTH - 1 and j + 1 < npair:
-                        extra_move(b)
                     if tasks:
                         fn, arg = tasks.pop(0)
                         fn(arg)
                 for fn, arg in tasks:
                     fn(arg)
-                tasks = []
-                x_ready = x_done
-                for item in t_list[len(t_list) * ph // 3 : len(t_list) * (ph + 1) // 3]:
-                    if item:
-                        kind, n, s = item
-                        if kind == "x":
-                            a_transpose(n, s)
-                            if s == 3:
-                                x_done = n + 1
-                        else:
-                            f_transpose(n, s)
-                for i in range(Q_RUN[ph]):
-                    if q_n < nh:
-                        quant(q_n)
-                        q_n += 1
-                    if ph == 2 and i == 1 and j >= 1:
-                        lane_join(2 * j - 2)
-                        row_max(2 * j - 2)
-                while r_n < min(2 * nh, x_n + R_LEAD - 10 + (10 * (ph + 1)) // 3):
+                if ph == 1:
+                    for b in (b0, b0 + 1):
+                        move_second(b)
+                        move_first(b)
+                x_run = [(n, s) for n in range(x_n, min(2 * nh, x_n + 8)) for s in range(4)][X_CUTS[ph] : X_CUTS[ph + 1]]
+                for n, s in x_run[:F_AT]:
+                    a_transpose(n, s)
+                if ph < 2 and j >= 3:
+                    for s in range(4):
+                        f_transpose(b0 - 6 + ph, s)
+                for n, s in x_run[F_AT:]:
+                    a_transpose(n, s)
+                for i in range(Q_RUN[ph] + (2 if j == npair - 3 and ph == 2 else 0)):
+                    quant(q_n)
+                    q_n += 1
+                while r_n < min(2 * nh, x_n + R_LEAD + (X_CUTS[ph + 1] + 3) // 4):
                     reorder(r_n, R_ENG[r_n % 8])
                     r_n += 1
-                e = 2 * j - 2 if ph == 2 and j >= 1 else 2 * j - 3 if ph == 0 and j >= 2 else -1
-                if e >= 0:
+                if ph >= 1 and j >= 3:
+                    e = b0 - 7 + ph
                     exps(e)
                     if group < len(GROUPS) - 1 and e == GROUPS[group][1] - 1:
                         group_ln(group, nc.gpsimd)
                         pending.extend(range(GROUPS[group][0], GROUPS[group][1], 2))
                         group += 1
-                if j + 1 < npair:
-                    finish_some()
                 loads_flush(due)
-        z = NBLK - 1
-        last = [(b, fb) for b in (z - 1, z) for fb in range(2)]
-        end_bank(z - 1, 0, ps_m, "pm")
-        end_bank(z - 1, 1, ps_m, "pm")
-        end_bank(z, 0, ps_m, "pm")
-        lane_join(z - 2)
-        row_max(z - 2)
-        end_bank(z, 1, ps_f, "pf")
-        exps(z - 2)
-        for half in (last[:2], last[2:]):
-            for step in range(3):
-                for b, fb in half:
-                    end_join(b, fb, step)
-        for b in (z - 1, z):
+            x_n += 8
+
+        z = NBLK
+
+        def moves(b):
+            move_second(b)
+            move_first(b)
+
+        def last_f(b):
+            for s in range(4):
+                f_transpose(b, s, ps_t, "pt")
+
+        def last_max(b):
             row_max(b)
             exps(b)
+            for s0 in stores:
+                store(s0, s0 + 2, nc.sync)
+            stores.clear()
+            if pending:
+                s0 = pending.pop(0)
+                finish(s0, s0 + 2, nc.gpsimd)
+                stores.append(s0)
+            if pending:
+                s0 = pending.pop(0)
+                finish_scalar(s0, s0 + 2)
+                stores.append(s0)
 
-        for s0 in pending:
-            finish(s0, s0 + 2, nc.gpsimd)
-        for s0 in stores + pending:
+        c, f, lj, rm = combine, last_f, lane_join, last_max
+        for fn, b, *d in (
+            (mx, 4, 1), (c, 9), (mx, 3, 1), (mx, 2, 0), (mx, 1, 0), (quad_join, 2), (mx, 4, 2), (mx, 3, 2), (f, 10), (mx, 2, 1), (lj, 10), (mx, 1, 1),
+            (rm, 10), (f, 9), (mx, 2, 2), (c, 8), (mx, 1, 2), (lj, 9), (mx, 4, 3), (mx, 3, 3), (moves, 4), (moves, 3), (mx, 6, 4), (rm, 9), (mx, 5, 4),
+            (c, 7), (f, 8), (mx, 2, 3), (mx, 1, 3), (moves, 2), (moves, 1), (c, 6), (mx, 4, 4), (lj, 8), (f, 7), (c, 5), (rm, 8), (mx, 3, 4), (lj, 7), (f, 6),
+            (quad_join, 1), (mx, 2, 4), (rm, 7), (lj, 6), (f, 5), (mx, 1, 4), (rm, 6), (lj, 5), (c, 4), (rm, 5), (f, 4), (c, 3), (f, 3), (c, 2), (f, 2),
+            (lj, 4), (c, 1), (f, 1), (lj, 3), (rm, 4), (lj, 2), (rm, 3), (lj, 1), (rm, 2), (rm, 1),
+        ):
+            fn((NBLK // 4 if fn is quad_join else z) - b, *d)
+
+        for s0 in stores:
             store(s0, s0 + 2, nc.sync)
         g0 = GROUPS[-1][0]
         group_ln(len(GROUPS) - 1, nc.vector)
-        finish(g0, g0 + 3, nc.vector)
-        store(g0, g0 + 3, nc.sync)
-        finish_scalar(g0 + 3, g0 + 6)
-        store(g0 + 3, g0 + 6, nc.scalar)
+        for i in range(3):
+            if i < 2:
+                finish_scalar(g0 + 2 * i, g0 + 2 * i + 2)
+                store(g0 + 2 * i, g0 + 2 * i + 2, nc.sync)
+            finish(g0 + 4 + 2 * i, g0 + 6 + 2 * i, nc.vector)
+            store(g0 + 4 + 2 * i, g0 + 6 + 2 * i, nc.sync)

@@ -26,6 +26,7 @@ DEPTH = 5
 FIRST = 3
 PARTNERS = 16
 SECOND = 3
+MOVED = 4
 HELP = 96
 HELPERS = SECOND + PARTNERS
 STRIDED = 1
@@ -39,10 +40,6 @@ HEAD_ENG = "pp"
 HEAD_R = (2, 3, 3, 2, 2)
 HEAD_Q = (0, 1, 1, 2, 2)
 R_LEAD = 6
-Q_RUN = (1, 1, 2)
-Q_LEAD = 6
-X_CUTS = (0, 10, 20, 32)
-F_AT = 8
 R_ENG = "vsvvsvsv"
 NEG_BIG = -3.0e38
 W_ENG = ("sv", "vv", "sv", "vv", "sv")
@@ -214,6 +211,13 @@ def tile_compositionalphoneticsmodel_t_kernel(tc, enc_output, feature2phone, map
         perm = const.tile([P, P], F32)
         bias_h = const.tile([P, 1], F32)
 
+        bias_q = const.tile([P, 1], F32)
+
+        def bias_make():
+            rest_i = const.tile([P, 1], I32)
+            nc.vector.tensor_single_scalar(out=rest_i[:], in_=part_i[:], scalar=31, op=ALU.bitwise_and)
+            nc.vector.tensor_scalar(out=bias_q[:], in0=rest_i[:], scalar1=float(SECOND), scalar2=NEG_BIG, op0=ALU.is_equal, op1=ALU.mult)
+
         def gain_make():
             nc.vector.tensor_single_scalar(out=gain[:], in_=gain_l[:], scalar=1.0 / 32.0, op=ALU.mult)
 
@@ -323,16 +327,18 @@ def tile_compositionalphoneticsmodel_t_kernel(tc, enc_output, feature2phone, map
 
         def move_second(b):
             q, r = b // 4, 32 * (b % 4)
-            nc.sync.dma_start(out=e2s[q % 2][r : r + SECOND, :], in_=accs[b][HELP : HELP + SECOND, :])
-            nc.sync.dma_start(out=p2s[q % 2][r : r + SECOND, :], in_=accs[b][0:SECOND, :])
+            nc.sync.dma_start(out=e2s[q % 2][r : r + MOVED, :], in_=accs[b][HELP : HELP + MOVED, :])
+            nc.sync.dma_start(out=p2s[q % 2][r : r + MOVED, :], in_=accs[b][0:MOVED, :])
 
         def move_first(b):
             nc.sync.dma_start(out=tops[b][0:PARTNERS, :], in_=accs[b][HELP + SECOND : HELP + HELPERS, :])
 
         def quad_join(q):
-            nc.vector.tensor_tensor(out=p2s[q % 2][:], in0=e2s[q % 2][:], in1=p2s[q % 2][:], op=ALU.max)
+            nc.vector.scalar_tensor_tensor(
+                out=p2s[q % 2][:], in0=e2s[q % 2][:], scalar=bias_q[:, 0:1], in1=p2s[q % 2][:], op0=ALU.add, op1=ALU.max
+            )
             for i in range(4):
-                nc.sync.dma_start(out=accs[4 * q + i][0:SECOND, :], in_=p2s[q % 2][32 * i : 32 * i + SECOND, :])
+                nc.sync.dma_start(out=accs[4 * q + i][0:MOVED, :], in_=p2s[q % 2][32 * i : 32 * i + MOVED, :])
 
         def combine(b):
             nc.vector.scalar_tensor_tensor(out=tops[b][:], in0=accs[b][:], scalar=bias_h[:, 0:1], in1=tops[b][:], op0=ALU.add, op1=ALU.max)
@@ -498,6 +504,7 @@ def tile_compositionalphoneticsmodel_t_kernel(tc, enc_output, feature2phone, map
         mx(0, 0)
         mx(1, 0)
         perm_make()
+        bias_make()
         e2s = []
         p2s = []
         for i in range(2):
@@ -520,20 +527,22 @@ def tile_compositionalphoneticsmodel_t_kernel(tc, enc_output, feature2phone, map
 
         for j in range(npair - 2):
             b0 = 2 * j
-            for ph in range(3):
+            for ph in range(4):
                 due = len(loads)
                 m_run = (
                     [(b0, 1), (b0 + 1, 1), (b0, 3)],
-                    [(b0, 2), (b0 + 1, 2), (b0 + 1, 3)],
-                    ([(b0 - 2, 4), (b0 - 1, 4)] if j >= 1 else []) + [(b0 + 2, 0), (b0 + 3, 0)],
+                    [(b0, 2), (b0 + 1, 2)],
+                    [(b0 + 1, 3)] + ([(b0 - 2, 4), (b0 - 1, 4)] if j >= 1 else []),
+                    [(b0 + 2, 0), (b0 + 3, 0)],
                 )[ph]
                 tasks = []
-                if ph == 0 and j >= 3:
+                if ph == 1 and j >= 3:
                     tasks.append((combine, b0 - 5))
-                if ph == 2 and j >= 2:
+                if ph == 3 and j >= 2:
                     tasks.append((combine, b0 - 4))
-                if ph >= 1 and j >= 3:
-                    tasks += [(lane_join, b0 - 7 + ph), (row_max, b0 - 7 + ph)]
+                joined = b0 - 8 + ph
+                if ph >= 2 and j >= 3:
+                    tasks += [(lane_join, joined), (row_max, joined)]
                 if ph == 0 and j >= 2 and j % 2 == 0:
                     tasks.append((quad_join, j // 2 - 1))
                 for b, d in m_run:
@@ -544,38 +553,33 @@ def tile_compositionalphoneticsmodel_t_kernel(tc, enc_output, feature2phone, map
                 for fn, arg in tasks:
                     fn(arg)
                 if ph == 1:
-                    for b in (b0, b0 + 1):
-                        move_second(b)
-                        move_first(b)
-                x_run = [(n, s) for n in range(x_n, min(2 * nh, x_n + 8)) for s in range(4)][X_CUTS[ph] : X_CUTS[ph + 1]]
-                for n, s in x_run[:F_AT]:
-                    a_transpose(n, s)
-                if ph < 2 and j >= 3:
+                    move_second(b0)
+                    move_second(b0 + 1)
+                    move_first(b0)
+                if ph == 2:
+                    move_first(b0 + 1)
+                for n in range(x_n, x_n + 2):
+                    if n < 2 * nh:
+                        a_bank(n)
+                x_n += 2
+                if ph % 2 == 0 and j >= 3:
                     for s in range(4):
-                        f_transpose(b0 - 6 + ph, s)
-                for n, s in x_run[F_AT:]:
-                    a_transpose(n, s)
-                for i in range(Q_RUN[ph] + (2 if j == npair - 3 and ph == 2 else 0)):
+                        f_transpose(b0 - 6 + ph // 2, s)
+                for i in range(3 if j == npair - 3 and ph == 3 else 1):
                     quant(q_n)
                     q_n += 1
-                while r_n < min(2 * nh, x_n + R_LEAD + (X_CUTS[ph + 1] + 3) // 4):
+                while r_n < min(2 * nh, x_n + R_LEAD):
                     reorder(r_n, R_ENG[r_n % 8])
                     r_n += 1
-                if ph >= 1 and j >= 3:
-                    e = b0 - 7 + ph
-                    exps(e)
-                    if group < len(GROUPS) - 1 and e == GROUPS[group][1] - 1:
+                if ph >= 2 and j >= 3:
+                    exps(joined)
+                    if group < len(GROUPS) - 1 and joined == GROUPS[group][1] - 1:
                         group_ln(group, nc.gpsimd)
                         pending.extend(range(GROUPS[group][0], GROUPS[group][1], 2))
                         group += 1
                 loads_flush(due)
-            x_n += 8
 
         z = NBLK
-
-        def moves(b):
-            move_second(b)
-            move_first(b)
 
         def last_f(b):
             for s in range(4):
@@ -584,27 +588,26 @@ def tile_compositionalphoneticsmodel_t_kernel(tc, enc_output, feature2phone, map
         def last_max(b):
             row_max(b)
             exps(b)
-            for s0 in stores:
-                store(s0, s0 + 2, nc.sync)
-            stores.clear()
-            if pending:
-                s0 = pending.pop(0)
-                finish(s0, s0 + 2, nc.gpsimd)
-                stores.append(s0)
-            if pending:
-                s0 = pending.pop(0)
-                finish_scalar(s0, s0 + 2)
-                stores.append(s0)
 
-        c, f, lj, rm = combine, last_f, lane_join, last_max
+        def last_adds(n):
+            for i in range(n + 1):
+                if pending:
+                    s0 = pending.pop(0)
+                    if i == 0:
+                        finish(s0, s0 + 2, nc.gpsimd)
+                    else:
+                        finish_scalar(s0, s0 + 2)
+                    stores.append(s0)
+
+        m1, m2, c, f, lj, rm, qj = move_first, move_second, combine, last_f, lane_join, last_max, quad_join
         for fn, b, *d in (
-            (mx, 4, 1), (c, 9), (mx, 3, 1), (mx, 2, 0), (mx, 1, 0), (quad_join, 2), (mx, 4, 2), (mx, 3, 2), (f, 10), (mx, 2, 1), (lj, 10), (mx, 1, 1),
-            (rm, 10), (f, 9), (mx, 2, 2), (c, 8), (mx, 1, 2), (lj, 9), (mx, 4, 3), (mx, 3, 3), (moves, 4), (moves, 3), (mx, 6, 4), (rm, 9), (mx, 5, 4),
-            (c, 7), (f, 8), (mx, 2, 3), (mx, 1, 3), (moves, 2), (moves, 1), (c, 6), (mx, 4, 4), (lj, 8), (f, 7), (c, 5), (rm, 8), (mx, 3, 4), (lj, 7), (f, 6),
-            (quad_join, 1), (mx, 2, 4), (rm, 7), (lj, 6), (f, 5), (mx, 1, 4), (rm, 6), (lj, 5), (c, 4), (rm, 5), (f, 4), (c, 3), (f, 3), (c, 2), (f, 2),
+            (mx, 4, 1), (c, 9), (mx, 3, 1), (mx, 2, 0), (mx, 1, 0), (qj, 2), (mx, 4, 2), (m2, 4), (mx, 3, 2), (m2, 3), (mx, 4, 3), (m1, 4), (mx, 3, 3), (m1, 3), (f, 10),
+            (last_adds, 2), (mx, 2, 1), (lj, 10), (mx, 1, 1), (rm, 10), (mx, 2, 2), (m2, 2), (c, 8), (mx, 1, 2), (m2, 1), (f, 9), (mx, 2, 3), (m1, 2), (mx, 1, 3), (m1, 1),
+            (mx, 6, 4), (lj, 9), (mx, 5, 4), (rm, 9), (last_adds, 2), (c, 7), (mx, 4, 4), (c, 6), (f, 8), (mx, 3, 4), (lj, 8), (c, 5), (f, 7), (qj, 1), (rm, 8), (lj, 7), (mx, 2, 4), (f, 6), (rm, 7), (lj, 6), (mx, 1, 4), (f, 5),
+            (last_adds, 2), (rm, 6), (lj, 5), (last_adds, 2), (rm, 5), (c, 4), (f, 4), (c, 3), (f, 3), (c, 2), (f, 2),
             (lj, 4), (c, 1), (f, 1), (lj, 3), (rm, 4), (lj, 2), (rm, 3), (lj, 1), (rm, 2), (rm, 1),
         ):
-            fn((NBLK // 4 if fn is quad_join else z) - b, *d)
+            fn(b if fn is last_adds else (NBLK // 4 if fn is qj else z) - b, *d)
 
         for s0 in stores:
             store(s0, s0 + 2, nc.sync)

@@ -36,11 +36,11 @@ FAR = 1024.0
 WARM = (7, 2, 2, 3)
 HEAD_ORDER = (0, 2, 1, 3)
 HEAD_X = (2, 3, 3, 2, 2)
-HEAD_ENG = "pp"
+HEAD_ENG = "pppppppppsps"
 HEAD_R = (2, 3, 3, 2, 2)
 HEAD_Q = (0, 1, 1, 2, 2)
 R_LEAD = 6
-R_ENG = "vsvvsvsv"
+R_ENG = "spvpspvp"
 NEG_BIG = -3.0e38
 W_ENG = ("sv", "vv", "sv", "vv", "sv")
 
@@ -104,6 +104,9 @@ def tile_compositionalphoneticsmodel_t_kernel(tc, enc_output, feature2phone, map
         make_identity(nc, ident_f[:])
         ones = const.tile([P, BLOCK], BF16)
         nc.vector.memset(ones[:], 1.0)
+
+        first = const.tile([P, 1], F32)
+        nc.scalar.activation(out=first[:], in_=ones[:, 0:1], func=ACT.Exp)
 
         def warm(n):
             warm_p = ps_f.tile([P, BLOCK], F32, tag="pf")
@@ -489,7 +492,7 @@ def tile_compositionalphoneticsmodel_t_kernel(tc, enc_output, feature2phone, map
             if d + 2 < DEPTH:
                 sel_make(d + 2)
             for n in range(r_n, r_n + HEAD_R[d]):
-                reorder(n, HEAD_ENG[n % 2])
+                reorder(n, HEAD_ENG[n - 4 * STRIDED])
             r_n += HEAD_R[d]
             for n in range(x_n, x_n + HEAD_X[d]):
                 a_bank(n)
@@ -521,33 +524,29 @@ def tile_compositionalphoneticsmodel_t_kernel(tc, enc_output, feature2phone, map
 
         nh = 2 * NBLK
         npair = NBLK // 2
-        group = 0
         stores = []
         pending = []
 
         for j in range(npair - 2):
             b0 = 2 * j
+            banks = [(b0, 1), (b0 + 1, 1), (b0, 3), (b0, 2), (b0 + 1, 2), (b0 + 1, 3)]
+            banks += ([(b0 - 2, 4), (b0 - 1, 4)] if j >= 1 else []) + [(b0 + 2, 0), (b0 + 3, 0)]
+            passes = [(b, d, g) for b, d in banks for g in range(2)]
+            t_run = [(a_transpose, n, s) for n in range(x_n, min(2 * nh, x_n + 8)) for s in range(4)]
+            x_n += 8
             for ph in range(4):
                 due = len(loads)
-                m_run = (
-                    [(b0, 1), (b0 + 1, 1), (b0, 3)],
-                    [(b0, 2), (b0 + 1, 2)],
-                    [(b0 + 1, 3)] + ([(b0 - 2, 4), (b0 - 1, 4)] if j >= 1 else []),
-                    [(b0 + 2, 0), (b0 + 3, 0)],
-                )[ph]
                 tasks = []
-                if ph == 1 and j >= 3:
-                    tasks.append((combine, b0 - 5))
-                if ph == 3 and j >= 2:
-                    tasks.append((combine, b0 - 4))
-                joined = b0 - 8 + ph
-                if ph >= 2 and j >= 3:
+                joined = b0 - 6 + ph // 2
+                if ph % 2 == 0 and j >= 3:
                     tasks += [(lane_join, joined), (row_max, joined)]
-                if ph == 0 and j >= 2 and j % 2 == 0:
-                    tasks.append((quad_join, j // 2 - 1))
-                for b, d in m_run:
-                    mx(b, d)
-                    if tasks:
+                if ph % 2 == 1 and j >= 2:
+                    tasks.append((combine, b0 - 4 + ph // 2))
+                if ph == 3 and j % 2 == 1:
+                    tasks.append((quad_join, j // 2))
+                for b, d, g in passes[5 * ph : 5 * ph + 5] if len(passes) == 20 else [p for m in ((0, 1, 2), (3, 4), (5,), (6, 7))[ph] for p in passes[2 * m : 2 * m + 2]]:
+                    mx_pass(b, d, g)
+                    if g == 1 and tasks:
                         fn, arg = tasks.pop(0)
                         fn(arg)
                 for fn, arg in tasks:
@@ -558,25 +557,20 @@ def tile_compositionalphoneticsmodel_t_kernel(tc, enc_output, feature2phone, map
                     move_first(b0)
                 if ph == 2:
                     move_first(b0 + 1)
-                for n in range(x_n, x_n + 2):
-                    if n < 2 * nh:
-                        a_bank(n)
-                x_n += 2
-                if ph % 2 == 0 and j >= 3:
+                cuts = (0, 6 if j >= 3 else 8, 16, 22 if j >= 2 else 24, 32)
+                for fn, n, s in t_run[cuts[ph] : cuts[ph + 1]]:
+                    fn(n, s)
+                if ph == 0 and j >= 3 or ph == 2 and j >= 2:
                     for s in range(4):
-                        f_transpose(b0 - 6 + ph // 2, s)
+                        f_transpose(b0 - 5 + ph // 2, s)
                 for i in range(3 if j == npair - 3 and ph == 3 else 1):
                     quant(q_n)
                     q_n += 1
-                while r_n < min(2 * nh, x_n + R_LEAD):
+                while r_n < min(2 * nh, x_n - 8 + R_LEAD + 2 * (ph + 1)):
                     reorder(r_n, R_ENG[r_n % 8])
                     r_n += 1
-                if ph >= 2 and j >= 3:
+                if ph % 2 == 0 and j >= 3:
                     exps(joined)
-                    if group < len(GROUPS) - 1 and joined == GROUPS[group][1] - 1:
-                        group_ln(group, nc.gpsimd)
-                        pending.extend(range(GROUPS[group][0], GROUPS[group][1], 2))
-                        group += 1
                 loads_flush(due)
 
         z = NBLK
@@ -585,9 +579,9 @@ def tile_compositionalphoneticsmodel_t_kernel(tc, enc_output, feature2phone, map
             for s in range(4):
                 f_transpose(b, s, ps_t, "pt")
 
-        def last_max(b):
-            row_max(b)
-            exps(b)
+        def last_ln(n):
+            group_ln(n, nc.gpsimd)
+            pending.extend(range(GROUPS[n][0], GROUPS[n][1], 2))
 
         def last_adds(n):
             for i in range(n + 1):
@@ -599,15 +593,15 @@ def tile_compositionalphoneticsmodel_t_kernel(tc, enc_output, feature2phone, map
                         finish_scalar(s0, s0 + 2)
                     stores.append(s0)
 
-        m1, m2, c, f, lj, rm, qj = move_first, move_second, combine, last_f, lane_join, last_max, quad_join
+        m1, m2, c, f, lj, rm, ex, qj = move_first, move_second, combine, last_f, lane_join, row_max, exps, quad_join
         for fn, b, *d in (
-            (mx, 4, 1), (c, 9), (mx, 3, 1), (mx, 2, 0), (mx, 1, 0), (qj, 2), (mx, 4, 2), (m2, 4), (mx, 3, 2), (m2, 3), (mx, 4, 3), (m1, 4), (mx, 3, 3), (m1, 3), (f, 10),
-            (last_adds, 2), (mx, 2, 1), (lj, 10), (mx, 1, 1), (rm, 10), (mx, 2, 2), (m2, 2), (c, 8), (mx, 1, 2), (m2, 1), (f, 9), (mx, 2, 3), (m1, 2), (mx, 1, 3), (m1, 1),
-            (mx, 6, 4), (lj, 9), (mx, 5, 4), (rm, 9), (last_adds, 2), (c, 7), (mx, 4, 4), (c, 6), (f, 8), (mx, 3, 4), (lj, 8), (c, 5), (f, 7), (qj, 1), (rm, 8), (lj, 7), (mx, 2, 4), (f, 6), (rm, 7), (lj, 6), (mx, 1, 4), (f, 5),
-            (last_adds, 2), (rm, 6), (lj, 5), (last_adds, 2), (rm, 5), (c, 4), (f, 4), (c, 3), (f, 3), (c, 2), (f, 2),
-            (lj, 4), (c, 1), (f, 1), (lj, 3), (rm, 4), (lj, 2), (rm, 3), (lj, 1), (rm, 2), (rm, 1),
+            (last_ln, 0), (mx, 4, 1), (lj, 10), (mx, 3, 1), (mx, 2, 0), (mx, 1, 0), (rm, 10), (f, 9), (mx, 4, 2), (m2, 4), (c, 8), (mx, 3, 2), (m2, 3), (mx, 4, 3), (m1, 4), (mx, 3, 3), (m1, 3), (ex, 10),
+            (mx, 2, 1), (lj, 9), (mx, 1, 1), (rm, 9), (last_adds, 2), (f, 8), (mx, 2, 2), (m2, 2), (c, 7), (mx, 1, 2), (m2, 1), (mx, 2, 3), (m1, 2), (mx, 1, 3), (m1, 1), (ex, 9),
+            (mx, 6, 4), (lj, 8), (mx, 5, 4), (rm, 8), (ex, 8), (f, 7), (last_adds, 2), (c, 6), (mx, 4, 4), (lj, 7), (c, 5), (f, 6), (mx, 3, 4), (qj, 1), (rm, 7), (ex, 7), (lj, 6), (mx, 2, 4), (f, 5), (rm, 6), (ex, 6), (lj, 5), (mx, 1, 4),
+            (last_adds, 2), (rm, 5), (ex, 5), (last_adds, 2), (c, 4), (f, 4), (c, 3), (f, 3), (c, 2), (f, 2),
+            (lj, 4), (c, 1), (f, 1), (lj, 3), (rm, 4), (lj, 2), (rm, 3), (lj, 1), (ex, 4), (ex, 3), (rm, 2), (ex, 2), (rm, 1), (ex, 1),
         ):
-            fn(b if fn is last_adds else (NBLK // 4 if fn is qj else z) - b, *d)
+            fn(b if fn in (last_adds, last_ln) else (NBLK // 4 if fn is qj else z) - b, *d)
 
         for s0 in stores:
             store(s0, s0 + 2, nc.sync)

from contextlib import ExitStack

import concourse.mybir as mybir
from concourse.masks import make_identity

F32 = mybir.dt.float32
BF16 = mybir.dt.bfloat16
I32 = mybir.dt.int32
U32 = mybir.dt.uint32
U8 = mybir.dt.uint8
FP8X4 = mybir.dt.float8_e4m3fn_x4
ALU = mybir.AluOpType
ACT = mybir.ActivationFunctionType
AX = mybir.AxisListType

TOKENS = 16 * 1024
H = 1024
PHONES = 256
PHONEMES = 64
FLOPS = 2 * TOKENS * H * PHONES

P = 128
BLOCK = 512
NBLK = TOKENS // BLOCK
DEPTH = 5
FIRST = 3
PARTNERS = 16
SECOND = 3
MOVED = 4
HELP = 96
HELPERS = SECOND + PARTNERS
STRIDED = 1
GROUPS = ((0, 22), (22, 32))
XBUFS = 5
FAR = 1024.0
WARM = (7, 2, 2, 3)
HEAD_ORDER = (0, 2, 1, 3)
HEAD_X = (2, 3, 3, 2, 2)
HEAD_ENG = "pppppppppsps"
HEAD_R = (2, 3, 3, 2, 2)
HEAD_Q = (0, 1, 1, 2, 2)
R_LEAD = 6
R_ENG = "spvpspvp"
NEG_BIG = -3.0e38
W_ENG = ("sv", "vv", "sv", "vv", "sv")

def tile_compositionalphoneticsmodel_t_kernel(tc, enc_output, feature2phone, mapping, out):
    nc = tc.nc
    enc_v = enc_output.rearrange("b t k -> (b t) k").rearrange("(n p s) k -> n p (s k)", p=P, s=4)
    out_v = out.rearrange("b t m -> (b t) m").rearrange("(n p s) m -> p n (s m)", p=P, s=4)
    w_v = feature2phone.rearrange("(g q t) p -> q g (t p)", g=2, q=P, t=4)

    with ExitStack() as ctx:
        const = ctx.enter_context(tc.tile_pool(name="const", bufs=1))
        xpool = ctx.enter_context(tc.tile_pool(name="xpool", bufs=XBUFS))
        rpool = ctx.enter_context(tc.tile_pool(name="rpool", bufs=10))
        gpool = ctx.enter_context(tc.tile_pool(name="gpool", bufs=5))
        cpool = ctx.enter_context(tc.tile_pool(name="cpool", bufs=8))
        apool = ctx.enter_context(tc.tile_pool(name="apool", bufs=10))
        bpool = ctx.enter_context(tc.tile_pool(name="bpool", bufs=8))
        spool = ctx.enter_context(tc.tile_pool(name="spool", bufs=4))
        qpool = ctx.enter_context(tc.tile_pool(name="qpool", bufs=2))
        ps_t = ctx.enter_context(tc.psum_pool(name="ps_t", bufs=4))
        ps_m = ctx.enter_context(tc.psum_pool(name="ps_m", bufs=3))
        ps_f = ctx.enter_context(tc.psum_pool(name="ps_f", bufs=1))
        ctx.enter_context(tc.manual_schedule())

        xs = {}
        xrs = {}
        pts = {}
        pms = {}
        a1s = {}
        grs = {}
        cds = {}
        accs = {}
        tops = {}
        quads = {}
        pfs = {}

        map2 = const.tile([P, 2, PHONES], BF16)
        nc.sync.dma_start(out=map2[0:64, 1, :], in_=mapping)
        nc.sync.dma_start(out=map2[64:128, 1, :], in_=mapping)
        wl = const.tile([P, 4, 2, PHONES], BF16)

        def load(b, parts=1):
            x = xpool.tile([P, 4 * H], BF16)
            n = 4 * H // parts
            for i in range(parts):
                nc.sync.dma_start(out=x[:, i * n : (i + 1) * n], in_=enc_v[b][:, i * n : (i + 1) * n])
            xs[b] = x

        nc.sync.dma_start(out=wl[:].rearrange("q (g u) e p -> q g (u e p)", g=2), in_=w_v)
        load(0, 2)
        for b in range(1, XBUFS):
            load(b)

        part_i = const.tile([P, 1], I32)
        nc.gpsimd.iota(part_i[:], pattern=[[0, 1]], base=0, channel_multiplier=1)
        iota_i = const.tile([P, P], I32)
        nc.gpsimd.iota(iota_i[:], pattern=[[1, P]], base=0, channel_multiplier=0)
        ident_b = const.tile([P, P], BF16)
        make_identity(nc, ident_b[:])
        ident_f = const.tile([P, P], F32)
        make_identity(nc, ident_f[:])
        ones = const.tile([P, BLOCK], BF16)
        nc.vector.memset(ones[:], 1.0)

        first = const.tile([P, 1], F32)
        nc.scalar.activation(out=first[:], in_=ones[:, 0:1], func=ACT.Exp)

        def warm(n):
            warm_p = ps_f.tile([P, BLOCK], F32, tag="pf")
            for i in range(n):
                nc.tensor.matmul(out=warm_p[:], lhsT=ones[:, 0:P], rhs=ones[:], start=True, stop=True)

        warm(WARM[0])
        part_f = const.tile([P, 1], F32)
        nc.vector.tensor_copy(out=part_f[:], in_=part_i[:])
        iota_f = const.tile([P, P], F32)
        nc.vector.tensor_copy(out=iota_f[:], in_=iota_i[:])
        upper = const.tile([P, 1], F32)
        nc.vector.tensor_single_scalar(out=upper[:], in_=part_f[:], scalar=64.0, op=ALU.is_ge)
        lims = const.tile([P, 6], F32)
        for i, (lo, hi) in enumerate(((10, 12), (17, 14), (-1, 7), (FAR, 5), (FAR, 10), (FAR, 17))):
            nc.vector.tensor_scalar(out=lims[:, i : i + 1], in0=upper[:], scalar1=float(hi - lo), scalar2=float(lo), op0=ALU.mult, op1=ALU.add)
        tri = const.tile([P, P], BF16)
        nc.vector.tensor_scalar(out=tri[:], in0=iota_f[:], scalar1=part_f[:, 0:1], scalar2=None, op0=ALU.is_gt)
        rank_n = const.tile([P, P], F32)
        nc.vector.tensor_single_scalar(out=rank_n[:, 0:HELP], in_=iota_f[:, 0:HELP], scalar=-1.0, op=ALU.mult)
        nc.vector.tensor_scalar(
            out=rank_n[:, HELP + HELPERS : P], in0=iota_f[:, HELP + HELPERS : P], scalar1=-1.0, scalar2=float(HELPERS), op0=ALU.mult, op1=ALU.add
        )

        strides = const.tile([P, 3], F32)
        for i, w in enumerate((5.0, 2.0, 3.0)):
            nc.vector.memset(strides[:, i : i + 1], w)
        own = const.tile([P, 1], F32)
        nc.vector.tensor_scalar(out=own[:], in0=part_f[:], scalar1=float(PARTNERS), scalar2=-1.0, op0=ALU.is_lt, op1=ALU.mult)
        ge_h = const.tile([P, 1], F32)
        nc.vector.tensor_scalar(out=ge_h[:], in0=part_f[:], scalar1=float(HELP), scalar2=None, op0=ALU.is_ge)
        ge_e = const.tile([P, 1], F32)
        nc.vector.tensor_scalar(out=ge_e[:], in0=part_f[:], scalar1=float(HELP + HELPERS), scalar2=None, op0=ALU.is_ge)
        ge_f = const.tile([P, 1], F32)
        nc.vector.tensor_scalar(out=ge_f[:], in0=part_f[:], scalar1=float(HELP + SECOND), scalar2=-3.0, op0=ALU.is_ge, op1=ALU.mult)
        helper = const.tile([P, 1], F32)
        nc.vector.tensor_tensor(out=helper[:], in0=ge_h[:], in1=ge_e[:], op=ALU.subtract)
        aid = const.tile([P, 1], F32)
        nc.vector.scalar_tensor_tensor(out=aid[:], in0=ge_e[:], scalar=-4.0, in1=ge_f[:], op0=ALU.mult, op1=ALU.add)
        less = const.tile([P, 1], F32)
        nc.vector.scalar_tensor_tensor(out=less[:], in0=helper[:], scalar=-3.0, in1=own[:], op0=ALU.mult, op1=ALU.add)
        nc.vector.scalar_tensor_tensor(out=aid[:], in0=ge_h[:], scalar=7.0, in1=aid[:], op0=ALU.mult, op1=ALU.add)
        step = const.tile([P, DEPTH], F32)
        nc.vector.tensor_scalar(out=step[:, FIRST:DEPTH], in0=iota_f[:, FIRST:DEPTH], scalar1=less[:, 0:1], scalar2=1.0, op0=ALU.add, op1=ALU.add)
        nc.vector.tensor_scalar(out=step[:, 0:FIRST], in0=iota_f[:, 0:FIRST], scalar1=aid[:, 0:1], scalar2=1.0, op0=ALU.add, op1=ALU.add)

        mask = const.tile([P, PHONES], F32)
        nc.vector.tensor_single_scalar(out=mask[:], in_=map2[:, 1, :], scalar=0.0, op=ALU.is_gt)
        incl = const.tile([P, PHONES], F32)
        nc.vector.tensor_tensor_scan(out=incl[:], data0=mask[:], data1=mask[:], initial=0.0, op0=ALU.add, op1=ALU.max)
        count = incl[:, PHONES - 1 : PHONES]
        over = const.tile([P, 6], BF16)
        nc.vector.tensor_tensor(out=over[:], in0=count.to_broadcast([P, 6]), in1=lims[:], op=ALU.is_gt)
        nc.vector.tensor_tensor(out=map2[:, 0, :], in0=incl[:], in1=mask[:], op=ALU.mult)

        wt = []

        def wt_make(c):
            wt_p = ps_t.tile([P, 8 * P], BF16, tag="pt")
            for a in range(4):
                for e in range(2):
                    nc.tensor.transpose(wt_p[:, (a * 2 + e) * P : (a * 2 + e + 1) * P], wl[:, a, e, c * P : (c + 1) * P], ident_b[:])
            wt_c = const.tile([P, 8 * P], BF16, name="wt%d" % c)
            nc.scalar.copy(out=wt_c[:], in_=wt_p[:])
            wt.append(wt_c)

        sel = const.tile([P, DEPTH, 2, P], BF16)

        def sel_make(d):
            sel_p = ps_f.tile([P, 2, P], BF16, tag="pf")
            for c in range(2):
                nc.tensor.transpose(sel_p[:, c, :], takes[:, d, c * P : (c + 1) * P], ident_b[:])
            nc.scalar.activation(out=sel[:, d, :, :], in_=sel_p[:], func=ACT.Sign)

        wgs = {}
        w_codes = const.tile([P, 2, DEPTH, P], U32, align_bytes=64)
        w_scales = const.tile([P, 2, DEPTH, P], U8, align_bytes=64)

        def wslot_make(d, engines):
            wg = apool.tile([P, 2, P * 4], BF16, tag="acc", align_bytes=64)
            wgs[d] = wg
            for g in range(2):
                wp = ps_m.tile([P, 4 * P], F32, tag="pm")
                for ue in range(4):
                    for c in range(2):
                        nc.tensor.matmul(
                            out=wp[:, ue * P : (ue + 1) * P],
                            lhsT=wt[c][:, (g * 4 + ue) * P : (g * 4 + ue + 1) * P],
                            rhs=sel[:, d, c, :],
                            start=(c == 0),
                            stop=(c == 1),
                        )
                dst = wg[:, g, :].rearrange("q (l t) -> q l t", t=4)
                src = wp[:].rearrange("q (t l) -> q l t", t=4)
                if engines[g] == "v":
                    nc.vector.tensor_copy(out=dst, in_=src)
                else:
                    nc.scalar.copy(out=dst, in_=src)

        def wslot_quant(d):
            for g in range(2):
                nc.vector.quantize_mx(out=w_codes[:, g, d, :].bitcast(FP8X4), scales=w_scales[:, g, d, :], in_=wgs[d][:, g, :])

        gain = const.tile([P, DEPTH], F32)
        perm = const.tile([P, P], F32)
        bias_h = const.tile([P, 1], F32)

        bias_q = const.tile([P, 1], F32)

        def bias_make():
            rest_i = const.tile([P, 1], I32)
            nc.vector.tensor_single_scalar(out=rest_i[:], in_=part_i[:], scalar=31, op=ALU.bitwise_and)
            nc.vector.tensor_scalar(out=bias_q[:], in0=rest_i[:], scalar1=float(SECOND), scalar2=NEG_BIG, op0=ALU.is_equal, op1=ALU.mult)

        def gain_make():
            nc.vector.tensor_single_scalar(out=gain[:], in_=gain_l[:], scalar=1.0 / 32.0, op=ALU.mult)

        def perm_make():
            perm_p = ps_f.tile([P, P], BF16, tag="pf")
            nc.tensor.transpose(perm_p[:], place[:, 1, :], ident_b[:])
            nc.scalar.copy(out=perm[:], in_=perm_p[:])
            nc.vector.tensor_single_scalar(out=bias_h[:], in_=helper[:], scalar=NEG_BIG, op=ALU.mult)

        v_all = const.tile([P, NBLK * 256], F32)
        neg_max = const.tile([P, NBLK * 4], F32)
        sums = const.tile([P, NBLK * 4], F32)
        logs = const.tile([P, NBLK * 4], F32)
        neg_l = const.tile([P, NBLK * 4], F32)

        loads = []

        def loads_flush(n):
            for i in range(n):
                load(loads.pop(0))

        def reorder(n, eng="s"):
            b, k = n // 4, n % 4
            g, sp = k // 2, k % 2
            xr = rpool.tile([P, 2, 2, P], F32)
            xrs[n] = xr
            src = xs[b][:].bitcast(F32).rearrange("p (s c) -> p s c", s=4)[:, 2 * sp : 2 * sp + 2, g * 256 : (g + 1) * 256].rearrange("p s (w u) -> p s u w", u=2)
            if eng == "v":
                nc.vector.tensor_copy(out=xrs[n][:], in_=src)
            elif eng == "p":
                nc.gpsimd.tensor_copy(out=xrs[n][:].bitcast(I32), in_=src.bitcast(I32))
            else:
                nc.scalar.copy(out=xrs[n][:], in_=src)
            if k == 3 and b + XBUFS < NBLK:
                loads.append(b + XBUFS)

        def a_transpose(n, i):
            b, k = n // 4, n % 4
            g, sp = k // 2, k % 2
            if (b, g) not in grs:
                gr = gpool.tile([P, BLOCK * 4], BF16, align_bytes=64)
                grs[(b, g)] = gr
            if i == 0:
                pt = ps_t.tile([P, 4 * P], F32, tag="pt")
                pts[n] = pt
            u, s2 = i // 2, i % 2
            if b < STRIDED:
                lo = (2 * sp + s2) * 512 + 256 * g
                words = xs[b][:].bitcast(F32)[:, lo + u : lo + 256 : 2]
            else:
                words = xrs[n][:, s2, u, :]
            nc.tensor.transpose(pts[n][:, i * P : (i + 1) * P], words, ident_f[:])
            if i == 3:
                grw = grs[(b, g)][:].bitcast(F32)
                nc.scalar.copy(out=grw[:, sp * 512 : (sp + 1) * 512].rearrange("q (t u) -> q t u", u=2), in_=pts[n][:].rearrange("q (u t) -> q t u", u=2))
                if b < STRIDED and k == 3 and b + XBUFS < NBLK:
                    loads.append(b + XBUFS)

        def a_bank(n):
            for i in range(4):
                a_transpose(n, i)

        def quant(n):
            b, g = n // 2, n % 2
            if g == 0:
                codes = cpool.tile([P, 2 * BLOCK], U32, align_bytes=64)
                scales = cpool.tile([P, 2 * BLOCK], U8, align_bytes=64)
                cds[b] = (codes, scales)
            codes, scales = cds[b]
            nc.vector.quantize_mx(
                out=codes[:, g * BLOCK : (g + 1) * BLOCK].bitcast(FP8X4),
                scales=scales[:, g * BLOCK : (g + 1) * BLOCK],
                in_=grs[(b, g)][:],
            )

        def mx_pass(b, d, g):
            if g == 0:
                if d == 0:
                    acc = apool.tile([P, BLOCK], F32, tag="acc", align_bytes=64)
                    accs[b] = acc
                if d == FIRST:
                    top = bpool.tile([P, BLOCK], F32)
                    tops[b] = top
                pm = ps_m.tile([P, BLOCK], F32, tag="pm")
                pms[(b, d)] = pm
            pm = pms[(b, d)]
            codes, scales = cds[b]
            nc.tensor.matmul_mx(
                out=pm[:],
                lhsT=w_codes[:, g, d, :].bitcast(FP8X4),
                lhsT_scale=w_scales[:, g, d, :],
                rhs=codes[:, g * BLOCK : (g + 1) * BLOCK].bitcast(FP8X4),
                rhs_scale=scales[:, g * BLOCK : (g + 1) * BLOCK],
                start=(g == 0),
                stop=(g == 1),
            )
            if g == 1:
                dst = accs[b] if d < FIRST else tops[b]
                if d in (0, FIRST):
                    nc.scalar.activation(out=dst[:], in_=pm[:], func=ACT.Copy, scale=gain[:, d : d + 1])
                else:
                    nc.vector.scalar_tensor_tensor(out=dst[:], in0=pm[:], scalar=gain[:, d : d + 1], in1=dst[:], op0=ALU.mult, op1=ALU.max)

        def mx(b, d):
            mx_pass(b, d, 0)
            mx_pass(b, d, 1)

        def move_second(b):
            q, r = b // 4, 32 * (b % 4)
            nc.sync.dma_start(out=e2s[q % 2][r : r + MOVED, :], in_=accs[b][HELP : HELP + MOVED, :])
            nc.sync.dma_start(out=p2s[q % 2][r : r + MOVED, :], in_=accs[b][0:MOVED, :])

        def move_first(b):
            nc.sync.dma_start(out=tops[b][0:PARTNERS, :], in_=accs[b][HELP + SECOND : HELP + HELPERS, :])

        def quad_join(q):
            nc.vector.scalar_tensor_tensor(
                out=p2s[q % 2][:], in0=e2s[q % 2][:], scalar=bias_q[:, 0:1], in1=p2s[q % 2][:], op0=ALU.add, op1=ALU.max
            )
            for i in range(4):
                nc.sync.dma_start(out=accs[4 * q + i][0:MOVED, :], in_=p2s[q % 2][32 * i : 32 * i + MOVED, :])

        def combine(b):
            nc.vector.scalar_tensor_tensor(out=tops[b][:], in0=accs[b][:], scalar=bias_h[:, 0:1], in1=tops[b][:], op0=ALU.add, op1=ALU.max)

        def f_transpose(b, s, pool=ps_f, tag="pf"):
            if s == 0:
                pf = pool.tile([P, 4, P], F32, tag=tag)
                pfs[b] = pf
            nc.tensor.transpose(pfs[b][:, s, :], tops[b][:, s * P : (s + 1) * P], perm[:])
            if s == 3:
                a1 = spool.tile([P, 4, PHONEMES], F32)
                a1s[b] = a1
                nc.scalar.copy(out=a1[:], in_=pfs[b][:, :, 64:128])

        def lane_join(b):
            vv = v_all[:, b * 256 : (b + 1) * 256].rearrange("p (s m) -> p s m", m=PHONEMES)
            nc.vector.tensor_tensor(out=vv, in0=pfs[b][:, :, 0:64], in1=a1s[b][:], op=ALU.max)

        def row_max(b):
            vv = v_all[:, b * 256 : (b + 1) * 256].rearrange("p (s m) -> p s m", m=PHONEMES)
            nc.vector.tensor_reduce(out=neg_max[:, b * 4 : (b + 1) * 4], in_=vv, axis=AX.X, op=ALU.max, negate=True)

        def exps(b):
            for i in range(b * 4, b * 4 + 4):
                ex = spool.tile([P, PHONEMES], F32)
                nc.scalar.activation(
                    out=ex[:], in_=v_all[:, i * 64 : (i + 1) * 64], func=ACT.Exp,
                    bias=neg_max[:, i : i + 1], scale=1.0, accum_out=sums[:, i : i + 1],
                )

        def group_ln(gi, eng):
            g0, g1 = GROUPS[gi]
            cols = slice(g0 * 4, g1 * 4)
            nc.scalar.activation(out=logs[:, cols], in_=sums[:, cols], func=ACT.Ln)
            eng.tensor_tensor(out=neg_l[:, cols], in0=neg_max[:, cols], in1=logs[:, cols], op=ALU.subtract)

        def finish(b0, b1, eng):
            n = (b1 - b0) * 4
            vg3 = v_all[:, b0 * 256 : b1 * 256].rearrange("p (i m) -> p i m", m=PHONEMES)
            eng.tensor_tensor(out=vg3, in0=vg3, in1=neg_l[:, b0 * 4 : b1 * 4].unsqueeze(2).to_broadcast([P, n, PHONEMES]), op=ALU.add)

        def finish_scalar(b0, b1):
            for i in range(b0 * 4, b1 * 4):
                nc.scalar.activation(out=v_all[:, i * 64 : (i + 1) * 64], in_=v_all[:, i * 64 : (i + 1) * 64], func=ACT.Identity, bias=neg_l[:, i : i + 1], scale=1.0)

        def store(b0, b1, queue):
            queue.dma_start(out=out_v[:, b0:b1, :], in_=v_all[:, b0 * 256 : b1 * 256].rearrange("p (n f) -> p n f", f=256))

        wt_make(0)
        warm(WARM[1])
        lid_p = ps_m.tile([P, 2, 6], F32, tag="pm")
        nc.tensor.matmul(out=lid_p[:, 0, :], lhsT=tri[:], rhs=over[:], start=True, stop=True)
        nc.tensor.matmul(out=lid_p[:, 1, :], lhsT=ones[:, 0:P], rhs=over[:], start=True, stop=True)
        light = const.tile([P, 1], F32)
        nc.vector.tensor_scalar(out=light[:], in0=over[:, 2:3], scalar1=-1.0, scalar2=1.0, op0=ALU.mult, op1=ALU.add)
        aided = const.tile([P, 1], F32)
        nc.vector.tensor_copy(out=aided[:], in_=over[:, 0:1])
        only = const.tile([P, 1], F32)
        nc.vector.tensor_tensor(out=only[:], in0=over[:, 0:1], in1=over[:, 1:2], op=ALU.subtract)
        part_x = const.tile([P, 1], F32)
        nc.vector.scalar_tensor_tensor(out=part_x[:], in0=over[:, 0:1], scalar=-FAR, in1=part_f[:], op0=ALU.mult, op1=ALU.add)
        lid = const.tile([P, 2, 6], F32)
        nc.vector.tensor_copy(out=lid[:], in_=lid_p[:])
        steps = const.tile([P, 3], F32)
        nc.vector.tensor_tensor(out=steps[:], in0=over[:, 3:6], in1=strides[:], op=ALU.mult)
        lane_c = const.tile([P, 2], BF16)
        nc.vector.tensor_copy(out=lane_c[:, 1:2], in_=count)
        rank_l = const.tile([P, 1], F32)
        nc.vector.tensor_scalar(out=rank_l[:], in0=lid[:, 0, 2:3], scalar1=-1.0, scalar2=part_f[:, 0:1], op0=ALU.mult, op1=ALU.add)
        two = const.tile([P, 1], F32)
        nc.vector.scalar_tensor_tensor(out=two[:], in0=lid[:, 0, 1:2], scalar=-2.0, in1=lid[:, 0, 0:1], op0=ALU.mult, op1=ALU.add)
        rest = const.tile([P, 1], F32)
        nc.vector.scalar_tensor_tensor(
            out=rest[:], in0=lid[:, 0, 0:1], scalar=lid[:, 1, 0:1], in1=part_x[:], op0=ALU.subtract, op1=ALU.subtract
        )
        nc.vector.scalar_tensor_tensor(out=lane_c[:, 0:1], in0=steps[:, 0:1], scalar=steps[:, 1:2], in1=steps[:, 2:3], op0=ALU.add, op1=ALU.add)
        helps = const.tile([P, 1], F32)
        nc.vector.tensor_scalar(out=helps[:], in0=rank_l[:], scalar1=float(HELPERS), scalar2=light[:, 0:1], op0=ALU.is_lt, op1=ALU.mult)
        shift = const.tile([P, 1], F32)
        nc.vector.tensor_scalar(out=shift[:], in0=two[:], scalar1=lid[:, 1, 1:2], scalar2=only[:, 0:1], op0=ALU.add, op1=ALU.mult)
        rank_o = const.tile([P, 1], F32)
        nc.vector.tensor_scalar(out=rank_o[:], in0=rank_l[:], scalar1=float(HELPERS), scalar2=rest[:, 0:1], op0=ALU.min, op1=ALU.add)
        place = const.tile([P, 2, P], BF16)
        nc.vector.tensor_scalar(
            out=place[:, 1, HELP : HELP + HELPERS], in0=iota_f[:, 0:HELPERS], scalar1=rank_l[:, 0:1], scalar2=light[:, 0:1], op0=ALU.is_equal, op1=ALU.mult
        )
        rank_p = const.tile([P, 1], F32)
        nc.vector.tensor_tensor(out=rank_p[:], in0=shift[:], in1=lid[:, 0, 1:2], op=ALU.add)
        rank_r = const.tile([P, 1], F32)
        nc.vector.scalar_tensor_tensor(out=rank_r[:], in0=helps[:], scalar=FAR, in1=rank_o[:], op0=ALU.mult, op1=ALU.add)
        front = const.tile([P, HELP], BF16)
        nc.vector.tensor_scalar(out=front[:], in0=iota_f[:, 0:HELP], scalar1=rank_p[:, 0:1], scalar2=aided[:, 0:1], op0=ALU.is_equal, op1=ALU.mult)
        nc.vector.tensor_scalar(
            out=place[:, 0, HELP + HELPERS : P], in0=rank_n[:, HELP + HELPERS : P], scalar1=rank_r[:, 0:1], scalar2=None, op0=ALU.is_equal
        )
        nc.vector.scalar_tensor_tensor(
            out=place[:, 0, 0:HELP], in0=rank_n[:, 0:HELP], scalar=rank_r[:, 0:1], in1=front[:], op0=ALU.is_equal, op1=ALU.add
        )
        nc.vector.tensor_copy(out=place[:, 1, HELP + HELPERS : P], in_=place[:, 0, HELP + HELPERS : P])
        nc.vector.tensor_copy(out=place[:, 0, HELP : HELP + SECOND], in_=place[:, 0, 0:SECOND])
        nc.vector.tensor_copy(out=place[:, 0, HELP + SECOND : HELP + HELPERS], in_=place[:, 0, 0:PARTNERS])
        nc.vector.tensor_copy(out=place[:, 1, 0:HELP], in_=place[:, 0, 0:HELP])

        wt_make(1)
        warm(WARM[2])
        for n in HEAD_ORDER[:3]:
            a_bank(n)
        warm(WARM[3])

        lane_p = []
        rk_p = []
        for h in range(2):
            lane = ps_t.tile([P, 2], F32, tag="pt", name="lane%d" % h)
            nc.tensor.matmul(out=lane[:], lhsT=place[:, h, :], rhs=lane_c[:], start=True, stop=True)
            lane_p.append(lane)
            rk = ps_m.tile([P, 2, PHONES], F32, tag="pm", name="rk%d" % h)
            nc.tensor.matmul(out=rk[:].rearrange("p a b -> p (a b)"), lhsT=place[:, h, :], rhs=map2[:].rearrange("p a b -> p (a b)"), start=True, stop=True)
            rk_p.append(rk)
        gains = const.tile([P, 2, PHONES], BF16)
        for h in range(2):
            nc.scalar.copy(out=gains[:, h, :], in_=rk_p[h][:, 1, :])
        want = const.tile([P, DEPTH], F32)
        for h, cols in ((0, slice(0, FIRST)), (1, slice(FIRST, DEPTH))):
            nc.vector.tensor_scalar(
                out=want[:, cols], in0=step[:, cols], scalar1=lane_p[h][:, 0:1], scalar2=lane_p[h][:, 1:2], op0=ALU.add, op1=ALU.min
            )

        takes = const.tile([P, DEPTH, PHONES], BF16)
        gain_l = const.tile([P, DEPTH], F32)

        def takes_make(d):
            h = 0 if d < FIRST else 1
            nc.vector.scalar_tensor_tensor(
                out=takes[:, d, :], in0=rk_p[h][:, 0, :], scalar=want[:, d : d + 1], in1=gains[:, h, :], op0=ALU.is_equal, op1=ALU.mult,
                accum_out=gain_l[:, d : d + 1],
            )

        for d in range(DEPTH):
            takes_make(d)
        sel_make(0)
        a_bank(HEAD_ORDER[3])
        sel_make(1)
        x_n = 4
        r_n = 4 * STRIDED
        q_n = 0
        for d in range(DEPTH):
            wslot_make(d, W_ENG[d])
            if d + 2 < DEPTH:
                sel_make(d + 2)
            for n in range(r_n, r_n + HEAD_R[d]):
                reorder(n, HEAD_ENG[n - 4 * STRIDED])
            r_n += HEAD_R[d]
            for n in range(x_n, x_n + HEAD_X[d]):
                a_bank(n)
            x_n += HEAD_X[d]
            wslot_quant(d)
            loads_flush(len(loads))
            for n in range(q_n, q_n + HEAD_Q[d]):
                quant(n)
            q_n += HEAD_Q[d]
            if d == 3:
                gain_make()
        mx(0, 0)
        mx(1, 0)
        perm_make()
        bias_make()
        e2s = []
        p2s = []
        for i in range(2):
            e2 = const.tile([P, BLOCK], F32, name="e2%d" % i)
            nc.gpsimd.memset(e2[:], 0.0)
            e2s.append(e2)
            p2 = const.tile([P, BLOCK], F32, name="p2%d" % i)
            nc.gpsimd.memset(p2[:], 0.0)
            p2s.append(p2)

        for n in range(r_n, x_n + R_LEAD):
            reorder(n, R_ENG[n % 8])
        r_n = x_n + R_LEAD

        nh = 2 * NBLK
        npair = NBLK // 2
        stores = []
        pending = []

        for j in range(npair - 2):
            b0 = 2 * j
            banks = [(b0, 1), (b0 + 1, 1), (b0, 3), (b0, 2), (b0 + 1, 2), (b0 + 1, 3)]
            banks += ([(b0 - 2, 4), (b0 - 1, 4)] if j >= 1 else []) + [(b0 + 2, 0), (b0 + 3, 0)]
            passes = [(b, d, g) for b, d in banks for g in range(2)]
            t_run = [(a_transpose, n, s) for n in range(x_n, min(2 * nh, x_n + 8)) for s in range(4)]
            x_n += 8
            for ph in range(4):
                due = len(loads)
                tasks = []
                joined = b0 - 6 + ph // 2
                if ph % 2 == 0 and j >= 3:
                    tasks += [(lane_join, joined), (row_max, joined)]
                if ph % 2 == 1 and j >= 2:
                    tasks.append((combine, b0 - 4 + ph // 2))
                if ph == 3 and j % 2 == 1:
                    tasks.append((quad_join, j // 2))
                for b, d, g in passes[5 * ph : 5 * ph + 5] if len(passes) == 20 else [p for m in ((0, 1, 2), (3, 4), (5,), (6, 7))[ph] for p in passes[2 * m : 2 * m + 2]]:
                    mx_pass(b, d, g)
                    if g == 1 and tasks:
                        fn, arg = tasks.pop(0)
                        fn(arg)
                for fn, arg in tasks:
                    fn(arg)
                if ph == 1:
                    move_second(b0)
                    move_second(b0 + 1)
                    move_first(b0)
                if ph == 2:
                    move_first(b0 + 1)
                cuts = (0, 6 if j >= 3 else 8, 16, 22 if j >= 2 else 24, 32)
                for fn, n, s in t_run[cuts[ph] : cuts[ph + 1]]:
                    fn(n, s)
                if ph == 0 and j >= 3 or ph == 2 and j >= 2:
                    for s in range(4):
                        f_transpose(b0 - 5 + ph // 2, s)
                for i in range(3 if j == npair - 3 and ph == 3 else 1):
                    quant(q_n)
                    q_n += 1
                while r_n < min(2 * nh, x_n - 8 + R_LEAD + 2 * (ph + 1)):
                    reorder(r_n, R_ENG[r_n % 8])
                    r_n += 1
                if ph % 2 == 0 and j >= 3:
                    exps(joined)
                loads_flush(due)

        z = NBLK

        def last_f(b):
            for s in range(4):
                f_transpose(b, s, ps_t, "pt")

        def last_ln(n):
            group_ln(n, nc.gpsimd)
            pending.extend(range(GROUPS[n][0], GROUPS[n][1], 2))

        def last_adds(n):
            for i in range(n + 1):
                if pending:
                    s0 = pending.pop(0)
                    if i == 0:
                        finish(s0, s0 + 2, nc.gpsimd)
                    else:
                        finish_scalar(s0, s0 + 2)
                    stores.append(s0)

        m1, m2, c, f, lj, rm, ex, qj = move_first, move_second, combine, last_f, lane_join, row_max, exps, quad_join
        for fn, b, *d in (
            (last_ln, 0), (mx, 4, 1), (lj, 10), (mx, 3, 1), (mx, 2, 0), (mx, 1, 0), (rm, 10), (f, 9), (mx, 4, 2), (m2, 4), (c, 8), (mx, 3, 2), (m2, 3), (mx, 4, 3), (m1, 4), (mx, 3, 3), (m1, 3), (ex, 10),
            (mx, 2, 1), (lj, 9), (mx, 1, 1), (rm, 9), (last_adds, 2), (f, 8), (mx, 2, 2), (m2, 2), (c, 7), (mx, 1, 2), (m2, 1), (mx, 2, 3), (m1, 2), (mx, 1, 3), (m1, 1), (ex, 9),
            (mx, 6, 4), (lj, 8), (mx, 5, 4), (rm, 8), (ex, 8), (f, 7), (last_adds, 2), (c, 6), (mx, 4, 4), (lj, 7), (c, 5), (f, 6), (mx, 3, 4), (qj, 1), (rm, 7), (ex, 7), (lj, 6), (mx, 2, 4), (f, 5), (rm, 6), (ex, 6), (lj, 5), (mx, 1, 4),
            (last_adds, 2), (rm, 5), (ex, 5), (last_adds, 2), (c, 4), (f, 4), (c, 3), (f, 3), (c, 2), (f, 2),
            (lj, 4), (c, 1), (f, 1), (lj, 3), (rm, 4), (lj, 2), (rm, 3), (lj, 1), (ex, 4), (ex, 3), (rm, 2), (ex, 2), (rm, 1), (ex, 1),
        ):
            fn(b if fn in (last_adds, last_ln) else (NBLK // 4 if fn is qj else z) - b, *d)

        for s0 in stores:
            store(s0, s0 + 2, nc.sync)
        g0 = GROUPS[-1][0]
        group_ln(len(GROUPS) - 1, nc.vector)
        for i in range(3):
            if i < 2:
                finish_scalar(g0 + 2 * i, g0 + 2 * i + 2)
                store(g0 + 2 * i, g0 + 2 * i + 2, nc.sync)
            finish(g0 + 4 + 2 * i, g0 + 6 + 2 * i, nc.vector)
            store(g0 + 4 + 2 * i, g0 + 6 + 2 * i, nc.sync)
